import numpy as np
import ml_dtypes


def mxq(x, axis, fmt="e4m3"):
    dtype, down = {"e4m3": (ml_dtypes.float8_e4m3fn, 7), "e5m2": (ml_dtypes.float8_e5m2, 14)}[fmt]
    v = np.moveaxis(np.asarray(x, np.float32).astype(ml_dtypes.bfloat16).astype(np.float64), axis, -1)
    blocks = v.reshape(v.shape[:-1] + (-1, 32))
    amax = np.abs(blocks).max(-1, keepdims=True)
    byte = np.maximum(np.where(amax > 0, np.frexp(amax)[1] - 1 + 127, 0) - down, 1)
    scale = np.exp2(byte - 127.0)
    codes = (blocks / scale).astype(np.float32).astype(dtype).astype(np.float64)
    return np.moveaxis((codes * scale).reshape(v.shape), -1, axis)


WIDE = False


def mx_kscale(k):
    if not WIDE:
        return np.ones(k)
    levels = np.array([20, -20, 10, -10, 0])
    a = np.random.permutation(np.resize(levels, k // 512 * 4)).reshape(k // 512, 4)
    idx = np.arange(k)
    return np.exp2(a[idx // 512, idx % 128 // 32])


BF16 = ml_dtypes.bfloat16


def bf(x):
    return np.asarray(x, np.float32).astype(BF16)


def f64(x):
    return np.asarray(x).astype(np.float64)


B, IN, OUT, G, P = 2048, 512, 512, 5, 3
NB = G + P
LO, HI = -1.0, 1.0


def silu(v):
    return v / (1.0 + np.exp(-v))


def dsilu(v):
    sg = 1.0 / (1.0 + np.exp(-v))
    return sg * (1.0 + v * (1.0 - sg))


def b_splines(x, grid, order=P):
    xe = x[..., None]
    bases = np.logical_and(xe >= grid[:, :-1], xe < grid[:, 1:]).astype(np.float64)
    for k in range(1, order + 1):
        left = (xe - grid[:, :-(k + 1)]) / (grid[:, k:-1] - grid[:, :-(k + 1)])
        right = (grid[:, k + 1:] - xe) / (grid[:, k + 1:] - grid[:, 1:-k])
        bases = left * bases[..., :-1] + right * bases[..., 1:]
    return bases


def db_splines(x, grid):
    n2 = b_splines(x, grid, P - 1)
    return P * (n2[..., :-1] / (grid[:, P:-1] - grid[:, :-(P + 1)])
                - n2[..., 1:] / (grid[:, P + 1:] - grid[:, 1:-P]))


def setup_inputs():
    u = mx_kscale(OUT)
    h = (HI - LO) / G
    g = np.arange(-P, G + P + 1) * h + LO
    x = np.random.uniform(LO, HI, (B, IN))
    base_weight = np.random.standard_normal((OUT, IN)) * 2.5 / np.sqrt(IN) / u[:, None]
    spline_weight = np.random.standard_normal((OUT, IN, NB))
    spline_scaler = np.random.standard_normal((OUT, IN)) * 1.5 / np.sqrt(IN) / u[:, None]
    grad_out = np.random.standard_normal((B, OUT)) * np.exp2(np.random.randint(-12, 1, (B, 1))) * 4.0 * u[None, :]
    return {"x": bf(x),
            "base_weight": bf(base_weight),
            "spline_weight": bf(spline_weight),
            "spline_scaler": bf(spline_scaler),
            "grid": bf(np.tile(g[None, :], (IN, 1))),
            "grad_out": bf(grad_out)}


def reference(x, base_weight, spline_weight, spline_scaler, grid, grad_out):
    x, grid = f64(x), f64(grid)
    gq = mxq(f64(grad_out), 1, "e5m2")
    gb = gq @ mxq(f64(base_weight), 0, "e4m3")
    ssw = (f64(spline_weight) * f64(spline_scaler)[..., None]).reshape(OUT, -1)
    gs = (gq @ mxq(ssw, 0, "e4m3")).reshape(x.shape[0], IN, NB)
    return gb * dsilu(x) + (gs * db_splines(x, grid)).sum(-1)

@@ -1,0 +1,296 @@
+from contextlib import ExitStack
+
+import concourse.mybir as mybir
+from concourse.masks import make_identity
+
+F32 = mybir.dt.float32
+BF16 = mybir.dt.bfloat16
+U32 = mybir.dt.uint32
+U8 = mybir.dt.uint8
+E4M3X4 = mybir.dt.float8_e4m3fn_x4
+E5M2X4 = mybir.dt.float8_e5m2_x4
+ALU = mybir.AluOpType
+ACT = mybir.ActivationFunctionType
+
+P = 128
+PACK = 4
+ROWS = 2048
+FEATURES = 512
+OUTPUTS = 512
+BASES = 8
+KNOTS = 12
+DEGREE_SPAN = 4
+FIRST_LEFT = 4
+N = 512
+I_TILES = FEATURES // P
+B_CHUNKS = ROWS // N
+B_SUB = N // P
+TERMS = BASES + 1
+
+FLOPS = 2 * ROWS * OUTPUTS * (FEATURES + FEATURES * BASES)
+
+
+def toward_edge(j):
+    return 1 if j >= FIRST_LEFT else -1
+
+
+def extra_terms(j):
+    return BASES - 1 - j if j >= FIRST_LEFT else j
+
+
+def spline_constants(nc, consts, grid):
+    knots_bf = consts.tile([P, I_TILES, KNOTS], BF16)
+    nc.sync.dma_start(out=knots_bf[:], in_=grid.rearrange("(t p) k -> p t k", p=P))
+    knots = consts.tile([P, I_TILES, KNOTS], F32)
+    nc.vector.tensor_copy(out=knots[:], in_=knots_bf[:])
+
+    left = slice(FIRST_LEFT, BASES)
+    right = slice(0, FIRST_LEFT)
+
+    relu_bias = consts.tile([P, I_TILES, BASES], F32)
+    nc.vector.tensor_scalar_mul(out=relu_bias[:, :, left], in0=knots[:, :, left], scalar1=-1.0)
+    nc.vector.tensor_copy(out=relu_bias[:, :, right], in_=knots[:, :, left])
+
+    den = consts.tile([P, DEGREE_SPAN + 1, I_TILES, BASES], F32)
+    diff = consts.tile([P, I_TILES, BASES], F32)
+    for a in range(DEGREE_SPAN + 1):
+        others = [c for c in range(DEGREE_SPAN + 1) if c != a]
+        nc.vector.tensor_sub(
+            out=den[:, a], in0=knots[:, :, a : a + BASES], in1=knots[:, :, others[0] : others[0] + BASES]
+        )
+        for c in others[1:]:
+            nc.vector.tensor_sub(out=diff[:], in0=knots[:, :, a : a + BASES], in1=knots[:, :, c : c + BASES])
+            nc.vector.tensor_mul(out=den[:, a], in0=den[:, a], in1=diff[:])
+    inv_den = consts.tile([P, DEGREE_SPAN + 1, I_TILES, BASES], F32)
+    nc.vector.reciprocal(out=inv_den[:], in_=den[:])
+
+    span = consts.tile([P, I_TILES, BASES], F32)
+    nc.vector.tensor_sub(out=span[:], in0=knots[:, :, DEGREE_SPAN:KNOTS], in1=knots[:, :, 0:BASES])
+    lead = consts.tile([P, I_TILES, BASES], F32)
+    nc.vector.scalar_tensor_tensor(
+        out=lead[:, :, left], in0=span[:, :, left], scalar=3.0, in1=inv_den[:, 0, :, left], op0=ALU.mult, op1=ALU.mult
+    )
+    nc.vector.scalar_tensor_tensor(
+        out=lead[:, :, right],
+        in0=span[:, :, right],
+        scalar=-3.0,
+        in1=inv_den[:, DEGREE_SPAN, :, right],
+        op0=ALU.mult,
+        op1=ALU.mult,
+    )
+
+    ratio = consts.tile([P, DEGREE_SPAN, I_TILES, BASES], F32)
+    for s in range(1, DEGREE_SPAN):
+        nc.vector.tensor_mul(out=ratio[:, s, :, left], in0=den[:, 0, :, left], in1=inv_den[:, s, :, left])
+        nc.vector.tensor_mul(
+            out=ratio[:, s, :, right],
+            in0=den[:, DEGREE_SPAN, :, right],
+            in1=inv_den[:, DEGREE_SPAN - s, :, right],
+        )
+    return relu_bias, lead, ratio
+
+
+def load_k_first(nc, tile, rows):
+    half = OUTPUTS // 2
+    for u in range(2):
+        nc.sync.dma_start(
+            out=tile[:, 2 * u : 2 * u + 2, :],
+            in_=rows[u * half : (u + 1) * half].rearrange("(p e) w -> p e w", e=2),
+        )
+
+
+def load_spline_tile(nc, pool, spline_flat, it):
+    spline_raw = pool.tile([P, PACK, P * BASES], BF16)
+    load_k_first(nc, spline_raw, spline_flat[:, it * P * BASES : (it + 1) * P * BASES])
+    return spline_raw
+
+
+def tile_bsplinekanlayer_t_kernel(
+    tc, x, base_weight, spline_weight, spline_scaler, grid, grad_out, out
+):
+    nc = tc.nc
+    with ExitStack() as ctx:
+        consts = ctx.enter_context(tc.tile_pool(name="consts", bufs=1))
+        keep = ctx.enter_context(tc.tile_pool(name="keep", bufs=1))
+        stage = ctx.enter_context(tc.tile_pool(name="stage", bufs=2))
+        feats = ctx.enter_context(tc.tile_pool(name="feats", bufs=2))
+        prods = ctx.enter_context(tc.tile_pool(name="prods", bufs=2))
+        banks = ctx.enter_context(tc.psum_pool(name="banks", bufs=6))
+        sums = ctx.enter_context(tc.psum_pool(name="sums", bufs=2))
+
+        relu_bias, lead, ratio = spline_constants(nc, consts, grid)
+        ident_f32 = consts.tile([P, P], F32)
+        make_identity(nc, ident_f32[:])
+        ident_bf = consts.tile([P, P], BF16)
+        make_identity(nc, ident_bf[:])
+
+        scaler_raw = keep.tile([P, PACK, FEATURES], BF16)
+        load_k_first(nc, scaler_raw, spline_scaler)
+        spline_flat = spline_weight.rearrange("o i j -> o (i j)")
+        spline_raw = [load_spline_tile(nc, stage, spline_flat, 0)]
+        g_raw = keep.tile([P, ROWS // P, OUTPUTS], BF16)
+        x_raw = keep.tile([P, ROWS // P, FEATURES], BF16)
+        base_raw = keep.tile([P, PACK, FEATURES], BF16)
+        for bc in range(B_CHUNKS):
+            rows = slice(bc * N, (bc + 1) * N)
+            subs = slice(bc * B_SUB, (bc + 1) * B_SUB)
+            nc.sync.dma_start(out=g_raw[:, subs, :], in_=grad_out[rows, :].rearrange("(t p) o -> p t o", p=P))
+            nc.sync.dma_start(out=x_raw[:, subs, :], in_=x[rows, :].rearrange("(t p) i -> p t i", p=P))
+            if bc == 0:
+                load_k_first(nc, base_raw, base_weight)
+        spline_raw.append(load_spline_tile(nc, stage, spline_flat, 1))
+
+        g_codes = keep.tile([P, ROWS], U32, align_bytes=64)
+        g_scales = keep.tile([P, ROWS], U8, align_bytes=64)
+        for bc in range(B_CHUNKS):
+            g_grouped = stage.tile([P, N, PACK], BF16, align_bytes=64)
+            g_words = g_grouped[:].rearrange("p b t -> p (b t)").bitcast(F32).rearrange("p (b u) -> p b u", u=2)
+            for pair in range(B_SUB // 2):
+                g_t = banks.tile([P, 2, 2, P], F32, tag="bank")
+                for t in range(2):
+                    words = g_raw[:, bc * B_SUB + 2 * pair + t, :].bitcast(F32)
+                    for u in range(2):
+                        nc.tensor.transpose(g_t[:, t, u, :], words[:, u * P : (u + 1) * P], ident_f32[:])
+                nc.scalar.copy(
+                    out=g_words[:, 2 * pair * P : (2 * pair + 2) * P, :].rearrange("p (t b) u -> p t b u", t=2),
+                    in_=g_t[:].rearrange("p t u b -> p t b u"),
+                )
+            cols = slice(bc * N, (bc + 1) * N)
+            nc.vector.quantize_mx(
+                out=g_codes[:, cols].bitcast(E5M2X4),
+                scales=g_scales[:, cols],
+                in_=g_grouped[:].rearrange("p b t -> p (b t)"),
+            )
+
+        x_t = keep.tile([P, I_TILES, ROWS], BF16)
+        for bc in range(B_CHUNKS):
+            for it in range(I_TILES):
+                x_bank = banks.tile([P, N], BF16, tag="bank")
+                for t in range(B_SUB):
+                    nc.tensor.transpose(
+                        x_bank[:, t * P : (t + 1) * P],
+                        x_raw[:, bc * B_SUB + t, it * P : (it + 1) * P],
+                        ident_bf[:],
+                    )
+                nc.scalar.copy(out=x_t[:, it, bc * N : (bc + 1) * N], in_=x_bank[:])
+
+        base_grouped = keep.tile([P, FEATURES, PACK], BF16, align_bytes=64)
+        nc.scalar.copy(out=base_grouped[:], in_=base_raw[:].rearrange("p t i -> p i t"))
+        base_codes = keep.tile([P, FEATURES], U32, align_bytes=64)
+        base_scales = keep.tile([P, FEATURES], U8, align_bytes=64)
+        nc.vector.quantize_mx(
+            out=base_codes[:].bitcast(E4M3X4),
+            scales=base_scales[:],
+            in_=base_grouped[:].rearrange("p i t -> p (i t)"),
+        )
+
+        ssw_codes = keep.tile([P, I_TILES, BASES * P], U32, align_bytes=64)
+        ssw_scales = keep.tile([P, I_TILES, BASES * P], U8, align_bytes=64)
+
+        for it in range(I_TILES):
+            i_cols = slice(it * P, (it + 1) * P)
+
+            ssw_grouped = stage.tile([P, BASES, P, PACK], BF16, align_bytes=64)
+            nc.vector.tensor_tensor(
+                out=ssw_grouped[:],
+                in0=spline_raw[it][:].rearrange("p t (i j) -> p j i t", j=BASES),
+                in1=scaler_raw[:, :, i_cols]
+                .rearrange("p t i -> p i t")
+                .unsqueeze(1)
+                .to_broadcast([P, BASES, P, PACK]),
+                op=ALU.mult,
+            )
+            nc.vector.quantize_mx(
+                out=ssw_codes[:, it, :].bitcast(E4M3X4),
+                scales=ssw_scales[:, it, :],
+                in_=ssw_grouped[:].rearrange("p j i t -> p (j i t)"),
+            )
+            if it + 2 < I_TILES:
+                spline_raw.append(load_spline_tile(nc, stage, spline_flat, it + 2))
+
+            for bc in range(B_CHUNKS):
+                b_cols = slice(bc * N, (bc + 1) * N)
+                v = x_t[:, it, b_cols]
+
+                f = []
+                for j in range(BASES):
+                    ramp = feats.tile([P, N], F32, tag="ramp")
+                    nc.scalar.activation(
+                        out=ramp[:],
+                        in_=v,
+                        func=ACT.Relu,
+                        bias=relu_bias[:, it, j : j + 1],
+                        scale=float(toward_edge(j)),
+                    )
+                    f.append(feats.tile([P, N], F32, name="f%d" % j))
+                    nc.scalar.activation(out=f[j][:], in_=ramp[:], func=ACT.Square)
+
+                sig = feats.tile([P, N], F32)
+                nc.scalar.activation(out=sig[:], in_=v, func=ACT.Sigmoid)
+                dsilu = feats.tile([P, N], F32)
+                nc.scalar.activation(out=dsilu[:], in_=v, func=ACT.Sigmoid, scale=-1.0)
+                nc.gpsimd.tensor_tensor(out=dsilu[:], in0=v, in1=dsilu[:], op=ALU.mult)
+                nc.gpsimd.tensor_tensor(out=dsilu[:], in0=dsilu[:], in1=sig[:], op=ALU.mult)
+                nc.gpsimd.tensor_tensor(out=dsilu[:], in0=dsilu[:], in1=sig[:], op=ALU.add)
+
+                for j_left in range(FIRST_LEFT, BASES - 1):
+                    j_right = BASES - 1 - j_left
+                    for s in range(1, extra_terms(j_left) + 1):
+                        for j in (j_left, j_right):
+                            nc.vector.scalar_tensor_tensor(
+                                out=f[j][:],
+                                in0=f[j + s * toward_edge(j)][:],
+                                scalar=ratio[:, s, it, j : j + 1],
+                                in1=f[j][:],
+                                op0=ALU.mult,
+                                op1=ALU.add,
+                            )
+
+                prod = []
+                for j in range(TERMS):
+                    bank = banks.tile([P, N], F32, tag="bank")
+                    if j < BASES:
+                        w_codes = ssw_codes[:, it, j * P : (j + 1) * P]
+                        w_scales = ssw_scales[:, it, j * P : (j + 1) * P]
+                    else:
+                        w_codes = base_codes[:, i_cols]
+                        w_scales = base_scales[:, i_cols]
+                    nc.tensor.matmul_mx(
+                        out=bank[:],
+                        lhsT=w_codes.bitcast(E4M3X4),
+                        lhsT_scale=w_scales,
+                        rhs=g_codes[:, b_cols].bitcast(E5M2X4),
+                        rhs_scale=g_scales[:, b_cols],
+                        start=True,
+                        stop=True,
+                    )
+                    prod.append(prods.tile([P, N], F32, name="prod%d" % j))
+                    if j < BASES:
+                        nc.vector.scalar_tensor_tensor(
+                            out=prod[j][:],
+                            in0=bank[:],
+                            scalar=lead[:, it, j : j + 1],
+                            in1=f[j][:],
+                            op0=ALU.mult,
+                            op1=ALU.mult,
+                        )
+                    else:
+                        nc.vector.tensor_tensor(out=prod[j][:], in0=bank[:], in1=dsilu[:], op=ALU.mult)
+
+                total = sums.tile([P, B_SUB, P], F32)
+                for t in range(B_SUB):
+                    for j in range(TERMS):
+                        nc.tensor.matmul(
+                            out=total[:, t, :],
+                            lhsT=prod[j][:, t * P : (t + 1) * P],
+                            rhs=ident_f32[:],
+                            is_transpose=True,
+                            start=(j == 0),
+                            stop=(j == TERMS - 1),
+                        )
+                result = stage.tile([P, B_SUB, P], F32)
+                nc.scalar.copy(out=result[:], in_=total[:])
+                nc.sync.dma_start(
+                    out=out[b_cols, i_cols].rearrange("(t p) i -> p t i", p=P),
+                    in_=result[:],
+                )

@@ -229,9 +229,10 @@ def tile_bsplinekanlayer_t_kernel(
                 nc.scalar.activation(out=sig[:], in_=v, func=ACT.Sigmoid)
                 dsilu = feats.tile([P, N], F32)
                 nc.scalar.activation(out=dsilu[:], in_=v, func=ACT.Sigmoid, scale=-1.0)
-                nc.gpsimd.tensor_tensor(out=dsilu[:], in0=v, in1=dsilu[:], op=ALU.mult)
-                nc.gpsimd.tensor_tensor(out=dsilu[:], in0=dsilu[:], in1=sig[:], op=ALU.mult)
-                nc.gpsimd.tensor_tensor(out=dsilu[:], in0=dsilu[:], in1=sig[:], op=ALU.add)
+                nc.vector.tensor_tensor(out=dsilu[:], in0=v, in1=dsilu[:], op=ALU.mult)
+                nc.vector.scalar_tensor_tensor(
+                    out=dsilu[:], in0=dsilu[:], scalar=1.0, in1=sig[:], op0=ALU.add, op1=ALU.mult
+                )
 
                 for j_left in range(FIRST_LEFT, BASES - 1):
                     j_right = BASES - 1 - j_left

@@ -22,6 +22,7 @@ KNOTS = 12
 DEGREE_SPAN = 4
 FIRST_LEFT = 4
 N = 512
+X_COLS = 1024
 I_TILES = FEATURES // P
 B_CHUNKS = ROWS // N
 B_SUB = N // P
@@ -112,9 +113,7 @@ def tile_bsplinekanlayer_t_kernel(
     with ExitStack() as ctx:
         consts = ctx.enter_context(tc.tile_pool(name="consts", bufs=1))
         keep = ctx.enter_context(tc.tile_pool(name="keep", bufs=1))
-        stage = ctx.enter_context(tc.tile_pool(name="stage", bufs=2))
-        feats = ctx.enter_context(tc.tile_pool(name="feats", bufs=2))
-        prods = ctx.enter_context(tc.tile_pool(name="prods", bufs=2))
+        weights = ctx.enter_context(tc.tile_pool(name="weights", bufs=2))
         banks = ctx.enter_context(tc.psum_pool(name="banks", bufs=6))
         sums = ctx.enter_context(tc.psum_pool(name="sums", bufs=2))
 
@@ -124,73 +123,79 @@ def tile_bsplinekanlayer_t_kernel(
         ident_bf = consts.tile([P, P], BF16)
         make_identity(nc, ident_bf[:])
 
-        scaler_raw = keep.tile([P, PACK, FEATURES], BF16)
-        load_k_first(nc, scaler_raw, spline_scaler)
-        spline_flat = spline_weight.rearrange("o i j -> o (i j)")
-        spline_raw = [load_spline_tile(nc, stage, spline_flat, 0)]
-        g_raw = keep.tile([P, ROWS // P, OUTPUTS], BF16)
-        x_raw = keep.tile([P, ROWS // P, FEATURES], BF16)
-        base_raw = keep.tile([P, PACK, FEATURES], BF16)
-        for bc in range(B_CHUNKS):
-            rows = slice(bc * N, (bc + 1) * N)
-            subs = slice(bc * B_SUB, (bc + 1) * B_SUB)
-            nc.sync.dma_start(out=g_raw[:, subs, :], in_=grad_out[rows, :].rearrange("(t p) o -> p t o", p=P))
-            nc.sync.dma_start(out=x_raw[:, subs, :], in_=x[rows, :].rearrange("(t p) i -> p t i", p=P))
-            if bc == 0:
-                load_k_first(nc, base_raw, base_weight)
-        spline_raw.append(load_spline_tile(nc, stage, spline_flat, 1))
-
         g_codes = keep.tile([P, ROWS], U32, align_bytes=64)
         g_scales = keep.tile([P, ROWS], U8, align_bytes=64)
-        for bc in range(B_CHUNKS):
-            g_grouped = stage.tile([P, N, PACK], BF16, align_bytes=64)
-            g_words = g_grouped[:].rearrange("p b t -> p (b t)").bitcast(F32).rearrange("p (b u) -> p b u", u=2)
-            for pair in range(B_SUB // 2):
-                g_t = banks.tile([P, 2, 2, P], F32, tag="bank")
-                for t in range(2):
-                    words = g_raw[:, bc * B_SUB + 2 * pair + t, :].bitcast(F32)
-                    for u in range(2):
-                        nc.tensor.transpose(g_t[:, t, u, :], words[:, u * P : (u + 1) * P], ident_f32[:])
-                nc.scalar.copy(
-                    out=g_words[:, 2 * pair * P : (2 * pair + 2) * P, :].rearrange("p (t b) u -> p t b u", t=2),
-                    in_=g_t[:].rearrange("p t u b -> p t b u"),
-                )
-            cols = slice(bc * N, (bc + 1) * N)
-            nc.vector.quantize_mx(
-                out=g_codes[:, cols].bitcast(E5M2X4),
-                scales=g_scales[:, cols],
-                in_=g_grouped[:].rearrange("p b t -> p (b t)"),
-            )
-
         x_t = keep.tile([P, I_TILES, ROWS], BF16)
-        for bc in range(B_CHUNKS):
-            for it in range(I_TILES):
-                x_bank = banks.tile([P, N], BF16, tag="bank")
-                for t in range(B_SUB):
-                    nc.tensor.transpose(
-                        x_bank[:, t * P : (t + 1) * P],
-                        x_raw[:, bc * B_SUB + t, it * P : (it + 1) * P],
-                        ident_bf[:],
-                    )
-                nc.scalar.copy(out=x_t[:, it, bc * N : (bc + 1) * N], in_=x_bank[:])
-
-        base_grouped = keep.tile([P, FEATURES, PACK], BF16, align_bytes=64)
-        nc.scalar.copy(out=base_grouped[:], in_=base_raw[:].rearrange("p t i -> p i t"))
         base_codes = keep.tile([P, FEATURES], U32, align_bytes=64)
         base_scales = keep.tile([P, FEATURES], U8, align_bytes=64)
-        nc.vector.quantize_mx(
-            out=base_codes[:].bitcast(E4M3X4),
-            scales=base_scales[:],
-            in_=base_grouped[:].rearrange("p i t -> p (i t)"),
-        )
-
         ssw_codes = keep.tile([P, I_TILES, BASES * P], U32, align_bytes=64)
         ssw_scales = keep.tile([P, I_TILES, BASES * P], U8, align_bytes=64)
+
+        with tc.tile_pool(name="raw", bufs=1) as raw, tc.tile_pool(name="grouped", bufs=2) as grouped:
+            scaler_raw = keep.tile([P, PACK, FEATURES], BF16)
+            load_k_first(nc, scaler_raw, spline_scaler)
+            spline_flat = spline_weight.rearrange("o i j -> o (i j)")
+            spline_raw = [load_spline_tile(nc, weights, spline_flat, 0)]
+            g_raw = raw.tile([P, ROWS // P, OUTPUTS], BF16)
+            x_raw = raw.tile([P, ROWS // P, FEATURES], BF16)
+            base_raw = raw.tile([P, PACK, FEATURES], BF16)
+            for bc in range(B_CHUNKS):
+                rows = slice(bc * N, (bc + 1) * N)
+                subs = slice(bc * B_SUB, (bc + 1) * B_SUB)
+                nc.sync.dma_start(out=g_raw[:, subs, :], in_=grad_out[rows, :].rearrange("(t p) o -> p t o", p=P))
+                nc.sync.dma_start(out=x_raw[:, subs, :], in_=x[rows, :].rearrange("(t p) i -> p t i", p=P))
+                if bc == 0:
+                    load_k_first(nc, base_raw, base_weight)
+            spline_raw.append(load_spline_tile(nc, weights, spline_flat, 1))
+
+            for bc in range(B_CHUNKS):
+                g_grouped = grouped.tile([P, N, PACK], BF16, align_bytes=64)
+                g_words = (
+                    g_grouped[:].rearrange("p b t -> p (b t)").bitcast(F32).rearrange("p (b u) -> p b u", u=2)
+                )
+                for pair in range(B_SUB // 2):
+                    g_t = banks.tile([P, 2, 2, P], F32, tag="bank")
+                    for t in range(2):
+                        words = g_raw[:, bc * B_SUB + 2 * pair + t, :].bitcast(F32)
+                        for u in range(2):
+                            nc.tensor.transpose(g_t[:, t, u, :], words[:, u * P : (u + 1) * P], ident_f32[:])
+                    nc.scalar.copy(
+                        out=g_words[:, 2 * pair * P : (2 * pair + 2) * P, :].rearrange("p (t b) u -> p t b u", t=2),
+                        in_=g_t[:].rearrange("p t u b -> p t b u"),
+                    )
+                cols = slice(bc * N, (bc + 1) * N)
+                nc.vector.quantize_mx(
+                    out=g_codes[:, cols].bitcast(E5M2X4),
+                    scales=g_scales[:, cols],
+                    in_=g_grouped[:].rearrange("p b t -> p (b t)"),
+                )
+
+            for bc in range(B_CHUNKS):
+                for it in range(I_TILES):
+                    x_bank = banks.tile([P, N], BF16, tag="bank")
+                    for t in range(B_SUB):
+                        nc.tensor.transpose(
+                            x_bank[:, t * P : (t + 1) * P],
+                            x_raw[:, bc * B_SUB + t, it * P : (it + 1) * P],
+                            ident_bf[:],
+                        )
+                    nc.scalar.copy(out=x_t[:, it, bc * N : (bc + 1) * N], in_=x_bank[:])
+
+            base_grouped = raw.tile([P, FEATURES, PACK], BF16, align_bytes=64)
+            nc.scalar.copy(out=base_grouped[:], in_=base_raw[:].rearrange("p t i -> p i t"))
+            nc.vector.quantize_mx(
+                out=base_codes[:].bitcast(E4M3X4),
+                scales=base_scales[:],
+                in_=base_grouped[:].rearrange("p i t -> p (i t)"),
+            )
+
+        feats = ctx.enter_context(tc.tile_pool(name="feats", bufs=2, reuse_waits="tile"))
+        prods = ctx.enter_context(tc.tile_pool(name="prods", bufs=2, reuse_waits="tile"))
 
         for it in range(I_TILES):
             i_cols = slice(it * P, (it + 1) * P)
 
-            ssw_grouped = stage.tile([P, BASES, P, PACK], BF16, align_bytes=64)
+            ssw_grouped = weights.tile([P, BASES, P, PACK], BF16, align_bytes=64)
             nc.vector.tensor_tensor(
                 out=ssw_grouped[:],
                 in0=spline_raw[it][:].rearrange("p t (i j) -> p j i t", j=BASES),
@@ -206,15 +211,14 @@ def tile_bsplinekanlayer_t_kernel(
                 in_=ssw_grouped[:].rearrange("p j i t -> p (j i t)"),
             )
             if it + 2 < I_TILES:
-                spline_raw.append(load_spline_tile(nc, stage, spline_flat, it + 2))
+                spline_raw.append(load_spline_tile(nc, weights, spline_flat, it + 2))
 
-            for bc in range(B_CHUNKS):
-                b_cols = slice(bc * N, (bc + 1) * N)
-                v = x_t[:, it, b_cols]
+            for xc in range(ROWS // X_COLS):
+                v = x_t[:, it, xc * X_COLS : (xc + 1) * X_COLS]
 
                 f = []
                 for j in range(BASES):
-                    ramp = feats.tile([P, N], F32, tag="ramp")
+                    ramp = feats.tile([P, X_COLS], F32, tag="ramp")
                     nc.scalar.activation(
                         out=ramp[:],
                         in_=v,
@@ -222,12 +226,12 @@ def tile_bsplinekanlayer_t_kernel(
                         bias=relu_bias[:, it, j : j + 1],
                         scale=float(toward_edge(j)),
                     )
-                    f.append(feats.tile([P, N], F32, name="f%d" % j))
+                    f.append(feats.tile([P, X_COLS], F32, name="f%d" % j))
                     nc.scalar.activation(out=f[j][:], in_=ramp[:], func=ACT.Square)
 
-                sig = feats.tile([P, N], F32)
+                sig = feats.tile([P, X_COLS], F32)
                 nc.scalar.activation(out=sig[:], in_=v, func=ACT.Sigmoid)
-                dsilu = feats.tile([P, N], F32)
+                dsilu = feats.tile([P, X_COLS], F32)
                 nc.scalar.activation(out=dsilu[:], in_=v, func=ACT.Sigmoid, scale=-1.0)
                 nc.vector.tensor_tensor(out=dsilu[:], in0=v, in1=dsilu[:], op=ALU.mult)
                 nc.vector.scalar_tensor_tensor(
@@ -247,51 +251,55 @@ def tile_bsplinekanlayer_t_kernel(
                                 op1=ALU.add,
                             )
 
-                prod = []
-                for j in range(TERMS):
-                    bank = banks.tile([P, N], F32, tag="bank")
-                    if j < BASES:
-                        w_codes = ssw_codes[:, it, j * P : (j + 1) * P]
-                        w_scales = ssw_scales[:, it, j * P : (j + 1) * P]
-                    else:
-                        w_codes = base_codes[:, i_cols]
-                        w_scales = base_scales[:, i_cols]
-                    nc.tensor.matmul_mx(
-                        out=bank[:],
-                        lhsT=w_codes.bitcast(E4M3X4),
-                        lhsT_scale=w_scales,
-                        rhs=g_codes[:, b_cols].bitcast(E5M2X4),
-                        rhs_scale=g_scales[:, b_cols],
-                        start=True,
-                        stop=True,
-                    )
-                    prod.append(prods.tile([P, N], F32, name="prod%d" % j))
-                    if j < BASES:
-                        nc.vector.scalar_tensor_tensor(
-                            out=prod[j][:],
-                            in0=bank[:],
-                            scalar=lead[:, it, j : j + 1],
-                            in1=f[j][:],
-                            op0=ALU.mult,
-                            op1=ALU.mult,
-                        )
-                    else:
-                        nc.vector.tensor_tensor(out=prod[j][:], in0=bank[:], in1=dsilu[:], op=ALU.mult)
+                for c in range(X_COLS // N):
+                    here = slice(c * N, (c + 1) * N)
+                    b_cols = slice(xc * X_COLS + c * N, xc * X_COLS + (c + 1) * N)
 
-                total = sums.tile([P, B_SUB, P], F32)
-                for t in range(B_SUB):
+                    prod = []
                     for j in range(TERMS):
-                        nc.tensor.matmul(
-                            out=total[:, t, :],
-                            lhsT=prod[j][:, t * P : (t + 1) * P],
-                            rhs=ident_f32[:],
-                            is_transpose=True,
-                            start=(j == 0),
-                            stop=(j == TERMS - 1),
+                        bank = banks.tile([P, N], F32, tag="bank")
+                        if j < BASES:
+                            w_codes = ssw_codes[:, it, j * P : (j + 1) * P]
+                            w_scales = ssw_scales[:, it, j * P : (j + 1) * P]
+                        else:
+                            w_codes = base_codes[:, i_cols]
+                            w_scales = base_scales[:, i_cols]
+                        nc.tensor.matmul_mx(
+                            out=bank[:],
+                            lhsT=w_codes.bitcast(E4M3X4),
+                            lhsT_scale=w_scales,
+                            rhs=g_codes[:, b_cols].bitcast(E5M2X4),
+                            rhs_scale=g_scales[:, b_cols],
+                            start=True,
+                            stop=True,
                         )
-                result = stage.tile([P, B_SUB, P], F32)
-                nc.scalar.copy(out=result[:], in_=total[:])
-                nc.sync.dma_start(
-                    out=out[b_cols, i_cols].rearrange("(t p) i -> p t i", p=P),
-                    in_=result[:],
-                )
+                        prod.append(prods.tile([P, N], F32, name="prod%d" % j))
+                        if j < BASES:
+                            nc.vector.scalar_tensor_tensor(
+                                out=prod[j][:],
+                                in0=bank[:],
+                                scalar=lead[:, it, j : j + 1],
+                                in1=f[j][:, here],
+                                op0=ALU.mult,
+                                op1=ALU.mult,
+                            )
+                        else:
+                            nc.vector.tensor_tensor(out=prod[j][:], in0=bank[:], in1=dsilu[:, here], op=ALU.mult)
+
+                    total = sums.tile([P, B_SUB, P], F32)
+                    for t in range(B_SUB):
+                        for j in range(TERMS):
+                            nc.tensor.matmul(
+                                out=total[:, t, :],
+                                lhsT=prod[j][:, t * P : (t + 1) * P],
+                                rhs=ident_f32[:],
+                                is_transpose=True,
+                                start=(j == 0),
+                                stop=(j == TERMS - 1),
+                            )
+                    result = prods.tile([P, B_SUB, P], F32)
+                    nc.scalar.copy(out=result[:], in_=total[:])
+                    nc.sync.dma_start(
+                        out=out[b_cols, i_cols].rearrange("(t p) i -> p t i", p=P),
+                        in_=result[:],
+                    )

@@ -114,6 +114,7 @@ def tile_bsplinekanlayer_t_kernel(
         consts = ctx.enter_context(tc.tile_pool(name="consts", bufs=1))
         keep = ctx.enter_context(tc.tile_pool(name="keep", bufs=1))
         weights = ctx.enter_context(tc.tile_pool(name="weights", bufs=2))
+        feats = ctx.enter_context(tc.tile_pool(name="feats", bufs=2))
         banks = ctx.enter_context(tc.psum_pool(name="banks", bufs=6))
         sums = ctx.enter_context(tc.psum_pool(name="sums", bufs=2))
 
@@ -130,26 +131,59 @@ def tile_bsplinekanlayer_t_kernel(
         base_scales = keep.tile([P, FEATURES], U8, align_bytes=64)
         ssw_codes = keep.tile([P, I_TILES, BASES * P], U32, align_bytes=64)
         ssw_scales = keep.tile([P, I_TILES, BASES * P], U8, align_bytes=64)
+        scaler_sorted = keep.tile([P, FEATURES, PACK], BF16)
 
-        with tc.tile_pool(name="raw", bufs=1) as raw, tc.tile_pool(name="grouped", bufs=2) as grouped:
-            scaler_raw = keep.tile([P, PACK, FEATURES], BF16)
-            load_k_first(nc, scaler_raw, spline_scaler)
-            spline_flat = spline_weight.rearrange("o i j -> o (i j)")
-            spline_raw = [load_spline_tile(nc, weights, spline_flat, 0)]
+        spline_flat = spline_weight.rearrange("o i j -> o (i j)")
+        spline_raw = []
+
+        def prepare_ssw(it, sorting_copy):
+            ssw_grouped = weights.tile([P, BASES, P * PACK], BF16, align_bytes=64)
+            sorting_copy(
+                out=ssw_grouped[:].rearrange("p j (i t) -> p j i t", t=PACK),
+                in_=spline_raw[it][:].rearrange("p t (i j) -> p j i t", j=BASES),
+            )
+            nc.vector.tensor_tensor(
+                out=ssw_grouped[:],
+                in0=ssw_grouped[:],
+                in1=scaler_sorted[:, it * P : (it + 1) * P, :]
+                .rearrange("p i t -> p (i t)")
+                .unsqueeze(1)
+                .to_broadcast([P, BASES, P * PACK]),
+                op=ALU.mult,
+            )
+            nc.vector.quantize_mx(
+                out=ssw_codes[:, it, :].bitcast(E4M3X4),
+                scales=ssw_scales[:, it, :],
+                in_=ssw_grouped[:].rearrange("p j w -> p (j w)"),
+            )
+            if it + 2 < I_TILES:
+                spline_raw.append(load_spline_tile(nc, weights, spline_flat, it + 2))
+
+        with tc.tile_pool(name="raw", bufs=1) as raw:
             g_raw = raw.tile([P, ROWS // P, OUTPUTS], BF16)
             x_raw = raw.tile([P, ROWS // P, FEATURES], BF16)
+            scaler_raw = raw.tile([P, PACK, FEATURES], BF16)
             base_raw = raw.tile([P, PACK, FEATURES], BF16)
-            for bc in range(B_CHUNKS):
-                rows = slice(bc * N, (bc + 1) * N)
-                subs = slice(bc * B_SUB, (bc + 1) * B_SUB)
-                nc.sync.dma_start(out=g_raw[:, subs, :], in_=grad_out[rows, :].rearrange("(t p) o -> p t o", p=P))
-                nc.sync.dma_start(out=x_raw[:, subs, :], in_=x[rows, :].rearrange("(t p) i -> p t i", p=P))
-                if bc == 0:
-                    load_k_first(nc, base_raw, base_weight)
-            spline_raw.append(load_spline_tile(nc, weights, spline_flat, 1))
 
-            for bc in range(B_CHUNKS):
-                g_grouped = grouped.tile([P, N, PACK], BF16, align_bytes=64)
+            def load_rows(tile, rows_in_dram, bc):
+                nc.sync.dma_start(
+                    out=tile[:, bc * B_SUB : (bc + 1) * B_SUB, :],
+                    in_=rows_in_dram[bc * N : (bc + 1) * N, :].rearrange("(t p) c -> p t c", p=P),
+                )
+
+            def transpose_x(bc):
+                for it in range(I_TILES):
+                    x_bank = banks.tile([P, N], BF16, tag="bank")
+                    for t in range(B_SUB):
+                        nc.tensor.transpose(
+                            x_bank[:, t * P : (t + 1) * P],
+                            x_raw[:, bc * B_SUB + t, it * P : (it + 1) * P],
+                            ident_bf[:],
+                        )
+                    nc.vector.tensor_copy(out=x_t[:, it, bc * N : (bc + 1) * N], in_=x_bank[:])
+
+            def quantise_g(bc):
+                g_grouped = raw.tile([P, N, PACK], BF16, align_bytes=64)
                 g_words = (
                     g_grouped[:].rearrange("p b t -> p (b t)").bitcast(F32).rearrange("p (b u) -> p b u", u=2)
                 )
@@ -159,7 +193,7 @@ def tile_bsplinekanlayer_t_kernel(
                         words = g_raw[:, bc * B_SUB + 2 * pair + t, :].bitcast(F32)
                         for u in range(2):
                             nc.tensor.transpose(g_t[:, t, u, :], words[:, u * P : (u + 1) * P], ident_f32[:])
-                    nc.scalar.copy(
+                    nc.vector.tensor_copy(
                         out=g_words[:, 2 * pair * P : (2 * pair + 2) * P, :].rearrange("p (t b) u -> p t b u", t=2),
                         in_=g_t[:].rearrange("p t u b -> p t b u"),
                     )
@@ -170,50 +204,47 @@ def tile_bsplinekanlayer_t_kernel(
                     in_=g_grouped[:].rearrange("p b t -> p (b t)"),
                 )
 
-            for bc in range(B_CHUNKS):
-                for it in range(I_TILES):
-                    x_bank = banks.tile([P, N], BF16, tag="bank")
-                    for t in range(B_SUB):
-                        nc.tensor.transpose(
-                            x_bank[:, t * P : (t + 1) * P],
-                            x_raw[:, bc * B_SUB + t, it * P : (it + 1) * P],
-                            ident_bf[:],
-                        )
-                    nc.scalar.copy(out=x_t[:, it, bc * N : (bc + 1) * N], in_=x_bank[:])
+            first = range(X_COLS // N)
+            later = range(X_COLS // N, B_CHUNKS)
+            for bc in first:
+                load_rows(x_raw, x, bc)
+            load_k_first(nc, scaler_raw, spline_scaler)
+            spline_raw.append(load_spline_tile(nc, weights, spline_flat, 0))
+            for bc in first:
+                load_rows(g_raw, grad_out, bc)
+            load_k_first(nc, base_raw, base_weight)
+            for bc in later:
+                load_rows(x_raw, x, bc)
+                load_rows(g_raw, grad_out, bc)
+            spline_raw.append(load_spline_tile(nc, weights, spline_flat, 1))
 
+            for bc in first:
+                transpose_x(bc)
+            nc.vector.tensor_copy(out=scaler_sorted[:], in_=scaler_raw[:].rearrange("p t i -> p i t"))
+            prepare_ssw(0, nc.vector.tensor_copy)
+            for bc in first:
+                quantise_g(bc)
             base_grouped = raw.tile([P, FEATURES, PACK], BF16, align_bytes=64)
-            nc.scalar.copy(out=base_grouped[:], in_=base_raw[:].rearrange("p t i -> p i t"))
+            nc.vector.tensor_copy(out=base_grouped[:], in_=base_raw[:].rearrange("p t i -> p i t"))
             nc.vector.quantize_mx(
                 out=base_codes[:].bitcast(E4M3X4),
                 scales=base_scales[:],
                 in_=base_grouped[:].rearrange("p i t -> p (i t)"),
             )
+            for bc in later:
+                transpose_x(bc)
+                quantise_g(bc)
 
-        feats = ctx.enter_context(tc.tile_pool(name="feats", bufs=2, reuse_waits="tile"))
         prods = ctx.enter_context(tc.tile_pool(name="prods", bufs=2, reuse_waits="tile"))
+        scratch = ctx.enter_context(tc.tile_pool(name="scratch", bufs=1, reuse_waits="tile"))
 
         for it in range(I_TILES):
             i_cols = slice(it * P, (it + 1) * P)
 
-            ssw_grouped = weights.tile([P, BASES, P, PACK], BF16, align_bytes=64)
-            nc.vector.tensor_tensor(
-                out=ssw_grouped[:],
-                in0=spline_raw[it][:].rearrange("p t (i j) -> p j i t", j=BASES),
-                in1=scaler_raw[:, :, i_cols]
-                .rearrange("p t i -> p i t")
-                .unsqueeze(1)
-                .to_broadcast([P, BASES, P, PACK]),
-                op=ALU.mult,
-            )
-            nc.vector.quantize_mx(
-                out=ssw_codes[:, it, :].bitcast(E4M3X4),
-                scales=ssw_scales[:, it, :],
-                in_=ssw_grouped[:].rearrange("p j i t -> p (j i t)"),
-            )
-            if it + 2 < I_TILES:
-                spline_raw.append(load_spline_tile(nc, weights, spline_flat, it + 2))
-
             for xc in range(ROWS // X_COLS):
+                if xc == ROWS // X_COLS - 1 and it + 1 < I_TILES:
+                    prepare_ssw(it + 1, nc.scalar.copy)
+
                 v = x_t[:, it, xc * X_COLS : (xc + 1) * X_COLS]
 
                 f = []
@@ -229,14 +260,15 @@ def tile_bsplinekanlayer_t_kernel(
                     f.append(feats.tile([P, X_COLS], F32, name="f%d" % j))
                     nc.scalar.activation(out=f[j][:], in_=ramp[:], func=ACT.Square)
 
-                sig = feats.tile([P, X_COLS], F32)
-                nc.scalar.activation(out=sig[:], in_=v, func=ACT.Sigmoid)
-                dsilu = feats.tile([P, X_COLS], F32)
-                nc.scalar.activation(out=dsilu[:], in_=v, func=ACT.Sigmoid, scale=-1.0)
-                nc.vector.tensor_tensor(out=dsilu[:], in0=v, in1=dsilu[:], op=ALU.mult)
-                nc.vector.scalar_tensor_tensor(
-                    out=dsilu[:], in0=dsilu[:], scalar=1.0, in1=sig[:], op0=ALU.add, op1=ALU.mult
-                )
+                if xc == 0:
+                    v_all = x_t[:, it, :]
+                    sig = scratch.tile([P, ROWS], F32)
+                    nc.scalar.activation(out=sig[:], in_=v_all, func=ACT.Sigmoid)
+                    neg_dsilu = feats.tile([P, ROWS], F32)
+                    nc.scalar.activation(out=neg_dsilu[:], in_=v_all, func=ACT.Silu, scale=-1.0)
+                    nc.vector.scalar_tensor_tensor(
+                        out=neg_dsilu[:], in0=neg_dsilu[:], scalar=1.0, in1=sig[:], op0=ALU.subtract, op1=ALU.mult
+                    )
 
                 for j_left in range(FIRST_LEFT, BASES - 1):
                     j_right = BASES - 1 - j_left
@@ -284,7 +316,14 @@ def tile_bsplinekanlayer_t_kernel(
                                 op1=ALU.mult,
                             )
                         else:
-                            nc.vector.tensor_tensor(out=prod[j][:], in0=bank[:], in1=dsilu[:, here], op=ALU.mult)
+                            nc.vector.scalar_tensor_tensor(
+                                out=prod[j][:],
+                                in0=bank[:],
+                                scalar=-1.0,
+                                in1=neg_dsilu[:, b_cols],
+                                op0=ALU.mult,
+                                op1=ALU.mult,
+                            )
 
                     total = sums.tile([P, B_SUB, P], F32)
                     for t in range(B_SUB):

@@ -238,6 +238,23 @@ def tile_bsplinekanlayer_t_kernel(
         prods = ctx.enter_context(tc.tile_pool(name="prods", bufs=2, reuse_waits="tile"))
         scratch = ctx.enter_context(tc.tile_pool(name="scratch", bufs=1, reuse_waits="tile"))
 
+        def add_up_and_store(prod, b_cols, i_cols):
+            total = sums.tile([P, B_SUB, P], F32)
+            for t in range(B_SUB):
+                for j in range(TERMS):
+                    nc.tensor.matmul(
+                        out=total[:, t, :],
+                        lhsT=prod[j][:, t * P : (t + 1) * P],
+                        rhs=ident_f32[:],
+                        is_transpose=True,
+                        start=(j == 0),
+                        stop=(j == TERMS - 1),
+                    )
+            result = prods.tile([P, B_SUB, P], F32)
+            nc.scalar.copy(out=result[:], in_=total[:])
+            nc.sync.dma_start(out=out[b_cols, i_cols].rearrange("(t p) i -> p t i", p=P), in_=result[:])
+
+        waiting = None
         for it in range(I_TILES):
             i_cols = slice(it * P, (it + 1) * P)
 
@@ -325,20 +342,7 @@ def tile_bsplinekanlayer_t_kernel(
                                 op1=ALU.mult,
                             )
 
-                    total = sums.tile([P, B_SUB, P], F32)
-                    for t in range(B_SUB):
-                        for j in range(TERMS):
-                            nc.tensor.matmul(
-                                out=total[:, t, :],
-                                lhsT=prod[j][:, t * P : (t + 1) * P],
-                                rhs=ident_f32[:],
-                                is_transpose=True,
-                                start=(j == 0),
-                                stop=(j == TERMS - 1),
-                            )
-                    result = prods.tile([P, B_SUB, P], F32)
-                    nc.scalar.copy(out=result[:], in_=total[:])
-                    nc.sync.dma_start(
-                        out=out[b_cols, i_cols].rearrange("(t p) i -> p t i", p=P),
-                        in_=result[:],
-                    )
+                    if waiting:
+                        add_up_and_store(*waiting)
+                    waiting = (prod, b_cols, i_cols)
+        add_up_and_store(*waiting)

@@ -19,10 +19,9 @@ FEATURES = 512
 OUTPUTS = 512
 BASES = 8
 KNOTS = 12
-DEGREE_SPAN = 4
+SPAN = 4
 FIRST_LEFT = 4
 N = 512
-X_COLS = 1024
 I_TILES = FEATURES // P
 B_CHUNKS = ROWS // N
 B_SUB = N // P
@@ -30,65 +29,69 @@ TERMS = BASES + 1
 
 FLOPS = 2 * ROWS * OUTPUTS * (FEATURES + FEATURES * BASES)
 
+LEFT = slice(FIRST_LEFT, BASES)
+RIGHT = slice(0, FIRST_LEFT)
+
 
 def toward_edge(j):
     return 1 if j >= FIRST_LEFT else -1
 
 
-def extra_terms(j):
-    return BASES - 1 - j if j >= FIRST_LEFT else j
+def chain_steps():
+    steps = []
+    for j_left in range(FIRST_LEFT, BASES - 1):
+        for s in range(1, BASES - j_left):
+            steps.append((j_left, s))
+            steps.append((BASES - 1 - j_left, s))
+    return steps
 
 
-def spline_constants(nc, consts, grid):
-    knots_bf = consts.tile([P, I_TILES, KNOTS], BF16)
-    nc.sync.dma_start(out=knots_bf[:], in_=grid.rearrange("(t p) k -> p t k", p=P))
-    knots = consts.tile([P, I_TILES, KNOTS], F32)
-    nc.vector.tensor_copy(out=knots[:], in_=knots_bf[:])
-
-    left = slice(FIRST_LEFT, BASES)
-    right = slice(0, FIRST_LEFT)
-
+def load_knots(nc, consts, grid):
+    knots = consts.tile([P, I_TILES, KNOTS], BF16)
+    nc.sync.dma_start(out=knots[:], in_=grid.rearrange("(t p) k -> p t k", p=P))
     relu_bias = consts.tile([P, I_TILES, BASES], F32)
-    nc.vector.tensor_scalar_mul(out=relu_bias[:, :, left], in0=knots[:, :, left], scalar1=-1.0)
-    nc.vector.tensor_copy(out=relu_bias[:, :, right], in_=knots[:, :, left])
+    nc.vector.tensor_scalar_mul(out=relu_bias[:, :, LEFT], in0=knots[:, :, LEFT], scalar1=-1.0)
+    nc.vector.tensor_copy(out=relu_bias[:, :, RIGHT], in_=knots[:, :, LEFT])
+    return knots, relu_bias
 
-    den = consts.tile([P, DEGREE_SPAN + 1, I_TILES, BASES], F32)
-    diff = consts.tile([P, I_TILES, BASES], F32)
-    for a in range(DEGREE_SPAN + 1):
-        others = [c for c in range(DEGREE_SPAN + 1) if c != a]
-        nc.vector.tensor_sub(
-            out=den[:, a], in0=knots[:, :, a : a + BASES], in1=knots[:, :, others[0] : others[0] + BASES]
-        )
-        for c in others[1:]:
-            nc.vector.tensor_sub(out=diff[:], in0=knots[:, :, a : a + BASES], in1=knots[:, :, c : c + BASES])
-            nc.vector.tensor_mul(out=den[:, a], in0=den[:, a], in1=diff[:])
-    inv_den = consts.tile([P, DEGREE_SPAN + 1, I_TILES, BASES], F32)
+
+def chain_constants(nc, consts, knots):
+    ends = SPAN + 1
+    shape = [P, ends, I_TILES, BASES]
+    window = consts.tile(shape, F32)
+    for a in range(ends):
+        nc.vector.tensor_copy(out=window[:, a], in_=knots[:, :, a : a + BASES])
+
+    diff = consts.tile([P, SPAN] + shape[1:], F32)
+    for r in range(1, ends):
+        wrap = ends - r
+        nc.vector.tensor_sub(out=diff[:, r - 1, 0:wrap], in0=window[:, 0:wrap], in1=window[:, r:ends])
+        nc.vector.tensor_sub(out=diff[:, r - 1, wrap:ends], in0=window[:, wrap:ends], in1=window[:, 0:r])
+    den = consts.tile(shape, F32)
+    nc.vector.tensor_mul(out=den[:], in0=diff[:, 0], in1=diff[:, 1])
+    nc.vector.tensor_mul(out=diff[:, 2], in0=diff[:, 2], in1=diff[:, 3])
+    nc.vector.tensor_mul(out=den[:], in0=den[:], in1=diff[:, 2])
+    inv_den = consts.tile(shape, F32)
     nc.vector.reciprocal(out=inv_den[:], in_=den[:])
 
-    span = consts.tile([P, I_TILES, BASES], F32)
-    nc.vector.tensor_sub(out=span[:], in0=knots[:, :, DEGREE_SPAN:KNOTS], in1=knots[:, :, 0:BASES])
     lead = consts.tile([P, I_TILES, BASES], F32)
-    nc.vector.scalar_tensor_tensor(
-        out=lead[:, :, left], in0=span[:, :, left], scalar=3.0, in1=inv_den[:, 0, :, left], op0=ALU.mult, op1=ALU.mult
-    )
-    nc.vector.scalar_tensor_tensor(
-        out=lead[:, :, right],
-        in0=span[:, :, right],
-        scalar=-3.0,
-        in1=inv_den[:, DEGREE_SPAN, :, right],
-        op0=ALU.mult,
-        op1=ALU.mult,
-    )
-
-    ratio = consts.tile([P, DEGREE_SPAN, I_TILES, BASES], F32)
-    for s in range(1, DEGREE_SPAN):
-        nc.vector.tensor_mul(out=ratio[:, s, :, left], in0=den[:, 0, :, left], in1=inv_den[:, s, :, left])
-        nc.vector.tensor_mul(
-            out=ratio[:, s, :, right],
-            in0=den[:, DEGREE_SPAN, :, right],
-            in1=inv_den[:, DEGREE_SPAN - s, :, right],
+    ratio = consts.tile(shape, F32)
+    inner = slice(1, SPAN)
+    for side, own, sign in ((LEFT, 0, 1.0), (RIGHT, SPAN, -1.0)):
+        nc.vector.scalar_tensor_tensor(
+            out=lead[:, :, side],
+            in0=diff[:, SPAN - 1, 0, :, side],
+            scalar=-3.0 * sign,
+            in1=inv_den[:, own, :, side],
+            op0=ALU.mult,
+            op1=ALU.mult,
         )
-    return relu_bias, lead, ratio
+        nc.vector.tensor_mul(
+            out=ratio[:, inner, :, side],
+            in0=den[:, own : own + 1, :, side].to_broadcast([P, SPAN - 1, I_TILES, FIRST_LEFT]),
+            in1=inv_den[:, inner, :, side],
+        )
+    return lead, ratio
 
 
 def load_k_first(nc, tile, rows):
@@ -114,11 +117,14 @@ def tile_bsplinekanlayer_t_kernel(
         consts = ctx.enter_context(tc.tile_pool(name="consts", bufs=1))
         keep = ctx.enter_context(tc.tile_pool(name="keep", bufs=1))
         weights = ctx.enter_context(tc.tile_pool(name="weights", bufs=2))
-        feats = ctx.enter_context(tc.tile_pool(name="feats", bufs=2))
+        ramps = ctx.enter_context(tc.tile_pool(name="ramps", bufs=2))
+        squares = ctx.enter_context(tc.tile_pool(name="squares", bufs=4))
+        silu = ctx.enter_context(tc.tile_pool(name="silu", bufs=2))
+        scratch = ctx.enter_context(tc.tile_pool(name="scratch", bufs=1))
         banks = ctx.enter_context(tc.psum_pool(name="banks", bufs=6))
         sums = ctx.enter_context(tc.psum_pool(name="sums", bufs=2))
 
-        relu_bias, lead, ratio = spline_constants(nc, consts, grid)
+        knots, relu_bias = load_knots(nc, consts, grid)
         ident_f32 = consts.tile([P, P], F32)
         make_identity(nc, ident_f32[:])
         ident_bf = consts.tile([P, P], BF16)
@@ -204,26 +210,21 @@ def tile_bsplinekanlayer_t_kernel(
                     in_=g_grouped[:].rearrange("p b t -> p (b t)"),
                 )
 
-            first = range(X_COLS // N)
-            later = range(X_COLS // N, B_CHUNKS)
-            for bc in first:
-                load_rows(x_raw, x, bc)
+            load_rows(x_raw, x, 0)
             load_k_first(nc, scaler_raw, spline_scaler)
             spline_raw.append(load_spline_tile(nc, weights, spline_flat, 0))
-            for bc in first:
-                load_rows(g_raw, grad_out, bc)
+            load_rows(g_raw, grad_out, 0)
             load_k_first(nc, base_raw, base_weight)
-            for bc in later:
+            for bc in range(1, B_CHUNKS):
                 load_rows(x_raw, x, bc)
                 load_rows(g_raw, grad_out, bc)
             spline_raw.append(load_spline_tile(nc, weights, spline_flat, 1))
 
-            for bc in first:
-                transpose_x(bc)
+            transpose_x(0)
+            lead, ratio = chain_constants(nc, consts, knots)
             nc.vector.tensor_copy(out=scaler_sorted[:], in_=scaler_raw[:].rearrange("p t i -> p i t"))
             prepare_ssw(0, nc.vector.tensor_copy)
-            for bc in first:
-                quantise_g(bc)
+            quantise_g(0)
             base_grouped = raw.tile([P, FEATURES, PACK], BF16, align_bytes=64)
             nc.vector.tensor_copy(out=base_grouped[:], in_=base_raw[:].rearrange("p t i -> p i t"))
             nc.vector.quantize_mx(
@@ -231,14 +232,51 @@ def tile_bsplinekanlayer_t_kernel(
                 scales=base_scales[:],
                 in_=base_grouped[:].rearrange("p i t -> p (i t)"),
             )
-            for bc in later:
+            for bc in range(1, B_CHUNKS):
                 transpose_x(bc)
                 quantise_g(bc)
 
         prods = ctx.enter_context(tc.tile_pool(name="prods", bufs=2, reuse_waits="tile"))
-        scratch = ctx.enter_context(tc.tile_pool(name="scratch", bufs=1, reuse_waits="tile"))
 
-        def add_up_and_store(prod, b_cols, i_cols):
+        def truncated_squares(it, bc):
+            v = x_t[:, it, bc * N : (bc + 1) * N]
+            f = []
+            for j in range(BASES):
+                ramp = ramps.tile([P, N], F32)
+                nc.scalar.activation(
+                    out=ramp[:],
+                    in_=v,
+                    func=ACT.Relu,
+                    bias=relu_bias[:, it, j : j + 1],
+                    scale=float(toward_edge(j)),
+                )
+                f.append(squares.tile([P, N], F32, name="f%d" % j))
+                nc.scalar.activation(out=f[j][:], in_=ramp[:], func=ACT.Square)
+            return f
+
+        def chain_step(f, it, j, s):
+            a = s if j >= FIRST_LEFT else SPAN - s
+            nc.vector.scalar_tensor_tensor(
+                out=f[j][:],
+                in0=f[j + s * toward_edge(j)][:],
+                scalar=ratio[:, a, it, j : j + 1],
+                in1=f[j][:],
+                op0=ALU.mult,
+                op1=ALU.add,
+            )
+
+        def minus_dsilu(it):
+            v_all = x_t[:, it, :]
+            sig = scratch.tile([P, ROWS], F32)
+            nc.scalar.activation(out=sig[:], in_=v_all, func=ACT.Sigmoid)
+            neg_dsilu = silu.tile([P, ROWS], F32)
+            nc.scalar.activation(out=neg_dsilu[:], in_=v_all, func=ACT.Silu, scale=-1.0)
+            nc.vector.scalar_tensor_tensor(
+                out=neg_dsilu[:], in0=neg_dsilu[:], scalar=1.0, in1=sig[:], op0=ALU.subtract, op1=ALU.mult
+            )
+            return neg_dsilu
+
+        def add_up_and_store(prod, it, bc):
             total = sums.tile([P, B_SUB, P], F32)
             for t in range(B_SUB):
                 for j in range(TERMS):
@@ -252,97 +290,63 @@ def tile_bsplinekanlayer_t_kernel(
                     )
             result = prods.tile([P, B_SUB, P], F32)
             nc.scalar.copy(out=result[:], in_=total[:])
-            nc.sync.dma_start(out=out[b_cols, i_cols].rearrange("(t p) i -> p t i", p=P), in_=result[:])
+            nc.sync.dma_start(
+                out=out[bc * N : (bc + 1) * N, it * P : (it + 1) * P].rearrange("(t p) i -> p t i", p=P),
+                in_=result[:],
+            )
 
-        waiting = None
-        for it in range(I_TILES):
-            i_cols = slice(it * P, (it + 1) * P)
+        tiles = [(it, bc) for it in range(I_TILES) for bc in range(B_CHUNKS)]
+        steps = chain_steps()
+        f_next = truncated_squares(*tiles[0])
+        neg_dsilu_next = minus_dsilu(0)
+        for j, s in steps:
+            chain_step(f_next, 0, j, s)
+        before = None
 
-            for xc in range(ROWS // X_COLS):
-                if xc == ROWS // X_COLS - 1 and it + 1 < I_TILES:
-                    prepare_ssw(it + 1, nc.scalar.copy)
+        for n, (it, bc) in enumerate(tiles):
+            f = f_next
+            neg_dsilu = neg_dsilu_next
+            b_cols = slice(bc * N, (bc + 1) * N)
+            after = tiles[n + 1] if n + 1 < len(tiles) else None
+            if after:
+                f_next = truncated_squares(*after)
+                if after[0] != it:
+                    neg_dsilu_next = minus_dsilu(after[0])
+            if bc == B_CHUNKS - 2 and it + 1 < I_TILES:
+                prepare_ssw(it + 1, nc.scalar.copy)
 
-                v = x_t[:, it, xc * X_COLS : (xc + 1) * X_COLS]
+            prod = []
+            woven = 0
+            for j in range(TERMS):
+                bank = banks.tile([P, N], F32, tag="bank")
+                if j < BASES:
+                    w_codes = ssw_codes[:, it, j * P : (j + 1) * P]
+                    w_scales = ssw_scales[:, it, j * P : (j + 1) * P]
+                    factor = lead[:, it, j : j + 1]
+                    other = f[j][:]
+                else:
+                    w_codes = base_codes[:, it * P : (it + 1) * P]
+                    w_scales = base_scales[:, it * P : (it + 1) * P]
+                    factor = -1.0
+                    other = neg_dsilu[:, b_cols]
+                nc.tensor.matmul_mx(
+                    out=bank[:],
+                    lhsT=w_codes.bitcast(E4M3X4),
+                    lhsT_scale=w_scales,
+                    rhs=g_codes[:, b_cols].bitcast(E5M2X4),
+                    rhs_scale=g_scales[:, b_cols],
+                    start=True,
+                    stop=True,
+                )
+                prod.append(prods.tile([P, N], F32, name="prod%d" % j))
+                nc.vector.scalar_tensor_tensor(
+                    out=prod[j][:], in0=bank[:], scalar=factor, in1=other, op0=ALU.mult, op1=ALU.mult
+                )
+                while after and woven < (j + 1) * len(steps) // TERMS:
+                    chain_step(f_next, after[0], *steps[woven])
+                    woven += 1
 
-                f = []
-                for j in range(BASES):
-                    ramp = feats.tile([P, X_COLS], F32, tag="ramp")
-                    nc.scalar.activation(
-                        out=ramp[:],
-                        in_=v,
-                        func=ACT.Relu,
-                        bias=relu_bias[:, it, j : j + 1],
-                        scale=float(toward_edge(j)),
-                    )
-                    f.append(feats.tile([P, X_COLS], F32, name="f%d" % j))
-                    nc.scalar.activation(out=f[j][:], in_=ramp[:], func=ACT.Square)
-
-                if xc == 0:
-                    v_all = x_t[:, it, :]
-                    sig = scratch.tile([P, ROWS], F32)
-                    nc.scalar.activation(out=sig[:], in_=v_all, func=ACT.Sigmoid)
-                    neg_dsilu = feats.tile([P, ROWS], F32)
-                    nc.scalar.activation(out=neg_dsilu[:], in_=v_all, func=ACT.Silu, scale=-1.0)
-                    nc.vector.scalar_tensor_tensor(
-                        out=neg_dsilu[:], in0=neg_dsilu[:], scalar=1.0, in1=sig[:], op0=ALU.subtract, op1=ALU.mult
-                    )
-
-                for j_left in range(FIRST_LEFT, BASES - 1):
-                    j_right = BASES - 1 - j_left
-                    for s in range(1, extra_terms(j_left) + 1):
-                        for j in (j_left, j_right):
-                            nc.vector.scalar_tensor_tensor(
-                                out=f[j][:],
-                                in0=f[j + s * toward_edge(j)][:],
-                                scalar=ratio[:, s, it, j : j + 1],
-                                in1=f[j][:],
-                                op0=ALU.mult,
-                                op1=ALU.add,
-                            )
-
-                for c in range(X_COLS // N):
-                    here = slice(c * N, (c + 1) * N)
-                    b_cols = slice(xc * X_COLS + c * N, xc * X_COLS + (c + 1) * N)
-
-                    prod = []
-                    for j in range(TERMS):
-                        bank = banks.tile([P, N], F32, tag="bank")
-                        if j < BASES:
-                            w_codes = ssw_codes[:, it, j * P : (j + 1) * P]
-                            w_scales = ssw_scales[:, it, j * P : (j + 1) * P]
-                        else:
-                            w_codes = base_codes[:, i_cols]
-                            w_scales = base_scales[:, i_cols]
-                        nc.tensor.matmul_mx(
-                            out=bank[:],
-                            lhsT=w_codes.bitcast(E4M3X4),
-                            lhsT_scale=w_scales,
-                            rhs=g_codes[:, b_cols].bitcast(E5M2X4),
-                            rhs_scale=g_scales[:, b_cols],
-                            start=True,
-                            stop=True,
-                        )
-                        prod.append(prods.tile([P, N], F32, name="prod%d" % j))
-                        if j < BASES:
-                            nc.vector.scalar_tensor_tensor(
-                                out=prod[j][:],
-                                in0=bank[:],
-                                scalar=lead[:, it, j : j + 1],
-                                in1=f[j][:, here],
-                                op0=ALU.mult,
-                                op1=ALU.mult,
-                            )
-                        else:
-                            nc.vector.scalar_tensor_tensor(
-                                out=prod[j][:],
-                                in0=bank[:],
-                                scalar=-1.0,
-                                in1=neg_dsilu[:, b_cols],
-                                op0=ALU.mult,
-                                op1=ALU.mult,
-                            )
-
-                    if waiting:
-                        add_up_and_store(*waiting)
-                    waiting = (prod, b_cols, i_cols)
-        add_up_and_store(*waiting)
+            if before:
+                add_up_and_store(*before)
+            before = (prod, it, bc)
+        add_up_and_store(*before)

@@ -19,18 +19,19 @@ FEATURES = 512
 OUTPUTS = 512
 BASES = 8
 KNOTS = 12
-SPAN = 4
+SPAN = 3
+FIRST = 1
 FIRST_LEFT = 4
 N = 512
 I_TILES = FEATURES // P
 B_CHUNKS = ROWS // N
 B_SUB = N // P
-TERMS = BASES + 1
+TERMS = BASES - FIRST + 1
 
 FLOPS = 2 * ROWS * OUTPUTS * (FEATURES + FEATURES * BASES)
 
 LEFT = slice(FIRST_LEFT, BASES)
-RIGHT = slice(0, FIRST_LEFT)
+RIGHT = slice(FIRST, FIRST_LEFT)
 
 
 def toward_edge(j):
@@ -38,11 +39,13 @@ def toward_edge(j):
 
 
 def chain_steps():
+    left = [(m, s) for m in range(FIRST_LEFT, BASES - 1) for s in range(1, BASES - m)]
+    right = [(m, s) for m in range(FIRST_LEFT - 1, FIRST, -1) for s in range(1, m - FIRST + 1)]
     steps = []
-    for j_left in range(FIRST_LEFT, BASES - 1):
-        for s in range(1, BASES - j_left):
-            steps.append((j_left, s))
-            steps.append((BASES - 1 - j_left, s))
+    for n in range(len(left)):
+        steps.append(left[n])
+        if n < len(right):
+            steps.append(right[n])
     return steps
 
 
@@ -51,7 +54,7 @@ def load_knots(nc, consts, grid):
     nc.sync.dma_start(out=knots[:], in_=grid.rearrange("(t p) k -> p t k", p=P))
     relu_bias = consts.tile([P, I_TILES, BASES], F32)
     nc.vector.tensor_scalar_mul(out=relu_bias[:, :, LEFT], in0=knots[:, :, LEFT], scalar1=-1.0)
-    nc.vector.tensor_copy(out=relu_bias[:, :, RIGHT], in_=knots[:, :, LEFT])
+    nc.vector.tensor_copy(out=relu_bias[:, :, RIGHT], in_=knots[:, :, FIRST + SPAN : FIRST_LEFT + SPAN])
     return knots, relu_bias
 
 
@@ -69,27 +72,18 @@ def chain_constants(nc, consts, knots):
         nc.vector.tensor_sub(out=diff[:, r - 1, wrap:ends], in0=window[:, wrap:ends], in1=window[:, 0:r])
     den = consts.tile(shape, F32)
     nc.vector.tensor_mul(out=den[:], in0=diff[:, 0], in1=diff[:, 1])
-    nc.vector.tensor_mul(out=diff[:, 2], in0=diff[:, 2], in1=diff[:, 3])
     nc.vector.tensor_mul(out=den[:], in0=den[:], in1=diff[:, 2])
     inv_den = consts.tile(shape, F32)
     nc.vector.reciprocal(out=inv_den[:], in_=den[:])
 
     lead = consts.tile([P, I_TILES, BASES], F32)
     ratio = consts.tile(shape, F32)
-    inner = slice(1, SPAN)
-    for side, own, sign in ((LEFT, 0, 1.0), (RIGHT, SPAN, -1.0)):
-        nc.vector.scalar_tensor_tensor(
-            out=lead[:, :, side],
-            in0=diff[:, SPAN - 1, 0, :, side],
-            scalar=-3.0 * sign,
-            in1=inv_den[:, own, :, side],
-            op0=ALU.mult,
-            op1=ALU.mult,
-        )
+    for side, own, sign in ((LEFT, 0, -1.0), (RIGHT, SPAN, 1.0)):
+        nc.vector.tensor_scalar_mul(out=lead[:, :, side], in0=inv_den[:, own, :, side], scalar1=3.0 * sign)
         nc.vector.tensor_mul(
-            out=ratio[:, inner, :, side],
-            in0=den[:, own : own + 1, :, side].to_broadcast([P, SPAN - 1, I_TILES, FIRST_LEFT]),
-            in1=inv_den[:, inner, :, side],
+            out=ratio[:, :, :, side],
+            in0=den[:, own : own + 1, :, side].to_broadcast([P, ends, I_TILES, side.stop - side.start]),
+            in1=inv_den[:, :, :, side],
         )
     return lead, ratio
 
@@ -132,6 +126,8 @@ def tile_bsplinekanlayer_t_kernel(
 
         g_codes = keep.tile([P, ROWS], U32, align_bytes=64)
         g_scales = keep.tile([P, ROWS], U8, align_bytes=64)
+        g_neg_codes = keep.tile([P, ROWS], U32, align_bytes=64)
+        g_neg_scales = keep.tile([P, ROWS], U8, align_bytes=64)
         x_t = keep.tile([P, I_TILES, ROWS], BF16)
         base_codes = keep.tile([P, FEATURES], U32, align_bytes=64)
         base_scales = keep.tile([P, FEATURES], U8, align_bytes=64)
@@ -203,11 +199,20 @@ def tile_bsplinekanlayer_t_kernel(
                         out=g_words[:, 2 * pair * P : (2 * pair + 2) * P, :].rearrange("p (t b) u -> p t b u", t=2),
                         in_=g_t[:].rearrange("p t u b -> p t b u"),
                     )
+                g_neg_grouped = raw.tile([P, N * PACK], BF16, align_bytes=64)
+                nc.vector.tensor_scalar_mul(
+                    out=g_neg_grouped[:], in0=g_grouped[:].rearrange("p b t -> p (b t)"), scalar1=-1.0
+                )
                 cols = slice(bc * N, (bc + 1) * N)
                 nc.vector.quantize_mx(
                     out=g_codes[:, cols].bitcast(E5M2X4),
                     scales=g_scales[:, cols],
                     in_=g_grouped[:].rearrange("p b t -> p (b t)"),
+                )
+                nc.vector.quantize_mx(
+                    out=g_neg_codes[:, cols].bitcast(E5M2X4),
+                    scales=g_neg_scales[:, cols],
+                    in_=g_neg_grouped[:],
                 )
 
             load_rows(x_raw, x, 0)
@@ -240,8 +245,8 @@ def tile_bsplinekanlayer_t_kernel(
 
         def truncated_squares(it, bc):
             v = x_t[:, it, bc * N : (bc + 1) * N]
-            f = []
-            for j in range(BASES):
+            f = [None]
+            for j in range(FIRST, BASES):
                 ramp = ramps.tile([P, N], F32)
                 nc.scalar.activation(
                     out=ramp[:],
@@ -319,25 +324,30 @@ def tile_bsplinekanlayer_t_kernel(
             woven = 0
             for j in range(TERMS):
                 bank = banks.tile([P, N], F32, tag="bank")
-                if j < BASES:
-                    w_codes = ssw_codes[:, it, j * P : (j + 1) * P]
-                    w_scales = ssw_scales[:, it, j * P : (j + 1) * P]
-                    factor = lead[:, it, j : j + 1]
-                    other = f[j][:]
+                m = FIRST + j
+                if m < BASES:
+                    passes = [
+                        (ssw_codes[:, it, c * P : (c + 1) * P], ssw_scales[:, it, c * P : (c + 1) * P], gc, gsc)
+                        for c, gc, gsc in ((m, g_codes, g_scales), (m - 1, g_neg_codes, g_neg_scales))
+                    ]
+                    factor = lead[:, it, m : m + 1]
+                    other = f[m][:]
                 else:
-                    w_codes = base_codes[:, it * P : (it + 1) * P]
-                    w_scales = base_scales[:, it * P : (it + 1) * P]
+                    passes = [
+                        (base_codes[:, it * P : (it + 1) * P], base_scales[:, it * P : (it + 1) * P], g_codes, g_scales)
+                    ]
                     factor = -1.0
                     other = neg_dsilu[:, b_cols]
-                nc.tensor.matmul_mx(
-                    out=bank[:],
-                    lhsT=w_codes.bitcast(E4M3X4),
-                    lhsT_scale=w_scales,
-                    rhs=g_codes[:, b_cols].bitcast(E5M2X4),
-                    rhs_scale=g_scales[:, b_cols],
-                    start=True,
-                    stop=True,
-                )
+                for n_pass, (w_codes, w_scales, gc, gsc) in enumerate(passes):
+                    nc.tensor.matmul_mx(
+                        out=bank[:],
+                        lhsT=w_codes.bitcast(E4M3X4),
+                        lhsT_scale=w_scales,
+                        rhs=gc[:, b_cols].bitcast(E5M2X4),
+                        rhs_scale=gsc[:, b_cols],
+                        start=(n_pass == 0),
+                        stop=(n_pass == len(passes) - 1),
+                    )
                 prod.append(prods.tile([P, N], F32, name="prod%d" % j))
                 nc.vector.scalar_tensor_tensor(
                     out=prod[j][:], in0=bank[:], scalar=factor, in1=other, op0=ALU.mult, op1=ALU.mult

@@ -140,10 +140,11 @@ def tile_bsplinekanlayer_t_kernel(
 
         def prepare_ssw(it, sorting_copy):
             ssw_grouped = weights.tile([P, BASES, P * PACK], BF16, align_bytes=64)
-            sorting_copy(
-                out=ssw_grouped[:].rearrange("p j (i t) -> p j i t", t=PACK),
-                in_=spline_raw[it][:].rearrange("p t (i j) -> p j i t", j=BASES),
-            )
+            for j0 in range(0, BASES, 4):
+                sorting_copy(
+                    out=ssw_grouped[:, j0 : j0 + 4, :].rearrange("p j (i t) -> p i t j", t=PACK),
+                    in_=spline_raw[it][:].rearrange("p t (i j) -> p i t j", j=BASES)[:, :, :, j0 : j0 + 4],
+                )
             nc.vector.tensor_tensor(
                 out=ssw_grouped[:],
                 in0=ssw_grouped[:],

@@ -38,15 +38,8 @@ def toward_edge(j):
     return 1 if j >= FIRST_LEFT else -1
 
 
-def chain_steps():
-    left = [(m, s) for m in range(FIRST_LEFT, BASES - 1) for s in range(1, BASES - m)]
-    right = [(m, s) for m in range(FIRST_LEFT - 1, FIRST, -1) for s in range(1, m - FIRST + 1)]
-    steps = []
-    for n in range(len(left)):
-        steps.append(left[n])
-        if n < len(right):
-            steps.append(right[n])
-    return steps
+PLAIN_STEPS = ((4, 5), (5, 6), (6, 7), (3, 2))
+WEIGHTED_STEPS = ((4, 6), (5, 7), (3, 1), (4, 7), (2, 1))
 
 
 def load_knots(nc, consts, grid):
@@ -85,7 +78,41 @@ def chain_constants(nc, consts, knots):
             in0=den[:, own : own + 1, :, side].to_broadcast([P, ends, I_TILES, side.stop - side.start]),
             in1=inv_den[:, :, :, side],
         )
-    return lead, ratio
+    gain = consts.tile([P, I_TILES, BASES], F32)
+    nc.vector.memset(gain[:], 1.0)
+    for m, k in PLAIN_STEPS:
+        nc.vector.scalar_tensor_tensor(
+            out=gain[:, :, k : k + 1],
+            in0=ratio[:, knot_of(m, k), :, m : m + 1],
+            scalar=-1.0,
+            in1=gain[:, :, m : m + 1],
+            op0=ALU.mult,
+            op1=ALU.mult,
+        )
+    inv_gain = consts.tile([P, I_TILES, BASES], F32)
+    nc.vector.reciprocal(out=inv_gain[:], in_=gain[:])
+    root = consts.tile([P, I_TILES, BASES], F32)
+    nc.scalar.activation(out=root[:], in_=gain[:], func=ACT.Sqrt)
+    newton = consts.tile([P, I_TILES, BASES], F32)
+    nc.vector.reciprocal(out=newton[:], in_=root[:])
+    nc.vector.tensor_mul(out=newton[:], in0=newton[:], in1=gain[:])
+    nc.vector.tensor_add(out=newton[:], in0=newton[:], in1=root[:])
+    nc.vector.tensor_scalar_mul(out=root[:], in0=newton[:], scalar1=0.5)
+    nc.vector.tensor_mul(out=lead[:, :, FIRST:], in0=lead[:, :, FIRST:], in1=inv_gain[:, :, FIRST:])
+    weight = consts.tile([P, I_TILES, len(WEIGHTED_STEPS)], F32)
+    for n, (m, k) in enumerate(WEIGHTED_STEPS):
+        nc.vector.tensor_mul(
+            out=weight[:, :, n : n + 1], in0=ratio[:, knot_of(m, k), :, m : m + 1], in1=inv_gain[:, :, k : k + 1]
+        )
+        nc.vector.tensor_mul(out=weight[:, :, n : n + 1], in0=weight[:, :, n : n + 1], in1=gain[:, :, m : m + 1])
+    n46 = WEIGHTED_STEPS.index((4, 6))
+    n47 = WEIGHTED_STEPS.index((4, 7))
+    nc.vector.tensor_add(out=weight[:, :, n47 : n47 + 1], in0=weight[:, :, n47 : n47 + 1], in1=weight[:, :, n46 : n46 + 1])
+    return lead, root, weight
+
+
+def knot_of(m, k):
+    return k - m if m >= FIRST_LEFT else SPAN - (m - k)
 
 
 def load_k_first(nc, tile, rows):
@@ -227,7 +254,7 @@ def tile_bsplinekanlayer_t_kernel(
             spline_raw.append(load_spline_tile(nc, weights, spline_flat, 1))
 
             transpose_x(0)
-            lead, ratio = chain_constants(nc, consts, knots)
+            lead, root, weight = chain_constants(nc, consts, knots)
             nc.vector.tensor_copy(out=scaler_sorted[:], in_=scaler_raw[:].rearrange("p t i -> p i t"))
             prepare_ssw(0, nc.vector.tensor_copy)
             quantise_g(0)
@@ -257,16 +284,18 @@ def tile_bsplinekanlayer_t_kernel(
                     scale=float(toward_edge(j)),
                 )
                 f.append(squares.tile([P, N], F32, name="f%d" % j))
-                nc.scalar.activation(out=f[j][:], in_=ramp[:], func=ACT.Square)
+                nc.scalar.activation(out=f[j][:], in_=ramp[:], func=ACT.Square, scale=root[:, it, j : j + 1])
+            for m, k in PLAIN_STEPS:
+                nc.gpsimd.tensor_tensor(out=f[m][:], in0=f[m][:], in1=f[k][:], op=ALU.subtract)
             return f
 
-        def chain_step(f, it, j, s):
-            a = s if j >= FIRST_LEFT else SPAN - s
+        def chain_step(f, it, n_step):
+            m, k = WEIGHTED_STEPS[n_step]
             nc.vector.scalar_tensor_tensor(
-                out=f[j][:],
-                in0=f[j + s * toward_edge(j)][:],
-                scalar=ratio[:, a, it, j : j + 1],
-                in1=f[j][:],
+                out=f[m][:],
+                in0=f[k][:],
+                scalar=weight[:, it, n_step : n_step + 1],
+                in1=f[m][:],
                 op0=ALU.mult,
                 op1=ALU.add,
             )
@@ -302,11 +331,11 @@ def tile_bsplinekanlayer_t_kernel(
             )
 
         tiles = [(it, bc) for it in range(I_TILES) for bc in range(B_CHUNKS)]
-        steps = chain_steps()
+        steps = list(range(len(WEIGHTED_STEPS)))
         f_next = truncated_squares(*tiles[0])
         neg_dsilu_next = minus_dsilu(0)
-        for j, s in steps:
-            chain_step(f_next, 0, j, s)
+        for n_step in steps:
+            chain_step(f_next, 0, n_step)
         before = None
 
         for n, (it, bc) in enumerate(tiles):
@@ -354,7 +383,7 @@ def tile_bsplinekanlayer_t_kernel(
                     out=prod[j][:], in0=bank[:], scalar=factor, in1=other, op0=ALU.mult, op1=ALU.mult
                 )
                 while after and woven < (j + 1) * len(steps) // TERMS:
-                    chain_step(f_next, after[0], *steps[woven])
+                    chain_step(f_next, after[0], steps[woven])
                     woven += 1
 
             if before:

@@ -23,6 +23,7 @@ SPAN = 3
 FIRST = 1
 FIRST_LEFT = 4
 N = 512
+WIDE = 2 * N
 I_TILES = FEATURES // P
 B_CHUNKS = ROWS // N
 B_SUB = N // P
@@ -45,13 +46,13 @@ WEIGHTED_STEPS = ((4, 6), (5, 7), (3, 1), (4, 7), (2, 1))
 def load_knots(nc, consts, grid):
     knots = consts.tile([P, I_TILES, KNOTS], BF16)
     nc.sync.dma_start(out=knots[:], in_=grid.rearrange("(t p) k -> p t k", p=P))
-    relu_bias = consts.tile([P, I_TILES, BASES], F32)
-    nc.vector.tensor_scalar_mul(out=relu_bias[:, :, LEFT], in0=knots[:, :, LEFT], scalar1=-1.0)
-    nc.vector.tensor_copy(out=relu_bias[:, :, RIGHT], in_=knots[:, :, FIRST + SPAN : FIRST_LEFT + SPAN])
-    return knots, relu_bias
+    own_knot = consts.tile([P, I_TILES, BASES], F32)
+    nc.vector.tensor_copy(out=own_knot[:, :, LEFT], in_=knots[:, :, LEFT])
+    nc.vector.tensor_copy(out=own_knot[:, :, RIGHT], in_=knots[:, :, FIRST + SPAN : FIRST_LEFT + SPAN])
+    return knots, own_knot
 
 
-def chain_constants(nc, consts, knots):
+def chain_constants(nc, consts, knots, own_knot):
     ends = SPAN + 1
     shape = [P, ends, I_TILES, BASES]
     window = consts.tile(shape, F32)
@@ -98,6 +99,15 @@ def chain_constants(nc, consts, knots):
     nc.vector.tensor_mul(out=newton[:], in0=newton[:], in1=gain[:])
     nc.vector.tensor_add(out=newton[:], in0=newton[:], in1=root[:])
     nc.vector.tensor_scalar_mul(out=root[:], in0=newton[:], scalar1=0.5)
+    shift = consts.tile([P, I_TILES, BASES], F32)
+    nc.vector.scalar_tensor_tensor(
+        out=shift[:, :, FIRST:],
+        in0=root[:, :, FIRST:],
+        scalar=-1.0,
+        in1=own_knot[:, :, FIRST:],
+        op0=ALU.mult,
+        op1=ALU.mult,
+    )
     nc.vector.tensor_mul(out=lead[:, :, FIRST:], in0=lead[:, :, FIRST:], in1=inv_gain[:, :, FIRST:])
     weight = consts.tile([P, I_TILES, len(WEIGHTED_STEPS)], F32)
     for n, (m, k) in enumerate(WEIGHTED_STEPS):
@@ -108,7 +118,7 @@ def chain_constants(nc, consts, knots):
     n46 = WEIGHTED_STEPS.index((4, 6))
     n47 = WEIGHTED_STEPS.index((4, 7))
     nc.vector.tensor_add(out=weight[:, :, n47 : n47 + 1], in0=weight[:, :, n47 : n47 + 1], in1=weight[:, :, n46 : n46 + 1])
-    return lead, root, weight
+    return lead, root, shift, weight
 
 
 def knot_of(m, k):
@@ -138,14 +148,14 @@ def tile_bsplinekanlayer_t_kernel(
         consts = ctx.enter_context(tc.tile_pool(name="consts", bufs=1))
         keep = ctx.enter_context(tc.tile_pool(name="keep", bufs=1))
         weights = ctx.enter_context(tc.tile_pool(name="weights", bufs=2))
-        ramps = ctx.enter_context(tc.tile_pool(name="ramps", bufs=2))
+        clamps = ctx.enter_context(tc.tile_pool(name="clamps", bufs=2))
         squares = ctx.enter_context(tc.tile_pool(name="squares", bufs=4))
         silu = ctx.enter_context(tc.tile_pool(name="silu", bufs=2))
         scratch = ctx.enter_context(tc.tile_pool(name="scratch", bufs=1))
         banks = ctx.enter_context(tc.psum_pool(name="banks", bufs=6))
         sums = ctx.enter_context(tc.psum_pool(name="sums", bufs=2))
 
-        knots, relu_bias = load_knots(nc, consts, grid)
+        knots, own_knot = load_knots(nc, consts, grid)
         ident_f32 = consts.tile([P, P], F32)
         make_identity(nc, ident_f32[:])
         ident_bf = consts.tile([P, P], BF16)
@@ -158,15 +168,17 @@ def tile_bsplinekanlayer_t_kernel(
         x_t = keep.tile([P, I_TILES, ROWS], BF16)
         base_codes = keep.tile([P, FEATURES], U32, align_bytes=64)
         base_scales = keep.tile([P, FEATURES], U8, align_bytes=64)
-        ssw_codes = keep.tile([P, I_TILES, BASES * P], U32, align_bytes=64)
-        ssw_scales = keep.tile([P, I_TILES, BASES * P], U8, align_bytes=64)
+        ssw = {}
         scaler_sorted = keep.tile([P, FEATURES, PACK], BF16)
 
         spline_flat = spline_weight.rearrange("o i j -> o (i j)")
         spline_raw = []
 
         def prepare_ssw(it, sorting_copy):
-            ssw_grouped = weights.tile([P, BASES, P * PACK], BF16, align_bytes=64)
+            ssw_grouped = weights.tile([P, BASES, P * PACK], BF16, align_bytes=64, bufs=1)
+            ssw_codes = weights.tile([P, BASES * P], U32, align_bytes=64)
+            ssw_scales = weights.tile([P, BASES * P], U8, align_bytes=64)
+            ssw[it] = (ssw_codes, ssw_scales)
             for j0 in range(0, BASES, 4):
                 sorting_copy(
                     out=ssw_grouped[:, j0 : j0 + 4, :].rearrange("p j (i t) -> p i t j", t=PACK),
@@ -182,24 +194,67 @@ def tile_bsplinekanlayer_t_kernel(
                 op=ALU.mult,
             )
             nc.vector.quantize_mx(
-                out=ssw_codes[:, it, :].bitcast(E4M3X4),
-                scales=ssw_scales[:, it, :],
+                out=ssw_codes[:].bitcast(E4M3X4),
+                scales=ssw_scales[:],
                 in_=ssw_grouped[:].rearrange("p j w -> p (j w)"),
             )
             if it + 2 < I_TILES:
                 spline_raw.append(load_spline_tile(nc, weights, spline_flat, it + 2))
 
+        def clamped(it, half):
+            v = x_t[:, it, half * WIDE : (half + 1) * WIDE]
+            u = [None]
+            for m in range(FIRST, BASES):
+                u.append(clamps.tile([P, WIDE], BF16, name="u%d" % m))
+                if m >= FIRST_LEFT:
+                    nc.vector.tensor_scalar_max(out=u[m][:], in0=v, scalar1=own_knot[:, it, m : m + 1])
+                else:
+                    nc.vector.tensor_scalar_min(out=u[m][:], in0=v, scalar1=own_knot[:, it, m : m + 1])
+            return u
+
+        def truncated_squares(it, bc, u):
+            cols = slice((bc % 2) * N, (bc % 2 + 1) * N)
+            f = [None]
+            for m in range(FIRST, BASES):
+                f.append(squares.tile([P, N], F32, name="f%d" % m))
+                nc.scalar.activation(
+                    out=f[m][:],
+                    in_=u[m][:, cols],
+                    func=ACT.Square,
+                    bias=shift[:, it, m : m + 1],
+                    scale=root[:, it, m : m + 1],
+                )
+            for m, k in PLAIN_STEPS:
+                nc.gpsimd.tensor_tensor(out=f[m][:], in0=f[m][:], in1=f[k][:], op=ALU.subtract)
+            return f
+
+        tiles = [(it, bc) for it in range(I_TILES) for bc in range(B_CHUNKS)]
+        u_of = {}
+        f_of = {}
+
+        def stage_clamps(pair):
+            if 2 * pair < len(tiles):
+                u_of[pair] = clamped(tiles[2 * pair][0], tiles[2 * pair][1] // 2)
+
+        def stage_squares(n):
+            if n < len(tiles):
+                f_of[n] = truncated_squares(tiles[n][0], tiles[n][1], u_of[n // 2])
+
         with tc.tile_pool(name="raw", bufs=1) as raw:
-            g_raw = raw.tile([P, ROWS // P, OUTPUTS], BF16)
-            x_raw = raw.tile([P, ROWS // P, FEATURES], BF16)
+            g_raw = {}
+            x_raw = {}
             scaler_raw = raw.tile([P, PACK, FEATURES], BF16)
             base_raw = raw.tile([P, PACK, FEATURES], BF16)
 
-            def load_rows(tile, rows_in_dram, bc):
-                nc.sync.dma_start(
-                    out=tile[:, bc * B_SUB : (bc + 1) * B_SUB, :],
-                    in_=rows_in_dram[bc * N : (bc + 1) * N, :].rearrange("(t p) c -> p t c", p=P),
-                )
+            def load_rows(bc):
+                x_rows = raw.tile([P, B_SUB, FEATURES], BF16, bufs=2)
+                g_rows = raw.tile([P, B_SUB, OUTPUTS], BF16, bufs=2)
+                for tile, rows_in_dram in ((x_rows, x), (g_rows, grad_out)):
+                    nc.sync.dma_start(
+                        out=tile[:], in_=rows_in_dram[bc * N : (bc + 1) * N, :].rearrange("(t p) c -> p t c", p=P)
+                    )
+                x_raw[bc] = x_rows
+                g_raw[bc] = g_rows
 
             def transpose_x(bc):
                 for it in range(I_TILES):
@@ -207,10 +262,11 @@ def tile_bsplinekanlayer_t_kernel(
                     for t in range(B_SUB):
                         nc.tensor.transpose(
                             x_bank[:, t * P : (t + 1) * P],
-                            x_raw[:, bc * B_SUB + t, it * P : (it + 1) * P],
+                            x_raw[bc][:, t, it * P : (it + 1) * P],
                             ident_bf[:],
                         )
-                    nc.vector.tensor_copy(out=x_t[:, it, bc * N : (bc + 1) * N], in_=x_bank[:])
+                    copy_out = nc.vector.tensor_copy if bc < 2 else nc.scalar.copy
+                    copy_out(out=x_t[:, it, bc * N : (bc + 1) * N], in_=x_bank[:])
 
             def quantise_g(bc):
                 g_grouped = raw.tile([P, N, PACK], BF16, align_bytes=64)
@@ -220,17 +276,21 @@ def tile_bsplinekanlayer_t_kernel(
                 for pair in range(B_SUB // 2):
                     g_t = banks.tile([P, 2, 2, P], F32, tag="bank")
                     for t in range(2):
-                        words = g_raw[:, bc * B_SUB + 2 * pair + t, :].bitcast(F32)
+                        words = g_raw[bc][:, 2 * pair + t, :].bitcast(F32)
                         for u in range(2):
                             nc.tensor.transpose(g_t[:, t, u, :], words[:, u * P : (u + 1) * P], ident_f32[:])
-                    nc.vector.tensor_copy(
+                    copy_out = nc.vector.tensor_copy if bc < 1 else nc.scalar.copy
+                    copy_out(
                         out=g_words[:, 2 * pair * P : (2 * pair + 2) * P, :].rearrange("p (t b) u -> p t b u", t=2),
                         in_=g_t[:].rearrange("p t u b -> p t b u"),
                     )
                 g_neg_grouped = raw.tile([P, N * PACK], BF16, align_bytes=64)
-                nc.vector.tensor_scalar_mul(
-                    out=g_neg_grouped[:], in0=g_grouped[:].rearrange("p b t -> p (b t)"), scalar1=-1.0
-                )
+                if bc < 1:
+                    nc.vector.tensor_scalar_mul(
+                        out=g_neg_grouped[:], in0=g_grouped[:].rearrange("p b t -> p (b t)"), scalar1=-1.0
+                    )
+                else:
+                    nc.scalar.mul(out=g_neg_grouped[:], in_=g_grouped[:].rearrange("p b t -> p (b t)"), mul=-1.0)
                 cols = slice(bc * N, (bc + 1) * N)
                 nc.vector.quantize_mx(
                     out=g_codes[:, cols].bitcast(E5M2X4),
@@ -243,18 +303,19 @@ def tile_bsplinekanlayer_t_kernel(
                     in_=g_neg_grouped[:],
                 )
 
-            load_rows(x_raw, x, 0)
+            load_rows(0)
             load_k_first(nc, scaler_raw, spline_scaler)
             spline_raw.append(load_spline_tile(nc, weights, spline_flat, 0))
-            load_rows(g_raw, grad_out, 0)
             load_k_first(nc, base_raw, base_weight)
-            for bc in range(1, B_CHUNKS):
-                load_rows(x_raw, x, bc)
-                load_rows(g_raw, grad_out, bc)
+            load_rows(1)
             spline_raw.append(load_spline_tile(nc, weights, spline_flat, 1))
 
             transpose_x(0)
-            lead, root, weight = chain_constants(nc, consts, knots)
+            lead, root, shift, weight = chain_constants(nc, consts, knots, own_knot)
+            transpose_x(1)
+            stage_clamps(0)
+            stage_squares(0)
+            stage_squares(1)
             nc.vector.tensor_copy(out=scaler_sorted[:], in_=scaler_raw[:].rearrange("p t i -> p i t"))
             prepare_ssw(0, nc.vector.tensor_copy)
             quantise_g(0)
@@ -266,28 +327,14 @@ def tile_bsplinekanlayer_t_kernel(
                 in_=base_grouped[:].rearrange("p i t -> p (i t)"),
             )
             for bc in range(1, B_CHUNKS):
-                transpose_x(bc)
+                if bc + 1 < B_CHUNKS:
+                    load_rows(bc + 1)
+                if bc > 1:
+                    transpose_x(bc)
                 quantise_g(bc)
+            stage_clamps(1)
 
         prods = ctx.enter_context(tc.tile_pool(name="prods", bufs=2, reuse_waits="tile"))
-
-        def truncated_squares(it, bc):
-            v = x_t[:, it, bc * N : (bc + 1) * N]
-            f = [None]
-            for j in range(FIRST, BASES):
-                ramp = ramps.tile([P, N], F32)
-                nc.scalar.activation(
-                    out=ramp[:],
-                    in_=v,
-                    func=ACT.Relu,
-                    bias=relu_bias[:, it, j : j + 1],
-                    scale=float(toward_edge(j)),
-                )
-                f.append(squares.tile([P, N], F32, name="f%d" % j))
-                nc.scalar.activation(out=f[j][:], in_=ramp[:], func=ACT.Square, scale=root[:, it, j : j + 1])
-            for m, k in PLAIN_STEPS:
-                nc.gpsimd.tensor_tensor(out=f[m][:], in0=f[m][:], in1=f[k][:], op=ALU.subtract)
-            return f
 
         def chain_step(f, it, n_step):
             m, k = WEIGHTED_STEPS[n_step]
@@ -330,23 +377,22 @@ def tile_bsplinekanlayer_t_kernel(
                 in_=result[:],
             )
 
-        tiles = [(it, bc) for it in range(I_TILES) for bc in range(B_CHUNKS)]
         steps = list(range(len(WEIGHTED_STEPS)))
-        f_next = truncated_squares(*tiles[0])
         neg_dsilu_next = minus_dsilu(0)
         for n_step in steps:
-            chain_step(f_next, 0, n_step)
+            chain_step(f_of[0], 0, n_step)
         before = None
 
         for n, (it, bc) in enumerate(tiles):
-            f = f_next
+            f = f_of[n]
             neg_dsilu = neg_dsilu_next
             b_cols = slice(bc * N, (bc + 1) * N)
             after = tiles[n + 1] if n + 1 < len(tiles) else None
-            if after:
-                f_next = truncated_squares(*after)
-                if after[0] != it:
-                    neg_dsilu_next = minus_dsilu(after[0])
+            if n % 2 == 1:
+                stage_clamps((n + 3) // 2)
+            stage_squares(n + 2)
+            if after and after[0] != it:
+                neg_dsilu_next = minus_dsilu(after[0])
             if bc == B_CHUNKS - 2 and it + 1 < I_TILES:
                 prepare_ssw(it + 1, nc.scalar.copy)
 
@@ -357,7 +403,7 @@ def tile_bsplinekanlayer_t_kernel(
                 m = FIRST + j
                 if m < BASES:
                     passes = [
-                        (ssw_codes[:, it, c * P : (c + 1) * P], ssw_scales[:, it, c * P : (c + 1) * P], gc, gsc)
+                        (ssw[it][0][:, c * P : (c + 1) * P], ssw[it][1][:, c * P : (c + 1) * P], gc, gsc)
                         for c, gc, gsc in ((m, g_codes, g_scales), (m - 1, g_neg_codes, g_neg_scales))
                     ]
                     factor = lead[:, it, m : m + 1]
@@ -383,7 +429,7 @@ def tile_bsplinekanlayer_t_kernel(
                     out=prod[j][:], in0=bank[:], scalar=factor, in1=other, op0=ALU.mult, op1=ALU.mult
                 )
                 while after and woven < (j + 1) * len(steps) // TERMS:
-                    chain_step(f_next, after[0], steps[woven])
+                    chain_step(f_of[n + 1], after[0], steps[woven])
                     woven += 1
 
             if before:

@@ -23,11 +23,9 @@ SPAN = 3
 FIRST = 1
 FIRST_LEFT = 4
 N = 512
-WIDE = 2 * N
 I_TILES = FEATURES // P
 B_CHUNKS = ROWS // N
 B_SUB = N // P
-TERMS = BASES - FIRST + 1
 
 FLOPS = 2 * ROWS * OUTPUTS * (FEATURES + FEATURES * BASES)
 
@@ -39,8 +37,8 @@ def toward_edge(j):
     return 1 if j >= FIRST_LEFT else -1
 
 
-PLAIN_STEPS = ((4, 5), (5, 6), (6, 7), (3, 2))
-WEIGHTED_STEPS = ((4, 6), (5, 7), (3, 1), (4, 7), (2, 1))
+PLAIN_STEPS = ((4, 5), (5, 6), (6, 7), (3, 2), (2, 1))
+WEIGHTED_STEPS = ((3, 1), (4, 6), (4, 7), (5, 7))
 
 
 def load_knots(nc, consts, grid):
@@ -118,6 +116,8 @@ def chain_constants(nc, consts, knots, own_knot):
     n46 = WEIGHTED_STEPS.index((4, 6))
     n47 = WEIGHTED_STEPS.index((4, 7))
     nc.vector.tensor_add(out=weight[:, :, n47 : n47 + 1], in0=weight[:, :, n47 : n47 + 1], in1=weight[:, :, n46 : n46 + 1])
+    for n, (m, k) in enumerate(WEIGHTED_STEPS):
+        nc.vector.tensor_mul(out=weight[:, :, n : n + 1], in0=weight[:, :, n : n + 1], in1=lead[:, :, m : m + 1])
     return lead, root, shift, weight
 
 
@@ -148,8 +148,8 @@ def tile_bsplinekanlayer_t_kernel(
         consts = ctx.enter_context(tc.tile_pool(name="consts", bufs=1))
         keep = ctx.enter_context(tc.tile_pool(name="keep", bufs=1))
         weights = ctx.enter_context(tc.tile_pool(name="weights", bufs=2))
-        clamps = ctx.enter_context(tc.tile_pool(name="clamps", bufs=2))
-        squares = ctx.enter_context(tc.tile_pool(name="squares", bufs=4))
+        clamps = ctx.enter_context(tc.tile_pool(name="clamps", bufs=1))
+        squares = ctx.enter_context(tc.tile_pool(name="squares", bufs=3))
         silu = ctx.enter_context(tc.tile_pool(name="silu", bufs=2))
         scratch = ctx.enter_context(tc.tile_pool(name="scratch", bufs=1))
         banks = ctx.enter_context(tc.psum_pool(name="banks", bufs=6))
@@ -201,19 +201,18 @@ def tile_bsplinekanlayer_t_kernel(
             if it + 2 < I_TILES:
                 spline_raw.append(load_spline_tile(nc, weights, spline_flat, it + 2))
 
-        def clamped(it, half):
-            v = x_t[:, it, half * WIDE : (half + 1) * WIDE]
-            u = [None]
+        def clamp_tiles():
+            return [None] + [clamps.tile([P, ROWS], BF16, name="u%d" % m) for m in range(FIRST, BASES)]
+
+        def clamp(u, it, rows):
             for m in range(FIRST, BASES):
-                u.append(clamps.tile([P, WIDE], BF16, name="u%d" % m))
                 if m >= FIRST_LEFT:
-                    nc.vector.tensor_scalar_max(out=u[m][:], in0=v, scalar1=own_knot[:, it, m : m + 1])
+                    nc.vector.tensor_scalar_max(out=u[m][:, rows], in0=x_t[:, it, rows], scalar1=own_knot[:, it, m : m + 1])
                 else:
-                    nc.vector.tensor_scalar_min(out=u[m][:], in0=v, scalar1=own_knot[:, it, m : m + 1])
-            return u
+                    nc.vector.tensor_scalar_min(out=u[m][:, rows], in0=x_t[:, it, rows], scalar1=own_knot[:, it, m : m + 1])
 
         def truncated_squares(it, bc, u):
-            cols = slice((bc % 2) * N, (bc % 2 + 1) * N)
+            cols = slice(bc * N, (bc + 1) * N)
             f = [None]
             for m in range(FIRST, BASES):
                 f.append(squares.tile([P, N], F32, name="f%d" % m))
@@ -232,29 +231,21 @@ def tile_bsplinekanlayer_t_kernel(
         u_of = {}
         f_of = {}
 
-        def stage_clamps(pair):
-            if 2 * pair < len(tiles):
-                u_of[pair] = clamped(tiles[2 * pair][0], tiles[2 * pair][1] // 2)
-
         def stage_squares(n):
             if n < len(tiles):
-                f_of[n] = truncated_squares(tiles[n][0], tiles[n][1], u_of[n // 2])
+                f_of[n] = truncated_squares(tiles[n][0], tiles[n][1], u_of[tiles[n][0]])
 
         with tc.tile_pool(name="raw", bufs=1) as raw:
-            g_raw = {}
-            x_raw = {}
+            g_raw = raw.tile([P, ROWS // P, OUTPUTS], BF16)
+            x_raw = raw.tile([P, ROWS // P, FEATURES], BF16)
             scaler_raw = raw.tile([P, PACK, FEATURES], BF16)
             base_raw = raw.tile([P, PACK, FEATURES], BF16)
 
-            def load_rows(bc):
-                x_rows = raw.tile([P, B_SUB, FEATURES], BF16, bufs=2)
-                g_rows = raw.tile([P, B_SUB, OUTPUTS], BF16, bufs=2)
-                for tile, rows_in_dram in ((x_rows, x), (g_rows, grad_out)):
-                    nc.sync.dma_start(
-                        out=tile[:], in_=rows_in_dram[bc * N : (bc + 1) * N, :].rearrange("(t p) c -> p t c", p=P)
-                    )
-                x_raw[bc] = x_rows
-                g_raw[bc] = g_rows
+            def load_rows(tile, rows_in_dram, bc):
+                nc.sync.dma_start(
+                    out=tile[:, bc * B_SUB : (bc + 1) * B_SUB, :],
+                    in_=rows_in_dram[bc * N : (bc + 1) * N, :].rearrange("(t p) c -> p t c", p=P),
+                )
 
             def transpose_x(bc):
                 for it in range(I_TILES):
@@ -262,7 +253,7 @@ def tile_bsplinekanlayer_t_kernel(
                     for t in range(B_SUB):
                         nc.tensor.transpose(
                             x_bank[:, t * P : (t + 1) * P],
-                            x_raw[bc][:, t, it * P : (it + 1) * P],
+                            x_raw[:, bc * B_SUB + t, it * P : (it + 1) * P],
                             ident_bf[:],
                         )
                     copy_out = nc.vector.tensor_copy if bc < 2 else nc.scalar.copy
@@ -276,7 +267,7 @@ def tile_bsplinekanlayer_t_kernel(
                 for pair in range(B_SUB // 2):
                     g_t = banks.tile([P, 2, 2, P], F32, tag="bank")
                     for t in range(2):
-                        words = g_raw[bc][:, 2 * pair + t, :].bitcast(F32)
+                        words = g_raw[:, bc * B_SUB + 2 * pair + t, :].bitcast(F32)
                         for u in range(2):
                             nc.tensor.transpose(g_t[:, t, u, :], words[:, u * P : (u + 1) * P], ident_f32[:])
                     copy_out = nc.vector.tensor_copy if bc < 1 else nc.scalar.copy
@@ -303,17 +294,23 @@ def tile_bsplinekanlayer_t_kernel(
                     in_=g_neg_grouped[:],
                 )
 
-            load_rows(0)
+            load_rows(x_raw, x, 0)
+            load_rows(x_raw, x, 1)
             load_k_first(nc, scaler_raw, spline_scaler)
             spline_raw.append(load_spline_tile(nc, weights, spline_flat, 0))
+            load_rows(g_raw, grad_out, 0)
             load_k_first(nc, base_raw, base_weight)
-            load_rows(1)
+            load_rows(g_raw, grad_out, 1)
+            for bc in range(2, B_CHUNKS):
+                load_rows(x_raw, x, bc)
+                load_rows(g_raw, grad_out, bc)
             spline_raw.append(load_spline_tile(nc, weights, spline_flat, 1))
 
             transpose_x(0)
             lead, root, shift, weight = chain_constants(nc, consts, knots, own_knot)
             transpose_x(1)
-            stage_clamps(0)
+            u_of[0] = clamp_tiles()
+            clamp(u_of[0], 0, slice(0, 2 * N))
             stage_squares(0)
             stage_squares(1)
             nc.vector.tensor_copy(out=scaler_sorted[:], in_=scaler_raw[:].rearrange("p t i -> p i t"))
@@ -327,25 +324,12 @@ def tile_bsplinekanlayer_t_kernel(
                 in_=base_grouped[:].rearrange("p i t -> p (i t)"),
             )
             for bc in range(1, B_CHUNKS):
-                if bc + 1 < B_CHUNKS:
-                    load_rows(bc + 1)
                 if bc > 1:
                     transpose_x(bc)
                 quantise_g(bc)
-            stage_clamps(1)
+            clamp(u_of[0], 0, slice(2 * N, ROWS))
 
         prods = ctx.enter_context(tc.tile_pool(name="prods", bufs=2, reuse_waits="tile"))
-
-        def chain_step(f, it, n_step):
-            m, k = WEIGHTED_STEPS[n_step]
-            nc.vector.scalar_tensor_tensor(
-                out=f[m][:],
-                in0=f[k][:],
-                scalar=weight[:, it, n_step : n_step + 1],
-                in1=f[m][:],
-                op0=ALU.mult,
-                op1=ALU.add,
-            )
 
         def minus_dsilu(it):
             v_all = x_t[:, it, :]
@@ -361,14 +345,14 @@ def tile_bsplinekanlayer_t_kernel(
         def add_up_and_store(prod, it, bc):
             total = sums.tile([P, B_SUB, P], F32)
             for t in range(B_SUB):
-                for j in range(TERMS):
+                for j in range(len(prod)):
                     nc.tensor.matmul(
                         out=total[:, t, :],
                         lhsT=prod[j][:, t * P : (t + 1) * P],
                         rhs=ident_f32[:],
                         is_transpose=True,
                         start=(j == 0),
-                        stop=(j == TERMS - 1),
+                        stop=(j == len(prod) - 1),
                     )
             result = prods.tile([P, B_SUB, P], F32)
             nc.scalar.copy(out=result[:], in_=total[:])
@@ -377,10 +361,7 @@ def tile_bsplinekanlayer_t_kernel(
                 in_=result[:],
             )
 
-        steps = list(range(len(WEIGHTED_STEPS)))
         neg_dsilu_next = minus_dsilu(0)
-        for n_step in steps:
-            chain_step(f_of[0], 0, n_step)
         before = None
 
         for n, (it, bc) in enumerate(tiles):
@@ -388,8 +369,9 @@ def tile_bsplinekanlayer_t_kernel(
             neg_dsilu = neg_dsilu_next
             b_cols = slice(bc * N, (bc + 1) * N)
             after = tiles[n + 1] if n + 1 < len(tiles) else None
-            if n % 2 == 1:
-                stage_clamps((n + 3) // 2)
+            if bc == B_CHUNKS - 2 and it + 1 < I_TILES:
+                u_of[it + 1] = clamp_tiles()
+                clamp(u_of[it + 1], it + 1, slice(0, ROWS))
             stage_squares(n + 2)
             if after and after[0] != it:
                 neg_dsilu_next = minus_dsilu(after[0])
@@ -397,23 +379,23 @@ def tile_bsplinekanlayer_t_kernel(
                 prepare_ssw(it + 1, nc.scalar.copy)
 
             prod = []
-            woven = 0
-            for j in range(TERMS):
+            for m in range(FIRST, BASES + 1):
                 bank = banks.tile([P, N], F32, tag="bank")
-                m = FIRST + j
                 if m < BASES:
                     passes = [
                         (ssw[it][0][:, c * P : (c + 1) * P], ssw[it][1][:, c * P : (c + 1) * P], gc, gsc)
                         for c, gc, gsc in ((m, g_codes, g_scales), (m - 1, g_neg_codes, g_neg_scales))
                     ]
-                    factor = lead[:, it, m : m + 1]
-                    other = f[m][:]
+                    terms = [(lead[:, it, m : m + 1], f[m][:])] + [
+                        (weight[:, it, n_step : n_step + 1], f[k][:])
+                        for n_step, (m_step, k) in enumerate(WEIGHTED_STEPS)
+                        if m_step == m
+                    ]
                 else:
                     passes = [
                         (base_codes[:, it * P : (it + 1) * P], base_scales[:, it * P : (it + 1) * P], g_codes, g_scales)
                     ]
-                    factor = -1.0
-                    other = neg_dsilu[:, b_cols]
+                    terms = [(-1.0, neg_dsilu[:, b_cols])]
                 for n_pass, (w_codes, w_scales, gc, gsc) in enumerate(passes):
                     nc.tensor.matmul_mx(
                         out=bank[:],
@@ -424,13 +406,11 @@ def tile_bsplinekanlayer_t_kernel(
                         start=(n_pass == 0),
                         stop=(n_pass == len(passes) - 1),
                     )
-                prod.append(prods.tile([P, N], F32, name="prod%d" % j))
-                nc.vector.scalar_tensor_tensor(
-                    out=prod[j][:], in0=bank[:], scalar=factor, in1=other, op0=ALU.mult, op1=ALU.mult
-                )
-                while after and woven < (j + 1) * len(steps) // TERMS:
-                    chain_step(f_of[n + 1], after[0], steps[woven])
-                    woven += 1
+                for factor, other in terms:
+                    prod.append(prods.tile([P, N], F32, name="prod%d" % len(prod)))
+                    nc.vector.scalar_tensor_tensor(
+                        out=prod[-1][:], in0=bank[:], scalar=factor, in1=other, op0=ALU.mult, op1=ALU.mult
+                    )
 
             if before:
                 add_up_and_store(*before)

@@ -135,7 +135,7 @@ def load_k_first(nc, tile, rows):
 
 
 def load_spline_tile(nc, pool, spline_flat, it):
-    spline_raw = pool.tile([P, PACK, P * BASES], BF16)
+    spline_raw = pool.tile([P, PACK, P * BASES], BF16, bufs=1)
     load_k_first(nc, spline_raw, spline_flat[:, it * P * BASES : (it + 1) * P * BASES])
     return spline_raw
 
@@ -149,7 +149,7 @@ def tile_bsplinekanlayer_t_kernel(
         keep = ctx.enter_context(tc.tile_pool(name="keep", bufs=1))
         weights = ctx.enter_context(tc.tile_pool(name="weights", bufs=2))
         clamps = ctx.enter_context(tc.tile_pool(name="clamps", bufs=1))
-        squares = ctx.enter_context(tc.tile_pool(name="squares", bufs=3))
+        squares = ctx.enter_context(tc.tile_pool(name="squares", bufs=4))
         silu = ctx.enter_context(tc.tile_pool(name="silu", bufs=2))
         scratch = ctx.enter_context(tc.tile_pool(name="scratch", bufs=1))
         banks = ctx.enter_context(tc.psum_pool(name="banks", bufs=6))
@@ -198,8 +198,8 @@ def tile_bsplinekanlayer_t_kernel(
                 scales=ssw_scales[:],
                 in_=ssw_grouped[:].rearrange("p j w -> p (j w)"),
             )
-            if it + 2 < I_TILES:
-                spline_raw.append(load_spline_tile(nc, weights, spline_flat, it + 2))
+            if it + 1 < I_TILES:
+                spline_raw.append(load_spline_tile(nc, weights, spline_flat, it + 1))
 
         def clamp_tiles():
             return [None] + [clamps.tile([P, ROWS], BF16, name="u%d" % m) for m in range(FIRST, BASES)]
@@ -256,7 +256,7 @@ def tile_bsplinekanlayer_t_kernel(
                             x_raw[:, bc * B_SUB + t, it * P : (it + 1) * P],
                             ident_bf[:],
                         )
-                    copy_out = nc.vector.tensor_copy if bc < 2 else nc.scalar.copy
+                    copy_out = nc.scalar.copy if bc < 2 else nc.vector.tensor_copy
                     copy_out(out=x_t[:, it, bc * N : (bc + 1) * N], in_=x_bank[:])
 
             def quantise_g(bc):
@@ -270,13 +270,13 @@ def tile_bsplinekanlayer_t_kernel(
                         words = g_raw[:, bc * B_SUB + 2 * pair + t, :].bitcast(F32)
                         for u in range(2):
                             nc.tensor.transpose(g_t[:, t, u, :], words[:, u * P : (u + 1) * P], ident_f32[:])
-                    copy_out = nc.vector.tensor_copy if bc < 1 else nc.scalar.copy
+                    copy_out = nc.scalar.copy if bc < 1 else nc.vector.tensor_copy
                     copy_out(
                         out=g_words[:, 2 * pair * P : (2 * pair + 2) * P, :].rearrange("p (t b) u -> p t b u", t=2),
                         in_=g_t[:].rearrange("p t u b -> p t b u"),
                     )
                 g_neg_grouped = raw.tile([P, N * PACK], BF16, align_bytes=64)
-                if bc < 1:
+                if bc < B_CHUNKS:
                     nc.vector.tensor_scalar_mul(
                         out=g_neg_grouped[:], in0=g_grouped[:].rearrange("p b t -> p (b t)"), scalar1=-1.0
                     )
@@ -304,7 +304,6 @@ def tile_bsplinekanlayer_t_kernel(
             for bc in range(2, B_CHUNKS):
                 load_rows(x_raw, x, bc)
                 load_rows(g_raw, grad_out, bc)
-            spline_raw.append(load_spline_tile(nc, weights, spline_flat, 1))
 
             transpose_x(0)
             lead, root, shift, weight = chain_constants(nc, consts, knots, own_knot)
@@ -328,6 +327,7 @@ def tile_bsplinekanlayer_t_kernel(
                     transpose_x(bc)
                 quantise_g(bc)
             clamp(u_of[0], 0, slice(2 * N, ROWS))
+            stage_squares(2)
 
         prods = ctx.enter_context(tc.tile_pool(name="prods", bufs=2, reuse_waits="tile"))
 
@@ -369,10 +369,10 @@ def tile_bsplinekanlayer_t_kernel(
             neg_dsilu = neg_dsilu_next
             b_cols = slice(bc * N, (bc + 1) * N)
             after = tiles[n + 1] if n + 1 < len(tiles) else None
-            if bc == B_CHUNKS - 2 and it + 1 < I_TILES:
+            if bc == B_CHUNKS - 3 and it + 1 < I_TILES:
                 u_of[it + 1] = clamp_tiles()
                 clamp(u_of[it + 1], it + 1, slice(0, ROWS))
-            stage_squares(n + 2)
+            stage_squares(n + 3)
             if after and after[0] != it:
                 neg_dsilu_next = minus_dsilu(after[0])
             if bc == B_CHUNKS - 2 and it + 1 < I_TILES:

@@ -26,6 +26,7 @@ N = 512
 I_TILES = FEATURES // P
 B_CHUNKS = ROWS // N
 B_SUB = N // P
+BANKS = 6
 
 FLOPS = 2 * ROWS * OUTPUTS * (FEATURES + FEATURES * BASES)
 
@@ -152,7 +153,7 @@ def tile_bsplinekanlayer_t_kernel(
         squares = ctx.enter_context(tc.tile_pool(name="squares", bufs=4))
         silu = ctx.enter_context(tc.tile_pool(name="silu", bufs=2))
         scratch = ctx.enter_context(tc.tile_pool(name="scratch", bufs=1))
-        banks = ctx.enter_context(tc.psum_pool(name="banks", bufs=6))
+        banks = ctx.enter_context(tc.psum_pool(name="banks", bufs=BANKS))
         sums = ctx.enter_context(tc.psum_pool(name="sums", bufs=2))
 
         knots, own_knot = load_knots(nc, consts, grid)
@@ -174,16 +175,25 @@ def tile_bsplinekanlayer_t_kernel(
         spline_flat = spline_weight.rearrange("o i j -> o (i j)")
         spline_raw = []
 
-        def prepare_ssw(it, sorting_copy):
+        ssw_sorted = {}
+
+        def sort_ssw(it, sorting_copy):
             ssw_grouped = weights.tile([P, BASES, P * PACK], BF16, align_bytes=64, bufs=1)
             ssw_codes = weights.tile([P, BASES * P], U32, align_bytes=64)
             ssw_scales = weights.tile([P, BASES * P], U8, align_bytes=64)
             ssw[it] = (ssw_codes, ssw_scales)
+            ssw_sorted[it] = ssw_grouped
             for j0 in range(0, BASES, 4):
                 sorting_copy(
                     out=ssw_grouped[:, j0 : j0 + 4, :].rearrange("p j (i t) -> p i t j", t=PACK),
                     in_=spline_raw[it][:].rearrange("p t (i j) -> p i t j", j=BASES)[:, :, :, j0 : j0 + 4],
                 )
+            if it + 1 < I_TILES:
+                spline_raw.append(load_spline_tile(nc, weights, spline_flat, it + 1))
+
+        def finish_ssw(it):
+            ssw_grouped = ssw_sorted[it]
+            ssw_codes, ssw_scales = ssw[it]
             nc.vector.tensor_tensor(
                 out=ssw_grouped[:],
                 in0=ssw_grouped[:],
@@ -198,8 +208,6 @@ def tile_bsplinekanlayer_t_kernel(
                 scales=ssw_scales[:],
                 in_=ssw_grouped[:].rearrange("p j w -> p (j w)"),
             )
-            if it + 1 < I_TILES:
-                spline_raw.append(load_spline_tile(nc, weights, spline_flat, it + 1))
 
         def clamp_tiles():
             return [None] + [clamps.tile([P, ROWS], BF16, name="u%d" % m) for m in range(FIRST, BASES)]
@@ -313,7 +321,8 @@ def tile_bsplinekanlayer_t_kernel(
             stage_squares(0)
             stage_squares(1)
             nc.vector.tensor_copy(out=scaler_sorted[:], in_=scaler_raw[:].rearrange("p t i -> p i t"))
-            prepare_ssw(0, nc.vector.tensor_copy)
+            sort_ssw(0, nc.vector.tensor_copy)
+            finish_ssw(0)
             quantise_g(0)
             base_grouped = raw.tile([P, FEATURES, PACK], BF16, align_bytes=64)
             nc.vector.tensor_copy(out=base_grouped[:], in_=base_raw[:].rearrange("p t i -> p i t"))
@@ -331,12 +340,18 @@ def tile_bsplinekanlayer_t_kernel(
 
         prods = ctx.enter_context(tc.tile_pool(name="prods", bufs=2, reuse_waits="tile"))
 
-        def minus_dsilu(it):
+        silu_parts = {}
+
+        def silu_factors(it):
             v_all = x_t[:, it, :]
             sig = scratch.tile([P, ROWS], F32)
             nc.scalar.activation(out=sig[:], in_=v_all, func=ACT.Sigmoid)
             neg_dsilu = silu.tile([P, ROWS], F32)
             nc.scalar.activation(out=neg_dsilu[:], in_=v_all, func=ACT.Silu, scale=-1.0)
+            silu_parts[it] = (neg_dsilu, sig)
+
+        def minus_dsilu(it):
+            neg_dsilu, sig = silu_parts[it]
             nc.vector.scalar_tensor_tensor(
                 out=neg_dsilu[:], in0=neg_dsilu[:], scalar=1.0, in1=sig[:], op0=ALU.subtract, op1=ALU.mult
             )
@@ -361,58 +376,77 @@ def tile_bsplinekanlayer_t_kernel(
                 in_=result[:],
             )
 
+        silu_factors(0)
         neg_dsilu_next = minus_dsilu(0)
         before = None
 
-        for n, (it, bc) in enumerate(tiles):
-            f = f_of[n]
-            neg_dsilu = neg_dsilu_next
-            b_cols = slice(bc * N, (bc + 1) * N)
-            after = tiles[n + 1] if n + 1 < len(tiles) else None
-            if bc == B_CHUNKS - 3 and it + 1 < I_TILES:
-                u_of[it + 1] = clamp_tiles()
-                clamp(u_of[it + 1], it + 1, slice(0, ROWS))
-            stage_squares(n + 3)
-            if after and after[0] != it:
-                neg_dsilu_next = minus_dsilu(after[0])
-            if bc == B_CHUNKS - 2 and it + 1 < I_TILES:
-                prepare_ssw(it + 1, nc.scalar.copy)
+        with tc.manual_schedule():
+            for n, (it, bc) in enumerate(tiles):
+                f = f_of[n]
+                neg_dsilu = neg_dsilu_next
+                b_cols = slice(bc * N, (bc + 1) * N)
+                after = tiles[n + 1] if n + 1 < len(tiles) else None
+                more = it + 1 < I_TILES
+                if more and bc == 1:
+                    u_of[it + 1] = clamp_tiles()
+                    clamp(u_of[it + 1], it + 1, slice(0, ROWS))
+                if more and bc == 2:
+                    finish_ssw(it + 1)
+                if more and bc == 3:
+                    neg_dsilu_next = minus_dsilu(it + 1)
+                stage_squares(n + 3)
+                if more and bc == 0:
+                    sort_ssw(it + 1, nc.scalar.copy)
+                if more and bc == 2:
+                    silu_factors(it + 1)
 
-            prod = []
-            for m in range(FIRST, BASES + 1):
-                bank = banks.tile([P, N], F32, tag="bank")
-                if m < BASES:
-                    passes = [
-                        (ssw[it][0][:, c * P : (c + 1) * P], ssw[it][1][:, c * P : (c + 1) * P], gc, gsc)
-                        for c, gc, gsc in ((m, g_codes, g_scales), (m - 1, g_neg_codes, g_neg_scales))
-                    ]
-                    terms = [(lead[:, it, m : m + 1], f[m][:])] + [
-                        (weight[:, it, n_step : n_step + 1], f[k][:])
-                        for n_step, (m_step, k) in enumerate(WEIGHTED_STEPS)
-                        if m_step == m
-                    ]
-                else:
-                    passes = [
-                        (base_codes[:, it * P : (it + 1) * P], base_scales[:, it * P : (it + 1) * P], g_codes, g_scales)
-                    ]
-                    terms = [(-1.0, neg_dsilu[:, b_cols])]
-                for n_pass, (w_codes, w_scales, gc, gsc) in enumerate(passes):
-                    nc.tensor.matmul_mx(
-                        out=bank[:],
-                        lhsT=w_codes.bitcast(E4M3X4),
-                        lhsT_scale=w_scales,
-                        rhs=gc[:, b_cols].bitcast(E5M2X4),
-                        rhs_scale=gsc[:, b_cols],
-                        start=(n_pass == 0),
-                        stop=(n_pass == len(passes) - 1),
-                    )
-                for factor, other in terms:
-                    prod.append(prods.tile([P, N], F32, name="prod%d" % len(prod)))
-                    nc.vector.scalar_tensor_tensor(
-                        out=prod[-1][:], in0=bank[:], scalar=factor, in1=other, op0=ALU.mult, op1=ALU.mult
-                    )
+                prod = []
+                bank_of = {}
 
-            if before:
-                add_up_and_store(*before)
-            before = (prod, it, bc)
-        add_up_and_store(*before)
+                def run_passes(m):
+                    bank_of[m] = banks.tile([P, N], F32, tag="bank", name="bank")
+                    if m < BASES:
+                        passes = [
+                            (ssw[it][0][:, c * P : (c + 1) * P], ssw[it][1][:, c * P : (c + 1) * P], gc, gsc)
+                            for c, gc, gsc in ((m, g_codes, g_scales), (m - 1, g_neg_codes, g_neg_scales))
+                        ]
+                    else:
+                        passes = [
+                            (base_codes[:, it * P : (it + 1) * P], base_scales[:, it * P : (it + 1) * P], g_codes, g_scales)
+                        ]
+                    for n_pass, (w_codes, w_scales, gc, gsc) in enumerate(passes):
+                        nc.tensor.matmul_mx(
+                            out=bank_of[m][:],
+                            lhsT=w_codes.bitcast(E4M3X4),
+                            lhsT_scale=w_scales,
+                            rhs=gc[:, b_cols].bitcast(E5M2X4),
+                            rhs_scale=gsc[:, b_cols],
+                            start=(n_pass == 0),
+                            stop=(n_pass == len(passes) - 1),
+                        )
+
+                def run_products(m):
+                    if m < BASES:
+                        terms = [(lead[:, it, m : m + 1], f[m][:])] + [
+                            (weight[:, it, n_step : n_step + 1], f[k][:])
+                            for n_step, (m_step, k) in enumerate(WEIGHTED_STEPS)
+                            if m_step == m
+                        ]
+                    else:
+                        terms = [(-1.0, neg_dsilu[:, b_cols])]
+                    for factor, other in terms:
+                        prod.append(prods.tile([P, N], F32, name="prod%d" % len(prod)))
+                        nc.vector.scalar_tensor_tensor(
+                            out=prod[-1][:], in0=bank_of[m][:], scalar=factor, in1=other, op0=ALU.mult, op1=ALU.mult
+                        )
+
+                for m in range(FIRST, FIRST + BANKS):
+                    run_passes(m)
+                if before:
+                    add_up_and_store(*before)
+                for m in range(FIRST, BASES + 1):
+                    run_products(m)
+                    if m + BANKS <= BASES:
+                        run_passes(m + BANKS)
+                before = (prod, it, bc)
+            add_up_and_store(*before)

@@ -39,6 +39,7 @@ def toward_edge(j):
 
 
 PLAIN_STEPS = ((4, 5), (5, 6), (6, 7), (3, 2), (2, 1))
+STEP_ORDER = (4, 5, 6, 7, 3, 2, 1)
 WEIGHTED_STEPS = ((3, 1), (4, 6), (4, 7), (5, 7))
 
 
@@ -78,6 +79,7 @@ def chain_constants(nc, consts, knots, own_knot):
             in0=den[:, own : own + 1, :, side].to_broadcast([P, ends, I_TILES, side.stop - side.start]),
             in1=inv_den[:, :, :, side],
         )
+    nc.vector.tensor_scalar_mul(out=lead[:, :, FIRST::2], in0=lead[:, :, FIRST::2], scalar1=-1.0)
     gain = consts.tile([P, I_TILES, BASES], F32)
     nc.vector.memset(gain[:], 1.0)
     for m, k in PLAIN_STEPS:
@@ -149,10 +151,9 @@ def tile_bsplinekanlayer_t_kernel(
         consts = ctx.enter_context(tc.tile_pool(name="consts", bufs=1))
         keep = ctx.enter_context(tc.tile_pool(name="keep", bufs=1))
         weights = ctx.enter_context(tc.tile_pool(name="weights", bufs=2))
-        clamps = ctx.enter_context(tc.tile_pool(name="clamps", bufs=1))
-        squares = ctx.enter_context(tc.tile_pool(name="squares", bufs=4))
+        clamps = ctx.enter_context(tc.tile_pool(name="clamps", bufs=2))
+        squares = ctx.enter_context(tc.tile_pool(name="squares", bufs=3))
         silu = ctx.enter_context(tc.tile_pool(name="silu", bufs=2))
-        scratch = ctx.enter_context(tc.tile_pool(name="scratch", bufs=1))
         banks = ctx.enter_context(tc.psum_pool(name="banks", bufs=BANKS))
         sums = ctx.enter_context(tc.psum_pool(name="sums", bufs=2))
 
@@ -164,84 +165,95 @@ def tile_bsplinekanlayer_t_kernel(
 
         g_codes = keep.tile([P, ROWS], U32, align_bytes=64)
         g_scales = keep.tile([P, ROWS], U8, align_bytes=64)
-        g_neg_codes = keep.tile([P, ROWS], U32, align_bytes=64)
-        g_neg_scales = keep.tile([P, ROWS], U8, align_bytes=64)
         x_t = keep.tile([P, I_TILES, ROWS], BF16)
         base_codes = keep.tile([P, FEATURES], U32, align_bytes=64)
         base_scales = keep.tile([P, FEATURES], U8, align_bytes=64)
         ssw = {}
-        scaler_sorted = keep.tile([P, FEATURES, PACK], BF16)
+        scaler_signed = keep.tile([P, 2, FEATURES, PACK], BF16)
 
         spline_flat = spline_weight.rearrange("o i j -> o (i j)")
         spline_raw = []
 
         ssw_sorted = {}
 
-        def sort_ssw(it, sorting_copy):
-            ssw_grouped = weights.tile([P, BASES, P * PACK], BF16, align_bytes=64, bufs=1)
+        HALF = BASES // 2
+
+        def sort_ssw(it, half, sorting_copy):
+            if half == 0:
+                ssw_sorted[it] = weights.tile([P, BASES, P * PACK], BF16, name="ssw_sorted", align_bytes=64, bufs=1)
+            js = slice(half * HALF, (half + 1) * HALF)
+            sorting_copy(
+                out=ssw_sorted[it][:, js, :].rearrange("p j (i t) -> p i t j", t=PACK),
+                in_=spline_raw[it][:].rearrange("p t (i j) -> p i t j", j=BASES)[:, :, :, js],
+            )
+            if half == 1 and it + 1 < I_TILES:
+                spline_raw.append(load_spline_tile(nc, weights, spline_flat, it + 1))
+
+        def scale_ssw(it, half):
+            js = slice(half * HALF, (half + 1) * HALF)
+            by_sign = ssw_sorted[it][:, js, :].rearrange("p (h s) w -> p h s w", s=2)
+            nc.vector.tensor_tensor(
+                out=by_sign,
+                in0=by_sign,
+                in1=scaler_signed[:, :, it * P : (it + 1) * P, :]
+                .rearrange("p s i t -> p s (i t)")
+                .unsqueeze(1)
+                .to_broadcast([P, HALF // 2, 2, P * PACK]),
+                op=ALU.mult,
+            )
+
+        def quantise_ssw(it):
             ssw_codes = weights.tile([P, BASES * P], U32, align_bytes=64)
             ssw_scales = weights.tile([P, BASES * P], U8, align_bytes=64)
             ssw[it] = (ssw_codes, ssw_scales)
-            ssw_sorted[it] = ssw_grouped
-            for j0 in range(0, BASES, 4):
-                sorting_copy(
-                    out=ssw_grouped[:, j0 : j0 + 4, :].rearrange("p j (i t) -> p i t j", t=PACK),
-                    in_=spline_raw[it][:].rearrange("p t (i j) -> p i t j", j=BASES)[:, :, :, j0 : j0 + 4],
-                )
-            if it + 1 < I_TILES:
-                spline_raw.append(load_spline_tile(nc, weights, spline_flat, it + 1))
-
-        def finish_ssw(it):
-            ssw_grouped = ssw_sorted[it]
-            ssw_codes, ssw_scales = ssw[it]
-            nc.vector.tensor_tensor(
-                out=ssw_grouped[:],
-                in0=ssw_grouped[:],
-                in1=scaler_sorted[:, it * P : (it + 1) * P, :]
-                .rearrange("p i t -> p (i t)")
-                .unsqueeze(1)
-                .to_broadcast([P, BASES, P * PACK]),
-                op=ALU.mult,
-            )
             nc.vector.quantize_mx(
                 out=ssw_codes[:].bitcast(E4M3X4),
                 scales=ssw_scales[:],
-                in_=ssw_grouped[:].rearrange("p j w -> p (j w)"),
+                in_=ssw_sorted[it][:].rearrange("p j w -> p (j w)"),
             )
 
-        def clamp_tiles():
-            return [None] + [clamps.tile([P, ROWS], BF16, name="u%d" % m) for m in range(FIRST, BASES)]
+        tiles = [(it, bc) for it in range(I_TILES) for bc in range(B_CHUNKS)]
+        f_of = {}
 
-        def clamp(u, it, rows):
-            for m in range(FIRST, BASES):
-                if m >= FIRST_LEFT:
-                    nc.vector.tensor_scalar_max(out=u[m][:, rows], in0=x_t[:, it, rows], scalar1=own_knot[:, it, m : m + 1])
-                else:
-                    nc.vector.tensor_scalar_min(out=u[m][:, rows], in0=x_t[:, it, rows], scalar1=own_knot[:, it, m : m + 1])
-
-        def truncated_squares(it, bc, u):
+        def make_squares(n):
+            it, bc = tiles[n]
             cols = slice(bc * N, (bc + 1) * N)
-            f = [None]
-            for m in range(FIRST, BASES):
-                f.append(squares.tile([P, N], F32, name="f%d" % m))
+            u = clamps.tile([P, BASES, N], BF16, name="u")
+            for m in STEP_ORDER:
+                cut = nc.vector.tensor_scalar_max if m >= FIRST_LEFT else nc.vector.tensor_scalar_min
+                cut(out=u[:, m, :], in0=x_t[:, it, cols], scalar1=own_knot[:, it, m : m + 1])
+            f = [None] * BASES
+            for m in STEP_ORDER:
+                f[m] = squares.tile([P, N], F32, name="f%d" % m)
                 nc.scalar.activation(
                     out=f[m][:],
-                    in_=u[m][:, cols],
+                    in_=u[:, m, :],
                     func=ACT.Square,
                     bias=shift[:, it, m : m + 1],
                     scale=root[:, it, m : m + 1],
                 )
             for m, k in PLAIN_STEPS:
                 nc.gpsimd.tensor_tensor(out=f[m][:], in0=f[m][:], in1=f[k][:], op=ALU.subtract)
-            return f
+            f_of[n] = f
 
-        tiles = [(it, bc) for it in range(I_TILES) for bc in range(B_CHUNKS)]
-        u_of = {}
-        f_of = {}
+        silu_of = {}
 
-        def stage_squares(n):
-            if n < len(tiles):
-                f_of[n] = truncated_squares(tiles[n][0], tiles[n][1], u_of[tiles[n][0]])
+        def sigmoid(it):
+            sig = silu.tile([P, ROWS], F32)
+            nc.scalar.activation(out=sig[:], in_=x_t[:, it, :], func=ACT.Sigmoid)
+            silu_of[it] = [sig]
+
+        def silu_minus(it):
+            neg_dsilu = silu.tile([P, ROWS], F32)
+            nc.scalar.activation(out=neg_dsilu[:], in_=x_t[:, it, :], func=ACT.Silu, scale=-1.0)
+            silu_of[it].append(neg_dsilu)
+
+        def minus_dsilu(it, bc):
+            sig, neg_dsilu = silu_of[it]
+            cols = slice(bc * N, (bc + 1) * N)
+            nc.vector.scalar_tensor_tensor(
+                out=neg_dsilu[:, cols], in0=neg_dsilu[:, cols], scalar=1.0, in1=sig[:, cols], op0=ALU.subtract, op1=ALU.mult
+            )
 
         with tc.tile_pool(name="raw", bufs=1) as raw:
             g_raw = raw.tile([P, ROWS // P, OUTPUTS], BF16)
@@ -283,23 +295,11 @@ def tile_bsplinekanlayer_t_kernel(
                         out=g_words[:, 2 * pair * P : (2 * pair + 2) * P, :].rearrange("p (t b) u -> p t b u", t=2),
                         in_=g_t[:].rearrange("p t u b -> p t b u"),
                     )
-                g_neg_grouped = raw.tile([P, N * PACK], BF16, align_bytes=64)
-                if bc < B_CHUNKS:
-                    nc.vector.tensor_scalar_mul(
-                        out=g_neg_grouped[:], in0=g_grouped[:].rearrange("p b t -> p (b t)"), scalar1=-1.0
-                    )
-                else:
-                    nc.scalar.mul(out=g_neg_grouped[:], in_=g_grouped[:].rearrange("p b t -> p (b t)"), mul=-1.0)
                 cols = slice(bc * N, (bc + 1) * N)
                 nc.vector.quantize_mx(
                     out=g_codes[:, cols].bitcast(E5M2X4),
                     scales=g_scales[:, cols],
                     in_=g_grouped[:].rearrange("p b t -> p (b t)"),
-                )
-                nc.vector.quantize_mx(
-                    out=g_neg_codes[:, cols].bitcast(E5M2X4),
-                    scales=g_neg_scales[:, cols],
-                    in_=g_neg_grouped[:],
                 )
 
             load_rows(x_raw, x, 0)
@@ -316,13 +316,15 @@ def tile_bsplinekanlayer_t_kernel(
             transpose_x(0)
             lead, root, shift, weight = chain_constants(nc, consts, knots, own_knot)
             transpose_x(1)
-            u_of[0] = clamp_tiles()
-            clamp(u_of[0], 0, slice(0, 2 * N))
-            stage_squares(0)
-            stage_squares(1)
-            nc.vector.tensor_copy(out=scaler_sorted[:], in_=scaler_raw[:].rearrange("p t i -> p i t"))
-            sort_ssw(0, nc.vector.tensor_copy)
-            finish_ssw(0)
+            make_squares(0)
+            make_squares(1)
+            nc.vector.tensor_copy(out=scaler_signed[:, 0], in_=scaler_raw[:].rearrange("p t i -> p i t"))
+            nc.vector.tensor_scalar_mul(out=scaler_signed[:, 1], in0=scaler_signed[:, 0], scalar1=-1.0)
+            for half in range(2):
+                sort_ssw(0, half, nc.vector.tensor_copy)
+            for half in range(2):
+                scale_ssw(0, half)
+            quantise_ssw(0)
             quantise_g(0)
             base_grouped = raw.tile([P, FEATURES, PACK], BF16, align_bytes=64)
             nc.vector.tensor_copy(out=base_grouped[:], in_=base_raw[:].rearrange("p t i -> p i t"))
@@ -335,27 +337,11 @@ def tile_bsplinekanlayer_t_kernel(
                 if bc > 1:
                     transpose_x(bc)
                 quantise_g(bc)
-            clamp(u_of[0], 0, slice(2 * N, ROWS))
-            stage_squares(2)
+            sigmoid(0)
+            silu_minus(0)
+            sort_ssw(1, 0, nc.scalar.copy)
 
         prods = ctx.enter_context(tc.tile_pool(name="prods", bufs=2, reuse_waits="tile"))
-
-        silu_parts = {}
-
-        def silu_factors(it):
-            v_all = x_t[:, it, :]
-            sig = scratch.tile([P, ROWS], F32)
-            nc.scalar.activation(out=sig[:], in_=v_all, func=ACT.Sigmoid)
-            neg_dsilu = silu.tile([P, ROWS], F32)
-            nc.scalar.activation(out=neg_dsilu[:], in_=v_all, func=ACT.Silu, scale=-1.0)
-            silu_parts[it] = (neg_dsilu, sig)
-
-        def minus_dsilu(it):
-            neg_dsilu, sig = silu_parts[it]
-            nc.vector.scalar_tensor_tensor(
-                out=neg_dsilu[:], in0=neg_dsilu[:], scalar=1.0, in1=sig[:], op0=ALU.subtract, op1=ALU.mult
-            )
-            return neg_dsilu
 
         def add_up_and_store(prod, it, bc):
             total = sums.tile([P, B_SUB, P], F32)
@@ -376,29 +362,12 @@ def tile_bsplinekanlayer_t_kernel(
                 in_=result[:],
             )
 
-        silu_factors(0)
-        neg_dsilu_next = minus_dsilu(0)
         before = None
 
         with tc.manual_schedule():
             for n, (it, bc) in enumerate(tiles):
                 f = f_of[n]
-                neg_dsilu = neg_dsilu_next
                 b_cols = slice(bc * N, (bc + 1) * N)
-                after = tiles[n + 1] if n + 1 < len(tiles) else None
-                more = it + 1 < I_TILES
-                if more and bc == 1:
-                    u_of[it + 1] = clamp_tiles()
-                    clamp(u_of[it + 1], it + 1, slice(0, ROWS))
-                if more and bc == 2:
-                    finish_ssw(it + 1)
-                if more and bc == 3:
-                    neg_dsilu_next = minus_dsilu(it + 1)
-                stage_squares(n + 3)
-                if more and bc == 0:
-                    sort_ssw(it + 1, nc.scalar.copy)
-                if more and bc == 2:
-                    silu_factors(it + 1)
 
                 prod = []
                 bank_of = {}
@@ -407,20 +376,17 @@ def tile_bsplinekanlayer_t_kernel(
                     bank_of[m] = banks.tile([P, N], F32, tag="bank", name="bank")
                     if m < BASES:
                         passes = [
-                            (ssw[it][0][:, c * P : (c + 1) * P], ssw[it][1][:, c * P : (c + 1) * P], gc, gsc)
-                            for c, gc, gsc in ((m, g_codes, g_scales), (m - 1, g_neg_codes, g_neg_scales))
+                            (ssw[it][0][:, c * P : (c + 1) * P], ssw[it][1][:, c * P : (c + 1) * P]) for c in (m, m - 1)
                         ]
                     else:
-                        passes = [
-                            (base_codes[:, it * P : (it + 1) * P], base_scales[:, it * P : (it + 1) * P], g_codes, g_scales)
-                        ]
-                    for n_pass, (w_codes, w_scales, gc, gsc) in enumerate(passes):
+                        passes = [(base_codes[:, it * P : (it + 1) * P], base_scales[:, it * P : (it + 1) * P])]
+                    for n_pass, (w_codes, w_scales) in enumerate(passes):
                         nc.tensor.matmul_mx(
                             out=bank_of[m][:],
                             lhsT=w_codes.bitcast(E4M3X4),
                             lhsT_scale=w_scales,
-                            rhs=gc[:, b_cols].bitcast(E5M2X4),
-                            rhs_scale=gsc[:, b_cols],
+                            rhs=g_codes[:, b_cols].bitcast(E5M2X4),
+                            rhs_scale=g_scales[:, b_cols],
                             start=(n_pass == 0),
                             stop=(n_pass == len(passes) - 1),
                         )
@@ -433,7 +399,7 @@ def tile_bsplinekanlayer_t_kernel(
                             if m_step == m
                         ]
                     else:
-                        terms = [(-1.0, neg_dsilu[:, b_cols])]
+                        terms = [(-1.0, silu_of[it][1][:, b_cols])]
                     for factor, other in terms:
                         prod.append(prods.tile([P, N], F32, name="prod%d" % len(prod)))
                         nc.vector.scalar_tensor_tensor(
@@ -442,6 +408,26 @@ def tile_bsplinekanlayer_t_kernel(
 
                 for m in range(FIRST, FIRST + BANKS):
                     run_passes(m)
+
+                more = it + 1 < I_TILES
+                if more and bc == 0:
+                    scale_ssw(it + 1, 0)
+                if more and bc == 2:
+                    scale_ssw(it + 1, 1)
+                if more and bc == 3:
+                    quantise_ssw(it + 1)
+                minus_dsilu(it, bc)
+                if n + 2 < len(tiles):
+                    make_squares(n + 2)
+                if more and bc == 0:
+                    sort_ssw(it + 1, 1, nc.scalar.copy)
+                if more and bc == 1:
+                    sigmoid(it + 1)
+                if more and bc == 2:
+                    silu_minus(it + 1)
+                if it + 2 < I_TILES and bc == 3:
+                    sort_ssw(it + 2, 0, nc.scalar.copy)
+
                 if before:
                     add_up_and_store(*before)
                 for m in range(FIRST, BASES + 1):

@@ -38,8 +38,8 @@ def toward_edge(j):
     return 1 if j >= FIRST_LEFT else -1
 
 
-PLAIN_STEPS = ((4, 5), (5, 6), (6, 7), (3, 2), (2, 1))
-STEP_ORDER = (4, 5, 6, 7, 3, 2, 1)
+PLAIN_STEPS = ((4, 5), (3, 2), (5, 6), (2, 1), (6, 7))
+STEP_ORDER = (4, 5, 3, 2, 6, 1, 7)
 WEIGHTED_STEPS = ((3, 1), (4, 6), (4, 7), (5, 7))
 
 
@@ -152,7 +152,7 @@ def tile_bsplinekanlayer_t_kernel(
         keep = ctx.enter_context(tc.tile_pool(name="keep", bufs=1))
         weights = ctx.enter_context(tc.tile_pool(name="weights", bufs=2))
         clamps = ctx.enter_context(tc.tile_pool(name="clamps", bufs=2))
-        squares = ctx.enter_context(tc.tile_pool(name="squares", bufs=3))
+        squares = ctx.enter_context(tc.tile_pool(name="squares", bufs=2))
         silu = ctx.enter_context(tc.tile_pool(name="silu", bufs=2))
         banks = ctx.enter_context(tc.psum_pool(name="banks", bufs=BANKS))
         sums = ctx.enter_context(tc.psum_pool(name="sums", bufs=2))
@@ -215,7 +215,7 @@ def tile_bsplinekanlayer_t_kernel(
         tiles = [(it, bc) for it in range(I_TILES) for bc in range(B_CHUNKS)]
         f_of = {}
 
-        def make_squares(n):
+        def make_squares(n, stepper):
             it, bc = tiles[n]
             cols = slice(bc * N, (bc + 1) * N)
             u = clamps.tile([P, BASES, N], BF16, name="u")
@@ -233,7 +233,7 @@ def tile_bsplinekanlayer_t_kernel(
                     scale=root[:, it, m : m + 1],
                 )
             for m, k in PLAIN_STEPS:
-                nc.gpsimd.tensor_tensor(out=f[m][:], in0=f[m][:], in1=f[k][:], op=ALU.subtract)
+                stepper.tensor_tensor(out=f[m][:], in0=f[m][:], in1=f[k][:], op=ALU.subtract)
             f_of[n] = f
 
         silu_of = {}
@@ -316,8 +316,7 @@ def tile_bsplinekanlayer_t_kernel(
             transpose_x(0)
             lead, root, shift, weight = chain_constants(nc, consts, knots, own_knot)
             transpose_x(1)
-            make_squares(0)
-            make_squares(1)
+            make_squares(0, nc.vector)
             nc.vector.tensor_copy(out=scaler_signed[:, 0], in_=scaler_raw[:].rearrange("p t i -> p i t"))
             nc.vector.tensor_scalar_mul(out=scaler_signed[:, 1], in0=scaler_signed[:, 0], scalar1=-1.0)
             for half in range(2):
@@ -417,8 +416,8 @@ def tile_bsplinekanlayer_t_kernel(
                 if more and bc == 3:
                     quantise_ssw(it + 1)
                 minus_dsilu(it, bc)
-                if n + 2 < len(tiles):
-                    make_squares(n + 2)
+                if n + 1 < len(tiles):
+                    make_squares(n + 1, nc.gpsimd)
                 if more and bc == 0:
                     sort_ssw(it + 1, 1, nc.scalar.copy)
                 if more and bc == 1:

@@ -1,4 +1,5 @@
 from contextlib import ExitStack
+from functools import partial
 
 import concourse.mybir as mybir
 from concourse.masks import make_identity
@@ -27,6 +28,7 @@ I_TILES = FEATURES // P
 B_CHUNKS = ROWS // N
 B_SUB = N // P
 BANKS = 6
+FREE_BANKS_AFTER = FIRST + BANKS - 2
 
 FLOPS = 2 * ROWS * OUTPUTS * (FEATURES + FEATURES * BASES)
 
@@ -46,82 +48,95 @@ WEIGHTED_STEPS = ((3, 1), (4, 6), (4, 7), (5, 7))
 def load_knots(nc, consts, grid):
     knots = consts.tile([P, I_TILES, KNOTS], BF16)
     nc.sync.dma_start(out=knots[:], in_=grid.rearrange("(t p) k -> p t k", p=P))
-    own_knot = consts.tile([P, I_TILES, BASES], F32)
-    nc.vector.tensor_copy(out=own_knot[:, :, LEFT], in_=knots[:, :, LEFT])
-    nc.vector.tensor_copy(out=own_knot[:, :, RIGHT], in_=knots[:, :, FIRST + SPAN : FIRST_LEFT + SPAN])
-    return knots, own_knot
+    return knots
 
 
-def chain_constants(nc, consts, knots, own_knot):
+def spline_constants(nc, consts, knots, own_knot):
     ends = SPAN + 1
-    shape = [P, ends, I_TILES, BASES]
+    shape = [P, ends, BASES, I_TILES]
+    calls = []
+
+    def then(builder, **operands):
+        calls.append(partial(builder, **operands))
+
     window = consts.tile(shape, F32)
     for a in range(ends):
-        nc.vector.tensor_copy(out=window[:, a], in_=knots[:, :, a : a + BASES])
+        then(nc.vector.tensor_copy, out=window[:, a], in_=knots[:, :, a : a + BASES].rearrange("p t k -> p k t"))
 
     diff = consts.tile([P, SPAN] + shape[1:], F32)
     for r in range(1, ends):
         wrap = ends - r
-        nc.vector.tensor_sub(out=diff[:, r - 1, 0:wrap], in0=window[:, 0:wrap], in1=window[:, r:ends])
-        nc.vector.tensor_sub(out=diff[:, r - 1, wrap:ends], in0=window[:, wrap:ends], in1=window[:, 0:r])
+        then(nc.vector.tensor_sub, out=diff[:, r - 1, 0:wrap], in0=window[:, 0:wrap], in1=window[:, r:ends])
+        then(nc.vector.tensor_sub, out=diff[:, r - 1, wrap:ends], in0=window[:, wrap:ends], in1=window[:, 0:r])
     den = consts.tile(shape, F32)
-    nc.vector.tensor_mul(out=den[:], in0=diff[:, 0], in1=diff[:, 1])
-    nc.vector.tensor_mul(out=den[:], in0=den[:], in1=diff[:, 2])
+    then(nc.vector.tensor_mul, out=den[:], in0=diff[:, 0], in1=diff[:, 1])
+    then(nc.vector.tensor_mul, out=den[:], in0=den[:], in1=diff[:, 2])
     inv_den = consts.tile(shape, F32)
-    nc.vector.reciprocal(out=inv_den[:], in_=den[:])
+    then(nc.vector.reciprocal, out=inv_den[:], in_=den[:])
 
-    lead = consts.tile([P, I_TILES, BASES], F32)
-    ratio = consts.tile(shape, F32)
-    for side, own, sign in ((LEFT, 0, -1.0), (RIGHT, SPAN, 1.0)):
-        nc.vector.tensor_scalar_mul(out=lead[:, :, side], in0=inv_den[:, own, :, side], scalar1=3.0 * sign)
-        nc.vector.tensor_mul(
-            out=ratio[:, :, :, side],
-            in0=den[:, own : own + 1, :, side].to_broadcast([P, ends, I_TILES, side.stop - side.start]),
-            in1=inv_den[:, :, :, side],
-        )
-    nc.vector.tensor_scalar_mul(out=lead[:, :, FIRST::2], in0=lead[:, :, FIRST::2], scalar1=-1.0)
-    gain = consts.tile([P, I_TILES, BASES], F32)
-    nc.vector.memset(gain[:], 1.0)
-    for m, k in PLAIN_STEPS:
-        nc.vector.scalar_tensor_tensor(
-            out=gain[:, :, k : k + 1],
-            in0=ratio[:, knot_of(m, k), :, m : m + 1],
+    gain = consts.tile([P, BASES, I_TILES], F32)
+    then(nc.vector.memset, ap=gain[:], constant=1.0)
+    neighbour = consts.tile([P, BASES, I_TILES], F32)
+    for side, own, next_to_own in ((LEFT, 0, 1), (RIGHT, SPAN, SPAN - 1)):
+        then(
+            nc.vector.scalar_tensor_tensor,
+            out=neighbour[:, side],
+            in0=den[:, own, side],
             scalar=-1.0,
-            in1=gain[:, :, m : m + 1],
+            in1=inv_den[:, next_to_own, side],
             op0=ALU.mult,
             op1=ALU.mult,
         )
-    inv_gain = consts.tile([P, I_TILES, BASES], F32)
-    nc.vector.reciprocal(out=inv_gain[:], in_=gain[:])
-    root = consts.tile([P, I_TILES, BASES], F32)
-    nc.scalar.activation(out=root[:], in_=gain[:], func=ACT.Sqrt)
-    newton = consts.tile([P, I_TILES, BASES], F32)
-    nc.vector.reciprocal(out=newton[:], in_=root[:])
-    nc.vector.tensor_mul(out=newton[:], in0=newton[:], in1=gain[:])
-    nc.vector.tensor_add(out=newton[:], in0=newton[:], in1=root[:])
-    nc.vector.tensor_scalar_mul(out=root[:], in0=newton[:], scalar1=0.5)
-    shift = consts.tile([P, I_TILES, BASES], F32)
-    nc.vector.scalar_tensor_tensor(
-        out=shift[:, :, FIRST:],
-        in0=root[:, :, FIRST:],
+    for m, k in PLAIN_STEPS:
+        then(nc.vector.tensor_mul, out=gain[:, k], in0=neighbour[:, m], in1=gain[:, m])
+
+    root = consts.tile([P, BASES, I_TILES], F32)
+    then(nc.scalar.activation, out=root[:], in_=gain[:], func=ACT.Sqrt)
+    inv_gain = consts.tile([P, BASES, I_TILES], F32)
+    then(nc.vector.reciprocal, out=inv_gain[:], in_=gain[:])
+
+    signs = {m: 3.0 if (m >= FIRST_LEFT) == (m % 2 == 1) else -3.0 for m in range(FIRST, BASES)}
+    lead = consts.tile([P, BASES, I_TILES], F32)
+    weight = consts.tile([P, len(WEIGHTED_STEPS), I_TILES], F32)
+    places = [(lead[:, m], m, m) for m in range(FIRST, BASES)]
+    places += [(weight[:, n], m, k) for n, (m, k) in enumerate(WEIGHTED_STEPS)]
+    for place, m, k in places:
+        then(
+            nc.vector.scalar_tensor_tensor,
+            out=place,
+            in0=inv_den[:, knot_of(m, k), m],
+            scalar=signs[m],
+            in1=inv_gain[:, k],
+            op0=ALU.mult,
+            op1=ALU.mult,
+        )
+    n46 = WEIGHTED_STEPS.index((4, 6))
+    n47 = WEIGHTED_STEPS.index((4, 7))
+
+    newton = consts.tile([P, BASES, I_TILES], F32)
+    then(nc.vector.reciprocal, out=newton[:], in_=root[:])
+    then(nc.vector.tensor_mul, out=newton[:], in0=newton[:], in1=gain[:])
+    then(nc.vector.tensor_add, out=newton[:], in0=newton[:], in1=root[:])
+    then(nc.vector.tensor_scalar_mul, out=root[:], in0=newton[:], scalar1=0.5)
+    shift = consts.tile([P, BASES, I_TILES], F32)
+    then(
+        nc.vector.scalar_tensor_tensor,
+        out=shift[:, FIRST:],
+        in0=root[:, FIRST:],
         scalar=-1.0,
-        in1=own_knot[:, :, FIRST:],
+        in1=own_knot[:, FIRST:],
         op0=ALU.mult,
         op1=ALU.mult,
     )
-    nc.vector.tensor_mul(out=lead[:, :, FIRST:], in0=lead[:, :, FIRST:], in1=inv_gain[:, :, FIRST:])
-    weight = consts.tile([P, I_TILES, len(WEIGHTED_STEPS)], F32)
-    for n, (m, k) in enumerate(WEIGHTED_STEPS):
-        nc.vector.tensor_mul(
-            out=weight[:, :, n : n + 1], in0=ratio[:, knot_of(m, k), :, m : m + 1], in1=inv_gain[:, :, k : k + 1]
-        )
-        nc.vector.tensor_mul(out=weight[:, :, n : n + 1], in0=weight[:, :, n : n + 1], in1=gain[:, :, m : m + 1])
-    n46 = WEIGHTED_STEPS.index((4, 6))
-    n47 = WEIGHTED_STEPS.index((4, 7))
-    nc.vector.tensor_add(out=weight[:, :, n47 : n47 + 1], in0=weight[:, :, n47 : n47 + 1], in1=weight[:, :, n46 : n46 + 1])
-    for n, (m, k) in enumerate(WEIGHTED_STEPS):
-        nc.vector.tensor_mul(out=weight[:, :, n : n + 1], in0=weight[:, :, n : n + 1], in1=lead[:, :, m : m + 1])
-    return lead, root, shift, weight
+    then(nc.vector.tensor_add, out=weight[:, n47], in0=weight[:, n47], in1=weight[:, n46])
+    return lead, weight, root, shift, calls
+
+
+def weave(chain, others):
+    for n in range(max(len(chain), len(others))):
+        for calls in (chain, others):
+            if n < len(calls):
+                calls[n]()
 
 
 def knot_of(m, k):
@@ -150,47 +165,52 @@ def tile_bsplinekanlayer_t_kernel(
     with ExitStack() as ctx:
         consts = ctx.enter_context(tc.tile_pool(name="consts", bufs=1))
         keep = ctx.enter_context(tc.tile_pool(name="keep", bufs=1))
+        raw = ctx.enter_context(tc.tile_pool(name="raw", bufs=1))
         weights = ctx.enter_context(tc.tile_pool(name="weights", bufs=2))
-        clamps = ctx.enter_context(tc.tile_pool(name="clamps", bufs=2))
+        clamps = ctx.enter_context(tc.tile_pool(name="clamps", bufs=1))
         squares = ctx.enter_context(tc.tile_pool(name="squares", bufs=2))
         silu = ctx.enter_context(tc.tile_pool(name="silu", bufs=2))
+        prods = ctx.enter_context(tc.tile_pool(name="prods", bufs=2))
         banks = ctx.enter_context(tc.psum_pool(name="banks", bufs=BANKS))
-        sums = ctx.enter_context(tc.psum_pool(name="sums", bufs=2))
+        sums = ctx.enter_context(tc.psum_pool(name="sums", bufs=1))
 
-        knots, own_knot = load_knots(nc, consts, grid)
         ident_f32 = consts.tile([P, P], F32)
         make_identity(nc, ident_f32[:])
         ident_bf = consts.tile([P, P], BF16)
         make_identity(nc, ident_bf[:])
 
+        x_raw = keep.tile([P, ROWS // P, FEATURES], BF16)
+        x_t = keep.tile([P, I_TILES, ROWS], BF16)
         g_codes = keep.tile([P, ROWS], U32, align_bytes=64)
         g_scales = keep.tile([P, ROWS], U8, align_bytes=64)
-        x_t = keep.tile([P, I_TILES, ROWS], BF16)
         base_codes = keep.tile([P, FEATURES], U32, align_bytes=64)
         base_scales = keep.tile([P, FEATURES], U8, align_bytes=64)
-        ssw = {}
         scaler_signed = keep.tile([P, 2, FEATURES, PACK], BF16)
+        own_knot = keep.tile([P, BASES, I_TILES], F32)
+
+        scaler_raw = raw.tile([P, PACK, FEATURES], BF16)
+        base_raw = raw.tile([P, PACK, FEATURES], BF16)
+        base_grouped = raw.tile([P, FEATURES, PACK], BF16, align_bytes=64)
 
         spline_flat = spline_weight.rearrange("o i j -> o (i j)")
         spline_raw = []
-
         ssw_sorted = {}
+        ssw = {}
+        half_bases = BASES // 2
 
-        HALF = BASES // 2
-
-        def sort_ssw(it, half, sorting_copy):
-            if half == 0:
-                ssw_sorted[it] = weights.tile([P, BASES, P * PACK], BF16, name="ssw_sorted", align_bytes=64, bufs=1)
-            js = slice(half * HALF, (half + 1) * HALF)
-            sorting_copy(
-                out=ssw_sorted[it][:, js, :].rearrange("p j (i t) -> p i t j", t=PACK),
-                in_=spline_raw[it][:].rearrange("p t (i j) -> p i t j", j=BASES)[:, :, :, js],
+        def load_rows(rows_in_dram, bc, tile):
+            nc.sync.dma_start(
+                out=tile, in_=rows_in_dram[bc * N : (bc + 1) * N, :].rearrange("(t p) c -> p t c", p=P)
             )
-            if half == 1 and it + 1 < I_TILES:
-                spline_raw.append(load_spline_tile(nc, weights, spline_flat, it + 1))
 
-        def scale_ssw(it, half):
-            js = slice(half * HALF, (half + 1) * HALF)
+        def sort_ssw(it, half, sorting_copy, features=slice(0, P)):
+            js = slice(half * half_bases, (half + 1) * half_bases)
+            sorting_copy(
+                out=ssw_sorted[it][:, js, :].rearrange("p j (i t) -> p i t j", t=PACK)[:, features],
+                in_=spline_raw[it][:].rearrange("p t (i j) -> p i t j", j=BASES)[:, features, :, js],
+            )
+
+        def scale_ssw(it, js):
             by_sign = ssw_sorted[it][:, js, :].rearrange("p (h s) w -> p h s w", s=2)
             nc.vector.tensor_tensor(
                 out=by_sign,
@@ -198,9 +218,12 @@ def tile_bsplinekanlayer_t_kernel(
                 in1=scaler_signed[:, :, it * P : (it + 1) * P, :]
                 .rearrange("p s i t -> p s (i t)")
                 .unsqueeze(1)
-                .to_broadcast([P, HALF // 2, 2, P * PACK]),
+                .to_broadcast([P, (js.stop - js.start) // 2, 2, P * PACK]),
                 op=ALU.mult,
             )
+
+        def new_sorted(it):
+            ssw_sorted[it] = weights.tile([P, BASES, P * PACK], BF16, name="ssw_sorted", align_bytes=64, bufs=1)
 
         def quantise_ssw(it):
             ssw_codes = weights.tile([P, BASES * P], U32, align_bytes=64)
@@ -212,138 +235,102 @@ def tile_bsplinekanlayer_t_kernel(
                 in_=ssw_sorted[it][:].rearrange("p j w -> p (j w)"),
             )
 
+        def transpose_x(it, bc, copy_out):
+            x_bank = banks.tile([P, N], BF16, tag="bank", name="x_bank")
+            for t in range(B_SUB):
+                nc.tensor.transpose(
+                    x_bank[:, t * P : (t + 1) * P],
+                    x_raw[:, bc * B_SUB + t, it * P : (it + 1) * P],
+                    ident_bf[:],
+                )
+            copy_out(out=x_t[:, it, bc * N : (bc + 1) * N], in_=x_bank[:])
+
+        g_grouped = {}
+
+        def transpose_g(bc, copy_out):
+            grouped = raw.tile([P, N, PACK], BF16, name="g_grouped", align_bytes=64, bufs=2)
+            g_grouped[bc] = grouped[:].rearrange("p b t -> p (b t)")
+            g_words = g_grouped[bc].bitcast(F32).rearrange("p (b u) -> p b u", u=2)
+            for pair in range(B_SUB // 2):
+                g_t = banks.tile([P, 2, 2, P], F32, tag="bank", name="g_t")
+                for t in range(2):
+                    words = g_raw[bc][:, 2 * pair + t, :].bitcast(F32)
+                    for u in range(2):
+                        nc.tensor.transpose(g_t[:, t, u, :], words[:, u * P : (u + 1) * P], ident_f32[:])
+                copy_out(
+                    out=g_words[:, 2 * pair * P : (2 * pair + 2) * P, :].rearrange("p (t b) u -> p t b u", t=2),
+                    in_=g_t[:].rearrange("p t u b -> p t b u"),
+                )
+
+        def quantise_g(bc):
+            cols = slice(bc * N, (bc + 1) * N)
+            nc.vector.quantize_mx(out=g_codes[:, cols].bitcast(E5M2X4), scales=g_scales[:, cols], in_=g_grouped[bc])
+
         tiles = [(it, bc) for it in range(I_TILES) for bc in range(B_CHUNKS)]
+        u_of = {}
         f_of = {}
 
-        def make_squares(n, stepper):
+        def clamp_calls(n):
             it, bc = tiles[n]
-            cols = slice(bc * N, (bc + 1) * N)
-            u = clamps.tile([P, BASES, N], BF16, name="u")
-            for m in STEP_ORDER:
+            u = clamps.tile([P, len(STEP_ORDER), N], BF16)
+            u_of[n] = u
+            v = x_t[:, it, bc * N : (bc + 1) * N]
+            calls = []
+            for place, m in enumerate(STEP_ORDER):
                 cut = nc.vector.tensor_scalar_max if m >= FIRST_LEFT else nc.vector.tensor_scalar_min
-                cut(out=u[:, m, :], in0=x_t[:, it, cols], scalar1=own_knot[:, it, m : m + 1])
-            f = [None] * BASES
-            for m in STEP_ORDER:
-                f[m] = squares.tile([P, N], F32, name="f%d" % m)
-                nc.scalar.activation(
-                    out=f[m][:],
-                    in_=u[:, m, :],
-                    func=ACT.Square,
-                    bias=shift[:, it, m : m + 1],
-                    scale=root[:, it, m : m + 1],
-                )
-            for m, k in PLAIN_STEPS:
-                stepper.tensor_tensor(out=f[m][:], in0=f[m][:], in1=f[k][:], op=ALU.subtract)
-            f_of[n] = f
+                calls.append(partial(cut, out=u[:, place, :], in0=v, scalar1=own_knot[:, m, it : it + 1]))
+            return calls
 
-        silu_of = {}
+        def square(n):
+            it = tiles[n][0]
+            f = squares.tile([P, len(STEP_ORDER), N], F32)
+            f_of[n] = {m: f[:, place, :] for place, m in enumerate(STEP_ORDER)}
+            for place, m in enumerate(STEP_ORDER):
+                nc.scalar.activation(
+                    out=f_of[n][m],
+                    in_=u_of[n][:, place, :],
+                    func=ACT.Square,
+                    bias=shift[:, m, it : it + 1],
+                    scale=root[:, m, it : it + 1],
+                )
+
+        def steps(n, engine):
+            f = f_of[n]
+            for m, k in PLAIN_STEPS:
+                engine.tensor_tensor(out=f[m], in0=f[m], in1=f[k], op=ALU.subtract)
+
+        sigmoid_of = {}
+        neg_silu_of = {}
 
         def sigmoid(it):
-            sig = silu.tile([P, ROWS], F32)
-            nc.scalar.activation(out=sig[:], in_=x_t[:, it, :], func=ACT.Sigmoid)
-            silu_of[it] = [sig]
+            sig = silu.tile([P, ROWS // P, P], F32, bufs=1)
+            nc.scalar.activation(out=sig[:], in_=x_raw[:, :, it * P : (it + 1) * P], func=ACT.Sigmoid)
+            sigmoid_of[it] = sig
 
         def silu_minus(it):
-            neg_dsilu = silu.tile([P, ROWS], F32)
-            nc.scalar.activation(out=neg_dsilu[:], in_=x_t[:, it, :], func=ACT.Silu, scale=-1.0)
-            silu_of[it].append(neg_dsilu)
+            neg_silu = silu.tile([P, ROWS], F32)
+            nc.scalar.activation(out=neg_silu[:], in_=x_t[:, it, :], func=ACT.Silu, scale=-1.0)
+            neg_silu_of[it] = neg_silu
 
-        def minus_dsilu(it, bc):
-            sig, neg_dsilu = silu_of[it]
-            cols = slice(bc * N, (bc + 1) * N)
+        def transpose_sigmoid(it, bc):
+            sig_t = sums.tile([P, B_SUB, P], F32)
+            for t in range(B_SUB):
+                nc.tensor.transpose(sig_t[:, t, :], sigmoid_of[it][:, bc * B_SUB + t, :], ident_f32[:])
+            return sig_t
+
+        def minus_dsilu(it, bc, sig_t):
+            part = neg_silu_of[it][:, bc * N : (bc + 1) * N]
             nc.vector.scalar_tensor_tensor(
-                out=neg_dsilu[:, cols], in0=neg_dsilu[:, cols], scalar=1.0, in1=sig[:, cols], op0=ALU.subtract, op1=ALU.mult
+                out=part,
+                in0=part,
+                scalar=1.0,
+                in1=sig_t[:].rearrange("p t b -> p (t b)"),
+                op0=ALU.subtract,
+                op1=ALU.mult,
             )
-
-        with tc.tile_pool(name="raw", bufs=1) as raw:
-            g_raw = raw.tile([P, ROWS // P, OUTPUTS], BF16)
-            x_raw = raw.tile([P, ROWS // P, FEATURES], BF16)
-            scaler_raw = raw.tile([P, PACK, FEATURES], BF16)
-            base_raw = raw.tile([P, PACK, FEATURES], BF16)
-
-            def load_rows(tile, rows_in_dram, bc):
-                nc.sync.dma_start(
-                    out=tile[:, bc * B_SUB : (bc + 1) * B_SUB, :],
-                    in_=rows_in_dram[bc * N : (bc + 1) * N, :].rearrange("(t p) c -> p t c", p=P),
-                )
-
-            def transpose_x(bc):
-                for it in range(I_TILES):
-                    x_bank = banks.tile([P, N], BF16, tag="bank")
-                    for t in range(B_SUB):
-                        nc.tensor.transpose(
-                            x_bank[:, t * P : (t + 1) * P],
-                            x_raw[:, bc * B_SUB + t, it * P : (it + 1) * P],
-                            ident_bf[:],
-                        )
-                    copy_out = nc.scalar.copy if bc < 2 else nc.vector.tensor_copy
-                    copy_out(out=x_t[:, it, bc * N : (bc + 1) * N], in_=x_bank[:])
-
-            def quantise_g(bc):
-                g_grouped = raw.tile([P, N, PACK], BF16, align_bytes=64)
-                g_words = (
-                    g_grouped[:].rearrange("p b t -> p (b t)").bitcast(F32).rearrange("p (b u) -> p b u", u=2)
-                )
-                for pair in range(B_SUB // 2):
-                    g_t = banks.tile([P, 2, 2, P], F32, tag="bank")
-                    for t in range(2):
-                        words = g_raw[:, bc * B_SUB + 2 * pair + t, :].bitcast(F32)
-                        for u in range(2):
-                            nc.tensor.transpose(g_t[:, t, u, :], words[:, u * P : (u + 1) * P], ident_f32[:])
-                    copy_out = nc.scalar.copy if bc < 1 else nc.vector.tensor_copy
-                    copy_out(
-                        out=g_words[:, 2 * pair * P : (2 * pair + 2) * P, :].rearrange("p (t b) u -> p t b u", t=2),
-                        in_=g_t[:].rearrange("p t u b -> p t b u"),
-                    )
-                cols = slice(bc * N, (bc + 1) * N)
-                nc.vector.quantize_mx(
-                    out=g_codes[:, cols].bitcast(E5M2X4),
-                    scales=g_scales[:, cols],
-                    in_=g_grouped[:].rearrange("p b t -> p (b t)"),
-                )
-
-            load_rows(x_raw, x, 0)
-            load_rows(x_raw, x, 1)
-            load_k_first(nc, scaler_raw, spline_scaler)
-            spline_raw.append(load_spline_tile(nc, weights, spline_flat, 0))
-            load_rows(g_raw, grad_out, 0)
-            load_k_first(nc, base_raw, base_weight)
-            load_rows(g_raw, grad_out, 1)
-            for bc in range(2, B_CHUNKS):
-                load_rows(x_raw, x, bc)
-                load_rows(g_raw, grad_out, bc)
-
-            transpose_x(0)
-            lead, root, shift, weight = chain_constants(nc, consts, knots, own_knot)
-            transpose_x(1)
-            make_squares(0, nc.vector)
-            nc.vector.tensor_copy(out=scaler_signed[:, 0], in_=scaler_raw[:].rearrange("p t i -> p i t"))
-            nc.vector.tensor_scalar_mul(out=scaler_signed[:, 1], in0=scaler_signed[:, 0], scalar1=-1.0)
-            for half in range(2):
-                sort_ssw(0, half, nc.vector.tensor_copy)
-            for half in range(2):
-                scale_ssw(0, half)
-            quantise_ssw(0)
-            quantise_g(0)
-            base_grouped = raw.tile([P, FEATURES, PACK], BF16, align_bytes=64)
-            nc.vector.tensor_copy(out=base_grouped[:], in_=base_raw[:].rearrange("p t i -> p i t"))
-            nc.vector.quantize_mx(
-                out=base_codes[:].bitcast(E4M3X4),
-                scales=base_scales[:],
-                in_=base_grouped[:].rearrange("p i t -> p (i t)"),
-            )
-            for bc in range(1, B_CHUNKS):
-                if bc > 1:
-                    transpose_x(bc)
-                quantise_g(bc)
-            sigmoid(0)
-            silu_minus(0)
-            sort_ssw(1, 0, nc.scalar.copy)
-
-        prods = ctx.enter_context(tc.tile_pool(name="prods", bufs=2, reuse_waits="tile"))
 
         def add_up_and_store(prod, it, bc):
-            total = sums.tile([P, B_SUB, P], F32)
+            total = sums.tile([P, B_SUB, P], F32, tag="total")
             for t in range(B_SUB):
                 for j in range(len(prod)):
                     nc.tensor.matmul(
@@ -361,9 +348,91 @@ def tile_bsplinekanlayer_t_kernel(
                 in_=result[:],
             )
 
-        before = None
+        added = []
+
+        def add_to_last(totals, prod, complete):
+            for j in range(len(added), len(prod)):
+                for t in range(B_SUB):
+                    nc.tensor.matmul(
+                        out=totals[t][:],
+                        lhsT=prod[j][:, t * P : (t + 1) * P],
+                        rhs=ident_f32[:],
+                        is_transpose=True,
+                        start=(j == 0),
+                        stop=(complete and j == len(prod) - 1),
+                    )
+                added.append(j)
+
+        def store_last(totals, it, bc):
+            for t in range(B_SUB):
+                piece = prods.tile([P, P], F32, name="piece%d" % t, bufs=1)
+                copy_out = nc.vector.tensor_copy if t % 2 == 0 else nc.scalar.copy
+                copy_out(out=piece[:], in_=totals[t][:])
+                nc.sync.dma_start(
+                    out=out[bc * N + t * P : bc * N + (t + 1) * P, it * P : (it + 1) * P], in_=piece[:]
+                )
 
         with tc.manual_schedule():
+            knots = load_knots(nc, consts, grid)
+            g_raw = [raw.tile([P, B_SUB, OUTPUTS], BF16, name="g_raw%d" % bc) for bc in range(B_CHUNKS)]
+            x_chunk = [x_raw[:, bc * B_SUB : (bc + 1) * B_SUB, :] for bc in range(B_CHUNKS)]
+            load_rows(x, 0, x_chunk[0])
+            load_k_first(nc, scaler_raw, spline_scaler)
+            spline_raw.append(load_spline_tile(nc, weights, spline_flat, 0))
+            load_rows(grad_out, 0, g_raw[0][:])
+            load_rows(x, 1, x_chunk[1])
+            load_k_first(nc, base_raw, base_weight)
+            load_rows(x, 2, x_chunk[2])
+            load_rows(x, 3, x_chunk[3])
+            for bc in range(1, B_CHUNKS):
+                load_rows(grad_out, bc, g_raw[bc][:])
+
+            nc.vector.tensor_copy(out=own_knot[:, LEFT], in_=knots[:, :, LEFT].rearrange("p t k -> p k t"))
+            nc.vector.tensor_copy(
+                out=own_knot[:, RIGHT],
+                in_=knots[:, :, FIRST + SPAN : FIRST_LEFT + SPAN].rearrange("p t k -> p k t"),
+            )
+            transpose_x(0, 0, nc.scalar.copy)
+            nc.scalar.copy(out=scaler_signed[:, 0], in_=scaler_raw[:].rearrange("p t i -> p i t"))
+            lead, weight, root, shift, chain = spline_constants(nc, consts, knots, own_knot)
+            new_sorted(0)
+            quarter = P // 4
+            others = clamp_calls(0)
+            others += [
+                partial(sort_ssw, 0, half, nc.vector.tensor_copy, slice(i0, i0 + quarter))
+                for half in range(2)
+                for i0 in range(0, P, quarter)
+            ]
+            others.append(partial(nc.vector.tensor_scalar_mul, out=scaler_signed[:, 1], in0=scaler_signed[:, 0], scalar1=-1.0))
+            others += [partial(scale_ssw, 0, slice(j0, j0 + 2)) for j0 in range(0, BASES, 2)]
+            head = len(chain) - len(others)
+            for call in chain[:head]:
+                call()
+            weave(chain[head:], others)
+            spline_raw.append(load_spline_tile(nc, weights, spline_flat, 1))
+            square(0)
+            steps(0, nc.vector)
+            quantise_ssw(0)
+            transpose_g(0, nc.scalar.copy)
+            quantise_g(0)
+            for bc in range(1, B_CHUNKS):
+                transpose_x(0, bc, nc.scalar.copy)
+            nc.vector.tensor_copy(out=base_grouped[:], in_=base_raw[:].rearrange("p t i -> p i t"))
+            nc.vector.quantize_mx(
+                out=base_codes[:].bitcast(E4M3X4),
+                scales=base_scales[:],
+                in_=base_grouped[:].rearrange("p i t -> p (i t)"),
+            )
+            sigmoid(0)
+            silu_minus(0)
+            for bc in range(1, B_CHUNKS):
+                transpose_g(bc, nc.vector.tensor_copy)
+                quantise_g(bc)
+            for it in range(1, I_TILES):
+                for bc in range(B_CHUNKS):
+                    transpose_x(it, bc, nc.vector.tensor_copy if it == 1 else nc.scalar.copy)
+
+            before = None
             for n, (it, bc) in enumerate(tiles):
                 f = f_of[n]
                 b_cols = slice(bc * N, (bc + 1) * N)
@@ -392,13 +461,13 @@ def tile_bsplinekanlayer_t_kernel(
 
                 def run_products(m):
                     if m < BASES:
-                        terms = [(lead[:, it, m : m + 1], f[m][:])] + [
-                            (weight[:, it, n_step : n_step + 1], f[k][:])
+                        terms = [(lead[:, m, it : it + 1], f[m])] + [
+                            (weight[:, n_step, it : it + 1], f[k])
                             for n_step, (m_step, k) in enumerate(WEIGHTED_STEPS)
                             if m_step == m
                         ]
                     else:
-                        terms = [(-1.0, silu_of[it][1][:, b_cols])]
+                        terms = [(-1.0, neg_silu_of[it][:, b_cols])]
                     for factor, other in terms:
                         prod.append(prods.tile([P, N], F32, name="prod%d" % len(prod)))
                         nc.vector.scalar_tensor_tensor(
@@ -409,29 +478,42 @@ def tile_bsplinekanlayer_t_kernel(
                     run_passes(m)
 
                 more = it + 1 < I_TILES
-                if more and bc == 0:
-                    scale_ssw(it + 1, 0)
                 if more and bc == 2:
-                    scale_ssw(it + 1, 1)
+                    scale_ssw(it + 1, slice(0, half_bases))
                 if more and bc == 3:
+                    scale_ssw(it + 1, slice(half_bases, BASES))
                     quantise_ssw(it + 1)
-                minus_dsilu(it, bc)
                 if n + 1 < len(tiles):
-                    make_squares(n + 1, nc.gpsimd)
-                if more and bc == 0:
-                    sort_ssw(it + 1, 1, nc.scalar.copy)
-                if more and bc == 1:
-                    sigmoid(it + 1)
-                if more and bc == 2:
-                    silu_minus(it + 1)
-                if it + 2 < I_TILES and bc == 3:
-                    sort_ssw(it + 2, 0, nc.scalar.copy)
+                    for call in clamp_calls(n + 1):
+                        call()
+                    square(n + 1)
+                    steps(n + 1, nc.gpsimd)
 
                 if before:
                     add_up_and_store(*before)
+                sig_t = transpose_sigmoid(it, bc)
+                if more and bc == 0:
+                    new_sorted(it + 1)
+                if more and bc < 2:
+                    sort_ssw(it + 1, bc, nc.scalar.copy)
+                if bc == 1 and it + 2 < I_TILES:
+                    spline_raw.append(load_spline_tile(nc, weights, spline_flat, it + 2))
+                if more and bc == 2:
+                    silu_minus(it + 1)
+                if more and bc == 3:
+                    sigmoid(it + 1)
+
+                last = n == len(tiles) - 1
                 for m in range(FIRST, BASES + 1):
+                    if m == BASES - 1:
+                        minus_dsilu(it, bc, sig_t)
                     run_products(m)
                     if m + BANKS <= BASES:
                         run_passes(m + BANKS)
+                    if last and m == FREE_BANKS_AFTER:
+                        totals = [sums.tile([P, P], F32, tag="total", name="total")]
+                        totals += [banks.tile([P, P], F32, tag="bank", name="bank") for t in range(1, B_SUB)]
+                    if last and m >= FREE_BANKS_AFTER:
+                        add_to_last(totals, prod, m == BASES)
                 before = (prod, it, bc)
-            add_up_and_store(*before)
+            store_last(totals, it, bc)

@@ -41,7 +41,8 @@ def toward_edge(j):
 
 
 PLAIN_STEPS = ((4, 5), (3, 2), (5, 6), (2, 1), (6, 7))
-STEP_ORDER = (4, 5, 3, 2, 6, 1, 7)
+STEP_ORDER = (4, 3, 5, 2, 6, 1, 7)
+STEP_GROUPS = (((4, 5), (3, 2)), ((5, 6), (2, 1)), ((6, 7),))
 WEIGHTED_STEPS = ((3, 1), (4, 6), (4, 7), (5, 7))
 
 
@@ -269,6 +270,7 @@ def tile_bsplinekanlayer_t_kernel(
         tiles = [(it, bc) for it in range(I_TILES) for bc in range(B_CHUNKS)]
         u_of = {}
         f_of = {}
+        f_tile_of = {}
 
         def clamp_calls(n):
             it, bc = tiles[n]
@@ -284,6 +286,7 @@ def tile_bsplinekanlayer_t_kernel(
         def square(n):
             it = tiles[n][0]
             f = squares.tile([P, len(STEP_ORDER), N], F32)
+            f_tile_of[n] = f
             f_of[n] = {m: f[:, place, :] for place, m in enumerate(STEP_ORDER)}
             for place, m in enumerate(STEP_ORDER):
                 nc.scalar.activation(
@@ -295,9 +298,12 @@ def tile_bsplinekanlayer_t_kernel(
                 )
 
         def steps(n, engine):
-            f = f_of[n]
-            for m, k in PLAIN_STEPS:
-                engine.tensor_tensor(out=f[m], in0=f[m], in1=f[k], op=ALU.subtract)
+            for group in STEP_GROUPS:
+                to, by = [
+                    f_tile_of[n][:, STEP_ORDER.index(group[0][end]) : STEP_ORDER.index(group[-1][end]) + 1, :]
+                    for end in range(2)
+                ]
+                engine.tensor_tensor(out=to, in0=to, in1=by, op=ALU.subtract)
 
         sigmoid_of = {}
         neg_silu_of = {}

@@ -166,12 +166,10 @@ def tile_bsplinekanlayer_t_kernel(
     with ExitStack() as ctx:
         consts = ctx.enter_context(tc.tile_pool(name="consts", bufs=1))
         keep = ctx.enter_context(tc.tile_pool(name="keep", bufs=1))
-        raw = ctx.enter_context(tc.tile_pool(name="raw", bufs=1))
         weights = ctx.enter_context(tc.tile_pool(name="weights", bufs=2))
-        clamps = ctx.enter_context(tc.tile_pool(name="clamps", bufs=1))
-        squares = ctx.enter_context(tc.tile_pool(name="squares", bufs=2))
+        clamps = ctx.enter_context(tc.tile_pool(name="clamps", bufs=2))
+        squares = ctx.enter_context(tc.tile_pool(name="squares", bufs=3))
         silu = ctx.enter_context(tc.tile_pool(name="silu", bufs=2))
-        prods = ctx.enter_context(tc.tile_pool(name="prods", bufs=2))
         banks = ctx.enter_context(tc.psum_pool(name="banks", bufs=BANKS))
         sums = ctx.enter_context(tc.psum_pool(name="sums", bufs=1))
 
@@ -188,10 +186,6 @@ def tile_bsplinekanlayer_t_kernel(
         base_scales = keep.tile([P, FEATURES], U8, align_bytes=64)
         scaler_signed = keep.tile([P, 2, FEATURES, PACK], BF16)
         own_knot = keep.tile([P, BASES, I_TILES], F32)
-
-        scaler_raw = raw.tile([P, PACK, FEATURES], BF16)
-        base_raw = raw.tile([P, PACK, FEATURES], BF16)
-        base_grouped = raw.tile([P, FEATURES, PACK], BF16, align_bytes=64)
 
         spline_flat = spline_weight.rearrange("o i j -> o (i j)")
         spline_raw = []
@@ -297,13 +291,19 @@ def tile_bsplinekanlayer_t_kernel(
                     scale=root[:, m, it : it + 1],
                 )
 
-        def steps(n, engine):
+        def step_calls(n, engine):
+            calls = []
             for group in STEP_GROUPS:
                 to, by = [
                     f_tile_of[n][:, STEP_ORDER.index(group[0][end]) : STEP_ORDER.index(group[-1][end]) + 1, :]
                     for end in range(2)
                 ]
-                engine.tensor_tensor(out=to, in0=to, in1=by, op=ALU.subtract)
+                calls.append(partial(engine.tensor_tensor, out=to, in0=to, in1=by, op=ALU.subtract))
+            return calls
+
+        def let_gpsimd_begin(n):
+            column = f_of[n][STEP_ORDER[0]][:, 0:1]
+            nc.vector.tensor_copy(out=column, in_=column)
 
         sigmoid_of = {}
         neg_silu_of = {}
@@ -379,64 +379,74 @@ def tile_bsplinekanlayer_t_kernel(
                 )
 
         with tc.manual_schedule():
-            knots = load_knots(nc, consts, grid)
-            g_raw = [raw.tile([P, B_SUB, OUTPUTS], BF16, name="g_raw%d" % bc) for bc in range(B_CHUNKS)]
-            x_chunk = [x_raw[:, bc * B_SUB : (bc + 1) * B_SUB, :] for bc in range(B_CHUNKS)]
-            load_rows(x, 0, x_chunk[0])
-            load_k_first(nc, scaler_raw, spline_scaler)
-            spline_raw.append(load_spline_tile(nc, weights, spline_flat, 0))
-            load_rows(grad_out, 0, g_raw[0][:])
-            load_rows(x, 1, x_chunk[1])
-            load_k_first(nc, base_raw, base_weight)
-            load_rows(x, 2, x_chunk[2])
-            load_rows(x, 3, x_chunk[3])
-            for bc in range(1, B_CHUNKS):
-                load_rows(grad_out, bc, g_raw[bc][:])
+            with tc.tile_pool(name="raw", bufs=1) as raw:
+                scaler_raw = raw.tile([P, PACK, FEATURES], BF16)
+                base_raw = raw.tile([P, PACK, FEATURES], BF16)
+                base_grouped = raw.tile([P, FEATURES, PACK], BF16, align_bytes=64)
+                knots = load_knots(nc, consts, grid)
+                g_raw = [raw.tile([P, B_SUB, OUTPUTS], BF16, name="g_raw%d" % bc) for bc in range(B_CHUNKS)]
+                x_chunk = [x_raw[:, bc * B_SUB : (bc + 1) * B_SUB, :] for bc in range(B_CHUNKS)]
+                load_rows(x, 0, x_chunk[0])
+                load_k_first(nc, scaler_raw, spline_scaler)
+                spline_raw.append(load_spline_tile(nc, weights, spline_flat, 0))
+                load_rows(grad_out, 0, g_raw[0][:])
+                load_rows(x, 1, x_chunk[1])
+                load_k_first(nc, base_raw, base_weight)
+                load_rows(x, 2, x_chunk[2])
+                load_rows(x, 3, x_chunk[3])
+                for bc in range(1, B_CHUNKS):
+                    load_rows(grad_out, bc, g_raw[bc][:])
 
-            nc.vector.tensor_copy(out=own_knot[:, LEFT], in_=knots[:, :, LEFT].rearrange("p t k -> p k t"))
-            nc.vector.tensor_copy(
-                out=own_knot[:, RIGHT],
-                in_=knots[:, :, FIRST + SPAN : FIRST_LEFT + SPAN].rearrange("p t k -> p k t"),
-            )
-            transpose_x(0, 0, nc.scalar.copy)
-            nc.scalar.copy(out=scaler_signed[:, 0], in_=scaler_raw[:].rearrange("p t i -> p i t"))
-            lead, weight, root, shift, chain = spline_constants(nc, consts, knots, own_knot)
-            new_sorted(0)
-            quarter = P // 4
-            others = clamp_calls(0)
-            others += [
-                partial(sort_ssw, 0, half, nc.vector.tensor_copy, slice(i0, i0 + quarter))
-                for half in range(2)
-                for i0 in range(0, P, quarter)
-            ]
-            others.append(partial(nc.vector.tensor_scalar_mul, out=scaler_signed[:, 1], in0=scaler_signed[:, 0], scalar1=-1.0))
-            others += [partial(scale_ssw, 0, slice(j0, j0 + 2)) for j0 in range(0, BASES, 2)]
-            head = len(chain) - len(others)
-            for call in chain[:head]:
-                call()
-            weave(chain[head:], others)
-            spline_raw.append(load_spline_tile(nc, weights, spline_flat, 1))
-            square(0)
-            steps(0, nc.vector)
-            quantise_ssw(0)
-            transpose_g(0, nc.scalar.copy)
-            quantise_g(0)
-            for bc in range(1, B_CHUNKS):
-                transpose_x(0, bc, nc.scalar.copy)
-            nc.vector.tensor_copy(out=base_grouped[:], in_=base_raw[:].rearrange("p t i -> p i t"))
-            nc.vector.quantize_mx(
-                out=base_codes[:].bitcast(E4M3X4),
-                scales=base_scales[:],
-                in_=base_grouped[:].rearrange("p i t -> p (i t)"),
-            )
-            sigmoid(0)
-            silu_minus(0)
-            for bc in range(1, B_CHUNKS):
-                transpose_g(bc, nc.vector.tensor_copy)
-                quantise_g(bc)
-            for it in range(1, I_TILES):
-                for bc in range(B_CHUNKS):
-                    transpose_x(it, bc, nc.vector.tensor_copy if it == 1 else nc.scalar.copy)
+                nc.vector.tensor_copy(out=own_knot[:, LEFT], in_=knots[:, :, LEFT].rearrange("p t k -> p k t"))
+                nc.vector.tensor_copy(
+                    out=own_knot[:, RIGHT],
+                    in_=knots[:, :, FIRST + SPAN : FIRST_LEFT + SPAN].rearrange("p t k -> p k t"),
+                )
+                transpose_x(0, 0, nc.scalar.copy)
+                nc.scalar.copy(out=scaler_signed[:, 0], in_=scaler_raw[:].rearrange("p t i -> p i t"))
+                lead, weight, root, shift, chain = spline_constants(nc, consts, knots, own_knot)
+                new_sorted(0)
+                quarter = P // 4
+                others = clamp_calls(0)
+                others += [
+                    partial(sort_ssw, 0, half, nc.vector.tensor_copy, slice(i0, i0 + quarter))
+                    for half in range(2)
+                    for i0 in range(0, P, quarter)
+                ]
+                others.append(partial(nc.vector.tensor_scalar_mul, out=scaler_signed[:, 1], in0=scaler_signed[:, 0], scalar1=-1.0))
+                others += [partial(scale_ssw, 0, slice(j0, j0 + 2)) for j0 in range(0, BASES, 2)]
+                head = len(chain) - len(others)
+                for call in chain[:head]:
+                    call()
+                weave(chain[head:], others)
+                spline_raw.append(load_spline_tile(nc, weights, spline_flat, 1))
+                square(0)
+                transpose_g(0, nc.scalar.copy)
+                for bc in range(1, B_CHUNKS):
+                    transpose_x(0, bc, nc.scalar.copy)
+                base_calls = [
+                    partial(nc.vector.tensor_copy, out=base_grouped[:], in_=base_raw[:].rearrange("p t i -> p i t")),
+                    partial(
+                        nc.vector.quantize_mx,
+                        out=base_codes[:].bitcast(E4M3X4),
+                        scales=base_scales[:],
+                        in_=base_grouped[:].rearrange("p i t -> p (i t)"),
+                    ),
+                ]
+                quantise_ssw(0)
+                base_calls[0]()
+                weave(step_calls(0, nc.vector), [partial(quantise_g, 0)] + base_calls[1:] + clamp_calls(1))
+                for it in range(1, I_TILES):
+                    for bc in range(B_CHUNKS):
+                        transpose_x(it, bc, nc.scalar.copy)
+                square(1)
+                sigmoid(0)
+                silu_minus(0)
+                for bc in range(1, B_CHUNKS):
+                    transpose_g(bc, nc.vector.tensor_copy)
+                    quantise_g(bc)
+
+            prods = ctx.enter_context(tc.tile_pool(name="prods", bufs=2, reuse_waits="tile"))
 
             before = None
             for n, (it, bc) in enumerate(tiles):
@@ -489,15 +499,21 @@ def tile_bsplinekanlayer_t_kernel(
                 if more and bc == 3:
                     scale_ssw(it + 1, slice(half_bases, BASES))
                     quantise_ssw(it + 1)
-                if n + 1 < len(tiles):
-                    for call in clamp_calls(n + 1):
+                if n + 2 < len(tiles):
+                    for call in clamp_calls(n + 2):
                         call()
-                    square(n + 1)
-                    steps(n + 1, nc.gpsimd)
+                    square(n + 2)
+                if n + 1 < len(tiles):
+                    let_gpsimd_begin(n + 1)
+                    for call in step_calls(n + 1, nc.gpsimd):
+                        call()
 
+                if bc > 0:
+                    sig_t = transpose_sigmoid(it, bc)
                 if before:
                     add_up_and_store(*before)
-                sig_t = transpose_sigmoid(it, bc)
+                if bc == 0:
+                    sig_t = transpose_sigmoid(it, bc)
                 if more and bc == 0:
                     new_sorted(it + 1)
                 if more and bc < 2:

@@ -93,6 +93,22 @@ def spline_constants(nc, consts, knots, own_knot):
 
     root = consts.tile([P, BASES, I_TILES], F32)
     then(nc.scalar.activation, out=root[:], in_=gain[:], func=ACT.Sqrt)
+    head, calls = calls, []
+    newton = consts.tile([P, BASES, I_TILES], F32)
+    then(nc.vector.reciprocal, out=newton[:], in_=root[:])
+    then(nc.vector.tensor_mul, out=newton[:], in0=newton[:], in1=gain[:])
+    then(nc.vector.tensor_add, out=newton[:], in0=newton[:], in1=root[:])
+    then(nc.vector.tensor_scalar_mul, out=root[:], in0=newton[:], scalar1=0.5)
+    shift = consts.tile([P, BASES, I_TILES], F32)
+    then(
+        nc.vector.scalar_tensor_tensor,
+        out=shift[:, FIRST:],
+        in0=root[:, FIRST:],
+        scalar=-1.0,
+        in1=own_knot[:, FIRST:],
+        op0=ALU.mult,
+        op1=ALU.mult,
+    )
     inv_gain = consts.tile([P, BASES, I_TILES], F32)
     then(nc.vector.reciprocal, out=inv_gain[:], in_=gain[:])
 
@@ -113,24 +129,13 @@ def spline_constants(nc, consts, knots, own_knot):
         )
     n46 = WEIGHTED_STEPS.index((4, 6))
     n47 = WEIGHTED_STEPS.index((4, 7))
-
-    newton = consts.tile([P, BASES, I_TILES], F32)
-    then(nc.vector.reciprocal, out=newton[:], in_=root[:])
-    then(nc.vector.tensor_mul, out=newton[:], in0=newton[:], in1=gain[:])
-    then(nc.vector.tensor_add, out=newton[:], in0=newton[:], in1=root[:])
-    then(nc.vector.tensor_scalar_mul, out=root[:], in0=newton[:], scalar1=0.5)
-    shift = consts.tile([P, BASES, I_TILES], F32)
-    then(
-        nc.vector.scalar_tensor_tensor,
-        out=shift[:, FIRST:],
-        in0=root[:, FIRST:],
-        scalar=-1.0,
-        in1=own_knot[:, FIRST:],
-        op0=ALU.mult,
-        op1=ALU.mult,
-    )
     then(nc.vector.tensor_add, out=weight[:, n47], in0=weight[:, n47], in1=weight[:, n46])
-    return lead, weight, root, shift, calls
+    bare = consts.tile([P, len(WEIGHTED_STEPS), I_TILES], F32)
+    inv_lead = consts.tile([P, BASES, I_TILES], F32)
+    then(nc.vector.reciprocal, out=inv_lead[:, FIRST:], in_=lead[:, FIRST:])
+    for n, (m, k) in enumerate(WEIGHTED_STEPS):
+        then(nc.vector.tensor_mul, out=bare[:, n], in0=weight[:, n], in1=inv_lead[:, m])
+    return lead, weight, bare, root, shift, head, calls
 
 
 def weave(chain, others):
@@ -177,6 +182,10 @@ def tile_bsplinekanlayer_t_kernel(
         make_identity(nc, ident_f32[:])
         ident_bf = consts.tile([P, P], BF16)
         make_identity(nc, ident_bf[:])
+
+        warm = consts.tile([P, 1], F32)
+        nc.vector.memset(warm[:], 1.0)
+        nc.scalar.activation(out=warm[:], in_=warm[:], func=ACT.Sqrt)
 
         x_raw = keep.tile([P, ROWS // P, FEATURES], BF16)
         x_t = keep.tile([P, I_TILES, ROWS], BF16)
@@ -309,8 +318,12 @@ def tile_bsplinekanlayer_t_kernel(
         neg_silu_of = {}
 
         def sigmoid(it):
-            sig = silu.tile([P, ROWS // P, P], F32, bufs=1)
-            nc.scalar.activation(out=sig[:], in_=x_raw[:, :, it * P : (it + 1) * P], func=ACT.Sigmoid)
+            if it == I_TILES - 1:
+                sig = silu.tile([P, ROWS], F32, bufs=1)
+                nc.scalar.activation(out=sig[:], in_=x_t[:, it, :], func=ACT.Sigmoid)
+            else:
+                sig = silu.tile([P, ROWS // P, P], F32, bufs=1)
+                nc.scalar.activation(out=sig[:], in_=x_raw[:, :, it * P : (it + 1) * P], func=ACT.Sigmoid)
             sigmoid_of[it] = sig
 
         def silu_minus(it):
@@ -322,7 +335,7 @@ def tile_bsplinekanlayer_t_kernel(
             sig_t = sums.tile([P, B_SUB, P], F32)
             for t in range(B_SUB):
                 nc.tensor.transpose(sig_t[:, t, :], sigmoid_of[it][:, bc * B_SUB + t, :], ident_f32[:])
-            return sig_t
+            return sig_t[:].rearrange("p t b -> p (t b)")
 
         def minus_dsilu(it, bc, sig_t):
             part = neg_silu_of[it][:, bc * N : (bc + 1) * N]
@@ -330,7 +343,7 @@ def tile_bsplinekanlayer_t_kernel(
                 out=part,
                 in0=part,
                 scalar=1.0,
-                in1=sig_t[:].rearrange("p t b -> p (t b)"),
+                in1=sig_t,
                 op0=ALU.subtract,
                 op1=ALU.mult,
             )
@@ -403,8 +416,10 @@ def tile_bsplinekanlayer_t_kernel(
                     in_=knots[:, :, FIRST + SPAN : FIRST_LEFT + SPAN].rearrange("p t k -> p k t"),
                 )
                 transpose_x(0, 0, nc.scalar.copy)
+                lead, weight, bare, root, shift, head, chain = spline_constants(nc, consts, knots, own_knot)
+                for call in head:
+                    call()
                 nc.scalar.copy(out=scaler_signed[:, 0], in_=scaler_raw[:].rearrange("p t i -> p i t"))
-                lead, weight, root, shift, chain = spline_constants(nc, consts, knots, own_knot)
                 new_sorted(0)
                 quarter = P // 4
                 others = clamp_calls(0)
@@ -415,10 +430,7 @@ def tile_bsplinekanlayer_t_kernel(
                 ]
                 others.append(partial(nc.vector.tensor_scalar_mul, out=scaler_signed[:, 1], in0=scaler_signed[:, 0], scalar1=-1.0))
                 others += [partial(scale_ssw, 0, slice(j0, j0 + 2)) for j0 in range(0, BASES, 2)]
-                head = len(chain) - len(others)
-                for call in chain[:head]:
-                    call()
-                weave(chain[head:], others)
+                weave(chain, others)
                 spline_raw.append(load_spline_tile(nc, weights, spline_flat, 1))
                 square(0)
                 transpose_g(0, nc.scalar.copy)
@@ -436,13 +448,15 @@ def tile_bsplinekanlayer_t_kernel(
                 quantise_ssw(0)
                 base_calls[0]()
                 weave(step_calls(0, nc.vector), [partial(quantise_g, 0)] + base_calls[1:] + clamp_calls(1))
+                transpose_g(1, nc.scalar.copy)
                 for it in range(1, I_TILES):
                     for bc in range(B_CHUNKS):
                         transpose_x(it, bc, nc.scalar.copy)
                 square(1)
+                quantise_g(1)
                 sigmoid(0)
                 silu_minus(0)
-                for bc in range(1, B_CHUNKS):
+                for bc in range(2, B_CHUNKS):
                     transpose_g(bc, nc.vector.tensor_copy)
                     quantise_g(bc)
 
@@ -480,7 +494,7 @@ def tile_bsplinekanlayer_t_kernel(
                         terms = [(lead[:, m, it : it + 1], f[m])] + [
                             (weight[:, n_step, it : it + 1], f[k])
                             for n_step, (m_step, k) in enumerate(WEIGHTED_STEPS)
-                            if m_step == m
+                            if m_step == m and not last
                         ]
                     else:
                         terms = [(-1.0, neg_silu_of[it][:, b_cols])]
@@ -493,6 +507,12 @@ def tile_bsplinekanlayer_t_kernel(
                 for m in range(FIRST, FIRST + BANKS):
                     run_passes(m)
 
+                last = n == len(tiles) - 1
+                if last:
+                    for n_step, (m, k) in enumerate(WEIGHTED_STEPS):
+                        nc.vector.scalar_tensor_tensor(
+                            out=f[m], in0=f[k], scalar=bare[:, n_step, it : it + 1], in1=f[m], op0=ALU.mult, op1=ALU.add
+                        )
                 more = it + 1 < I_TILES
                 if more and bc == 2:
                     scale_ssw(it + 1, slice(0, half_bases))
@@ -503,16 +523,18 @@ def tile_bsplinekanlayer_t_kernel(
                     for call in clamp_calls(n + 2):
                         call()
                     square(n + 2)
+                if not more and bc > 0:
+                    minus_dsilu(it, bc, sigmoid_of[it][:, b_cols])
                 if n + 1 < len(tiles):
                     let_gpsimd_begin(n + 1)
                     for call in step_calls(n + 1, nc.gpsimd):
                         call()
 
-                if bc > 0:
+                if bc > 0 and more:
                     sig_t = transpose_sigmoid(it, bc)
                 if before:
                     add_up_and_store(*before)
-                if bc == 0:
+                if bc == 0 and more:
                     sig_t = transpose_sigmoid(it, bc)
                 if more and bc == 0:
                     new_sorted(it + 1)
@@ -525,10 +547,11 @@ def tile_bsplinekanlayer_t_kernel(
                 if more and bc == 3:
                     sigmoid(it + 1)
 
-                last = n == len(tiles) - 1
                 for m in range(FIRST, BASES + 1):
-                    if m == BASES - 1:
+                    if m == BASES - 1 and more:
                         minus_dsilu(it, bc, sig_t)
+                    if m == BASES - 1 and not more and bc == 0:
+                        minus_dsilu(it, bc, sigmoid_of[it][:, b_cols])
                     run_products(m)
                     if m + BANKS <= BASES:
                         run_passes(m + BANKS)

@@ -36,69 +36,72 @@ LEFT = slice(FIRST_LEFT, BASES)
 RIGHT = slice(FIRST, FIRST_LEFT)
 
 
+def half_of(parity):
+    return slice(parity * (BASES // 2), (parity + 1) * (BASES // 2))
+
+
 def toward_edge(j):
     return 1 if j >= FIRST_LEFT else -1
 
 
 PLAIN_STEPS = ((4, 5), (3, 2), (5, 6), (2, 1), (6, 7))
 STEP_ORDER = (4, 3, 5, 2, 6, 1, 7)
-STEP_GROUPS = (((4, 5), (3, 2)), ((5, 6), (2, 1)), ((6, 7),))
-WEIGHTED_STEPS = ((3, 1), (4, 6), (4, 7), (5, 7))
+WEIGHTED_STEPS = ((3, 1), (4, 6), (5, 7), (4, 7))
 
 
 def load_knots(nc, consts, grid):
     knots = consts.tile([P, I_TILES, KNOTS], BF16)
     nc.sync.dma_start(out=knots[:], in_=grid.rearrange("(t p) k -> p t k", p=P))
-    return knots
+    return knots[:].rearrange("p t k -> p k t")
 
 
 def spline_constants(nc, consts, knots, own_knot):
     ends = SPAN + 1
-    shape = [P, ends, BASES, I_TILES]
     calls = []
 
     def then(builder, **operands):
         calls.append(partial(builder, **operands))
 
-    window = consts.tile(shape, F32)
-    for a in range(ends):
-        then(nc.vector.tensor_copy, out=window[:, a], in_=knots[:, :, a : a + BASES].rearrange("p t k -> p k t"))
-
-    diff = consts.tile([P, SPAN] + shape[1:], F32)
-    for r in range(1, ends):
-        wrap = ends - r
-        then(nc.vector.tensor_sub, out=diff[:, r - 1, 0:wrap], in0=window[:, 0:wrap], in1=window[:, r:ends])
-        then(nc.vector.tensor_sub, out=diff[:, r - 1, wrap:ends], in0=window[:, wrap:ends], in1=window[:, 0:r])
-    den = consts.tile(shape, F32)
-    then(nc.vector.tensor_mul, out=den[:], in0=diff[:, 0], in1=diff[:, 1])
-    then(nc.vector.tensor_mul, out=den[:], in0=den[:], in1=diff[:, 2])
-    inv_den = consts.tile(shape, F32)
-    then(nc.vector.reciprocal, out=inv_den[:], in_=den[:])
+    gap = consts.tile([P, SPAN, KNOTS, I_TILES], F32)
+    for s in range(1, ends):
+        then(nc.vector.tensor_sub, out=gap[:, s - 1, 0 : KNOTS - s], in0=knots[:, 0 : KNOTS - s], in1=knots[:, s:])
+    one, two, three = [gap[:, s] for s in range(SPAN)]
+    pair = consts.tile([P, SPAN, BASES + 1, I_TILES], F32)
+    next_m = slice(1, BASES + 1)
+    then(nc.vector.tensor_mul, out=pair[:, 0], in0=one[:, 0 : BASES + 1], in1=two[:, 0 : BASES + 1])
+    then(nc.vector.tensor_mul, out=pair[:, 1], in0=one[:, 0 : BASES + 1], in1=one[:, 1 : BASES + 2])
+    then(nc.vector.tensor_mul, out=pair[:, 2], in0=two[:, 0 : BASES + 1], in1=one[:, 1 : BASES + 2])
+    signed_den = consts.tile([P, ends, BASES, I_TILES], F32)
+    then(nc.vector.tensor_mul, out=signed_den[:, 0], in0=three[:, 0:BASES], in1=pair[:, 0, 0:BASES])
+    then(nc.vector.tensor_mul, out=signed_den[:, 1], in0=one[:, 0:BASES], in1=pair[:, 0, next_m])
+    then(nc.vector.tensor_mul, out=signed_den[:, 2], in0=two[:, 0:BASES], in1=pair[:, 1, next_m])
+    then(nc.vector.tensor_mul, out=signed_den[:, 3], in0=three[:, 0:BASES], in1=pair[:, 2, next_m])
+    inv_den = consts.tile([P, ends, BASES, I_TILES], F32)
+    then(nc.vector.reciprocal, out=inv_den[:], in_=signed_den[:])
 
     gain = consts.tile([P, BASES, I_TILES], F32)
     then(nc.vector.memset, ap=gain[:], constant=1.0)
     neighbour = consts.tile([P, BASES, I_TILES], F32)
     for side, own, next_to_own in ((LEFT, 0, 1), (RIGHT, SPAN, SPAN - 1)):
-        then(
-            nc.vector.scalar_tensor_tensor,
-            out=neighbour[:, side],
-            in0=den[:, own, side],
-            scalar=-1.0,
-            in1=inv_den[:, next_to_own, side],
-            op0=ALU.mult,
-            op1=ALU.mult,
-        )
+        then(nc.vector.tensor_mul, out=neighbour[:, side], in0=signed_den[:, own, side], in1=inv_den[:, next_to_own, side])
     for m, k in PLAIN_STEPS:
         then(nc.vector.tensor_mul, out=gain[:, k], in0=neighbour[:, m], in1=gain[:, m])
 
-    root = consts.tile([P, BASES, I_TILES], F32)
-    then(nc.scalar.activation, out=root[:], in_=gain[:], func=ACT.Sqrt)
+    half_root = consts.tile([P, BASES, I_TILES], F32)
+    then(nc.scalar.activation, out=half_root[:], in_=gain[:], func=ACT.Sqrt, scale=0.25)
     head, calls = calls, []
-    newton = consts.tile([P, BASES, I_TILES], F32)
-    then(nc.vector.reciprocal, out=newton[:], in_=root[:])
-    then(nc.vector.tensor_mul, out=newton[:], in0=newton[:], in1=gain[:])
-    then(nc.vector.tensor_add, out=newton[:], in0=newton[:], in1=root[:])
-    then(nc.vector.tensor_scalar_mul, out=root[:], in0=newton[:], scalar1=0.5)
+    root = consts.tile([P, BASES, I_TILES], F32)
+    then(nc.vector.reciprocal, out=root[:], in_=half_root[:])
+    then(
+        nc.vector.scalar_tensor_tensor,
+        out=root[:],
+        in0=root[:],
+        scalar=0.25,
+        in1=gain[:],
+        op0=ALU.mult,
+        op1=ALU.mult,
+    )
+    then(nc.vector.tensor_add, out=root[:], in0=root[:], in1=half_root[:])
     shift = consts.tile([P, BASES, I_TILES], F32)
     then(
         nc.vector.scalar_tensor_tensor,
@@ -112,30 +115,32 @@ def spline_constants(nc, consts, knots, own_knot):
     inv_gain = consts.tile([P, BASES, I_TILES], F32)
     then(nc.vector.reciprocal, out=inv_gain[:], in_=gain[:])
 
-    signs = {m: 3.0 if (m >= FIRST_LEFT) == (m % 2 == 1) else -3.0 for m in range(FIRST, BASES)}
+    def factor(m, a):
+        return (3.0 if m < FIRST_LEFT else -3.0) * (-1.0 if (m + a) % 2 else 1.0)
+
     lead = consts.tile([P, BASES, I_TILES], F32)
     weight = consts.tile([P, len(WEIGHTED_STEPS), I_TILES], F32)
-    places = [(lead[:, m], m, m) for m in range(FIRST, BASES)]
-    places += [(weight[:, n], m, k) for n, (m, k) in enumerate(WEIGHTED_STEPS)]
-    for place, m, k in places:
+    places = []
+    for side, own in ((LEFT, 0), (RIGHT, SPAN)):
+        for start in (side.start, side.start + 1):
+            ms = slice(start, side.stop, 2)
+            places.append((lead[:, ms], own, ms, ms))
+    for n, (m, k) in enumerate(WEIGHTED_STEPS):
+        places.append((weight[:, n : n + 1], knot_of(m, k), slice(m, m + 1), slice(k, k + 1)))
+    for place, a, ms, ks in places:
         then(
             nc.vector.scalar_tensor_tensor,
             out=place,
-            in0=inv_den[:, knot_of(m, k), m],
-            scalar=signs[m],
-            in1=inv_gain[:, k],
+            in0=inv_den[:, a, ms],
+            scalar=factor(ms.start, a),
+            in1=inv_gain[:, ks],
             op0=ALU.mult,
             op1=ALU.mult,
         )
     n46 = WEIGHTED_STEPS.index((4, 6))
     n47 = WEIGHTED_STEPS.index((4, 7))
     then(nc.vector.tensor_add, out=weight[:, n47], in0=weight[:, n47], in1=weight[:, n46])
-    bare = consts.tile([P, len(WEIGHTED_STEPS), I_TILES], F32)
-    inv_lead = consts.tile([P, BASES, I_TILES], F32)
-    then(nc.vector.reciprocal, out=inv_lead[:, FIRST:], in_=lead[:, FIRST:])
-    for n, (m, k) in enumerate(WEIGHTED_STEPS):
-        then(nc.vector.tensor_mul, out=bare[:, n], in0=weight[:, n], in1=inv_lead[:, m])
-    return lead, weight, bare, root, shift, head, calls
+    return lead, weight, root, shift, head, calls
 
 
 def weave(chain, others):
@@ -193,36 +198,37 @@ def tile_bsplinekanlayer_t_kernel(
         g_scales = keep.tile([P, ROWS], U8, align_bytes=64)
         base_codes = keep.tile([P, FEATURES], U32, align_bytes=64)
         base_scales = keep.tile([P, FEATURES], U8, align_bytes=64)
-        scaler_signed = keep.tile([P, 2, FEATURES, PACK], BF16)
+        scaler = keep.tile([P, FEATURES, PACK], BF16)
         own_knot = keep.tile([P, BASES, I_TILES], F32)
 
         spline_flat = spline_weight.rearrange("o i j -> o (i j)")
         spline_raw = []
         ssw_sorted = {}
         ssw = {}
-        half_bases = BASES // 2
-
         def load_rows(rows_in_dram, bc, tile):
             nc.sync.dma_start(
                 out=tile, in_=rows_in_dram[bc * N : (bc + 1) * N, :].rearrange("(t p) c -> p t c", p=P)
             )
 
-        def sort_ssw(it, half, sorting_copy, features=slice(0, P)):
-            js = slice(half * half_bases, (half + 1) * half_bases)
-            sorting_copy(
-                out=ssw_sorted[it][:, js, :].rearrange("p j (i t) -> p i t j", t=PACK)[:, features],
-                in_=spline_raw[it][:].rearrange("p t (i j) -> p i t j", j=BASES)[:, features, :, js],
-            )
+        def sort_ssw(it, parity, engine, features=slice(0, P)):
+            to = ssw_sorted[it][:, half_of(parity), :].rearrange("p j (i t) -> p i t j", t=PACK)[:, features]
+            by = spline_raw[it][:].rearrange("p t (i j) -> p i t j", j=BASES)[:, features, :, parity::2]
+            if parity == 0:
+                copy_out = nc.vector.tensor_copy if engine == "vector" else nc.scalar.copy
+                copy_out(out=to, in_=by)
+            elif engine == "vector":
+                nc.vector.tensor_scalar_mul(out=to, in0=by, scalar1=-1.0)
+            else:
+                nc.scalar.mul(out=to, in_=by, mul=-1.0)
 
-        def scale_ssw(it, js):
-            by_sign = ssw_sorted[it][:, js, :].rearrange("p (h s) w -> p h s w", s=2)
+        def scale_ssw(it, parity):
             nc.vector.tensor_tensor(
-                out=by_sign,
-                in0=by_sign,
-                in1=scaler_signed[:, :, it * P : (it + 1) * P, :]
-                .rearrange("p s i t -> p s (i t)")
+                out=ssw_sorted[it][:, half_of(parity), :],
+                in0=ssw_sorted[it][:, half_of(parity), :],
+                in1=scaler[:, it * P : (it + 1) * P, :]
+                .rearrange("p i t -> p (i t)")
                 .unsqueeze(1)
-                .to_broadcast([P, (js.stop - js.start) // 2, 2, P * PACK]),
+                .to_broadcast([P, BASES // 2, P * PACK]),
                 op=ALU.mult,
             )
 
@@ -271,17 +277,22 @@ def tile_bsplinekanlayer_t_kernel(
             nc.vector.quantize_mx(out=g_codes[:, cols].bitcast(E5M2X4), scales=g_scales[:, cols], in_=g_grouped[bc])
 
         tiles = [(it, bc) for it in range(I_TILES) for bc in range(B_CHUNKS)]
+        u_pair = {}
         u_of = {}
         f_of = {}
         f_tile_of = {}
 
-        def clamp_calls(n):
+        def clamp_calls(n, count, places=slice(0, BASES - FIRST)):
             it, bc = tiles[n]
-            u = clamps.tile([P, len(STEP_ORDER), N], BF16)
-            u_of[n] = u
-            v = x_t[:, it, bc * N : (bc + 1) * N]
+            if places.start == 0:
+                u_pair[n] = clamps.tile([P, len(STEP_ORDER), count * N], BF16, name="u")
+            u = u_pair[n]
+            for after in range(count):
+                u_of[n + after] = u[:, :, after * N : (after + 1) * N]
+            v = x_t[:, it, bc * N : (bc + count) * N]
             calls = []
-            for place, m in enumerate(STEP_ORDER):
+            for place in range(places.start, places.stop):
+                m = STEP_ORDER[place]
                 cut = nc.vector.tensor_scalar_max if m >= FIRST_LEFT else nc.vector.tensor_scalar_min
                 calls.append(partial(cut, out=u[:, place, :], in0=v, scalar1=own_knot[:, m, it : it + 1]))
             return calls
@@ -300,15 +311,10 @@ def tile_bsplinekanlayer_t_kernel(
                     scale=root[:, m, it : it + 1],
                 )
 
-        def step_calls(n, engine):
-            calls = []
-            for group in STEP_GROUPS:
-                to, by = [
-                    f_tile_of[n][:, STEP_ORDER.index(group[0][end]) : STEP_ORDER.index(group[-1][end]) + 1, :]
-                    for end in range(2)
-                ]
-                calls.append(partial(engine.tensor_tensor, out=to, in0=to, in1=by, op=ALU.subtract))
-            return calls
+        def step(n, engine):
+            f = f_tile_of[n]
+            steps = len(PLAIN_STEPS)
+            engine.tensor_tensor(out=f[:, 0:steps, :], in0=f[:, 0:steps, :], in1=f[:, 2 : 2 + steps, :], op=ALU.subtract)
 
         def let_gpsimd_begin(n):
             column = f_of[n][STEP_ORDER[0]][:, 0:1]
@@ -410,26 +416,19 @@ def tile_bsplinekanlayer_t_kernel(
                 for bc in range(1, B_CHUNKS):
                     load_rows(grad_out, bc, g_raw[bc][:])
 
-                nc.vector.tensor_copy(out=own_knot[:, LEFT], in_=knots[:, :, LEFT].rearrange("p t k -> p k t"))
-                nc.vector.tensor_copy(
-                    out=own_knot[:, RIGHT],
-                    in_=knots[:, :, FIRST + SPAN : FIRST_LEFT + SPAN].rearrange("p t k -> p k t"),
-                )
+                nc.vector.tensor_copy(out=own_knot[:, LEFT], in_=knots[:, LEFT])
+                nc.vector.tensor_copy(out=own_knot[:, RIGHT], in_=knots[:, FIRST + SPAN : FIRST_LEFT + SPAN])
                 transpose_x(0, 0, nc.scalar.copy)
-                lead, weight, bare, root, shift, head, chain = spline_constants(nc, consts, knots, own_knot)
+                lead, weight, root, shift, head, chain = spline_constants(nc, consts, knots, own_knot)
                 for call in head:
                     call()
-                nc.scalar.copy(out=scaler_signed[:, 0], in_=scaler_raw[:].rearrange("p t i -> p i t"))
+                nc.scalar.copy(out=scaler[:], in_=scaler_raw[:].rearrange("p t i -> p i t"))
                 new_sorted(0)
-                quarter = P // 4
-                others = clamp_calls(0)
-                others += [
-                    partial(sort_ssw, 0, half, nc.vector.tensor_copy, slice(i0, i0 + quarter))
-                    for half in range(2)
-                    for i0 in range(0, P, quarter)
-                ]
-                others.append(partial(nc.vector.tensor_scalar_mul, out=scaler_signed[:, 1], in0=scaler_signed[:, 0], scalar1=-1.0))
-                others += [partial(scale_ssw, 0, slice(j0, j0 + 2)) for j0 in range(0, BASES, 2)]
+                others = clamp_calls(0, 1)
+                for parity in range(2):
+                    for i0 in range(0, P, P // 2):
+                        others.append(partial(sort_ssw, 0, parity, "vector", slice(i0, i0 + P // 2)))
+                others += [partial(scale_ssw, 0, parity) for parity in range(2)]
                 weave(chain, others)
                 spline_raw.append(load_spline_tile(nc, weights, spline_flat, 1))
                 square(0)
@@ -447,7 +446,11 @@ def tile_bsplinekanlayer_t_kernel(
                 ]
                 quantise_ssw(0)
                 base_calls[0]()
-                weave(step_calls(0, nc.vector), [partial(quantise_g, 0)] + base_calls[1:] + clamp_calls(1))
+                step(0, nc.vector)
+                quantise_g(0)
+                base_calls[1]()
+                for call in clamp_calls(1, 1) + clamp_calls(2, 2, slice(0, 4)):
+                    call()
                 transpose_g(1, nc.scalar.copy)
                 for it in range(1, I_TILES):
                     for bc in range(B_CHUNKS):
@@ -473,9 +476,11 @@ def tile_bsplinekanlayer_t_kernel(
                 def run_passes(m):
                     bank_of[m] = banks.tile([P, N], F32, tag="bank", name="bank")
                     if m < BASES:
-                        passes = [
-                            (ssw[it][0][:, c * P : (c + 1) * P], ssw[it][1][:, c * P : (c + 1) * P]) for c in (m, m - 1)
-                        ]
+                        passes = []
+                        for j in (m, m - 1):
+                            place = half_of(j % 2).start + j // 2
+                            columns = slice(place * P, (place + 1) * P)
+                            passes.append((ssw[it][0][:, columns], ssw[it][1][:, columns]))
                     else:
                         passes = [(base_codes[:, it * P : (it + 1) * P], base_scales[:, it * P : (it + 1) * P])]
                     for n_pass, (w_codes, w_scales) in enumerate(passes):
@@ -509,26 +514,34 @@ def tile_bsplinekanlayer_t_kernel(
 
                 last = n == len(tiles) - 1
                 if last:
+                    inv_lead = consts.tile([P, BASES, I_TILES], F32)
+                    nc.vector.reciprocal(out=inv_lead[:, FIRST:], in_=lead[:, FIRST:])
+                    bare = consts.tile([P, len(WEIGHTED_STEPS), I_TILES], F32)
+                    for n_step, (m, k) in enumerate(WEIGHTED_STEPS):
+                        nc.vector.tensor_mul(out=bare[:, n_step], in0=weight[:, n_step], in1=inv_lead[:, m])
                     for n_step, (m, k) in enumerate(WEIGHTED_STEPS):
                         nc.vector.scalar_tensor_tensor(
                             out=f[m], in0=f[k], scalar=bare[:, n_step, it : it + 1], in1=f[m], op0=ALU.mult, op1=ALU.add
                         )
                 more = it + 1 < I_TILES
                 if more and bc == 2:
-                    scale_ssw(it + 1, slice(0, half_bases))
+                    scale_ssw(it + 1, 0)
                 if more and bc == 3:
-                    scale_ssw(it + 1, slice(half_bases, BASES))
+                    scale_ssw(it + 1, 1)
                     quantise_ssw(it + 1)
                 if n + 2 < len(tiles):
-                    for call in clamp_calls(n + 2):
-                        call()
+                    if n % 2 == 0:
+                        for call in clamp_calls(n + 2, 2, slice(4, BASES - FIRST)):
+                            call()
+                    elif n + 3 < len(tiles):
+                        for call in clamp_calls(n + 3, 2, slice(0, 4)):
+                            call()
                     square(n + 2)
                 if not more and bc > 0:
                     minus_dsilu(it, bc, sigmoid_of[it][:, b_cols])
                 if n + 1 < len(tiles):
                     let_gpsimd_begin(n + 1)
-                    for call in step_calls(n + 1, nc.gpsimd):
-                        call()
+                    step(n + 1, nc.gpsimd)
 
                 if bc > 0 and more:
                     sig_t = transpose_sigmoid(it, bc)
@@ -539,7 +552,7 @@ def tile_bsplinekanlayer_t_kernel(
                 if more and bc == 0:
                     new_sorted(it + 1)
                 if more and bc < 2:
-                    sort_ssw(it + 1, bc, nc.scalar.copy)
+                    sort_ssw(it + 1, bc, "scalar")
                 if bc == 1 and it + 2 < I_TILES:
                     spline_raw.append(load_spline_tile(nc, weights, spline_flat, it + 2))
                 if more and bc == 2:

@@ -28,6 +28,8 @@ I_TILES = FEATURES // P
 B_CHUNKS = ROWS // N
 B_SUB = N // P
 BANKS = 6
+CHAINED = {13:4,14:2,15:4}
+BARE_AT = 13
 FREE_BANKS_AFTER = FIRST + BANKS - 2
 
 FLOPS = 2 * ROWS * OUTPUTS * (FEATURES + FEATURES * BASES)
@@ -44,6 +46,7 @@ def toward_edge(j):
     return 1 if j >= FIRST_LEFT else -1
 
 
+HEADS = ((FIRST_LEFT, 0), (FIRST_LEFT - 1, SPAN))
 PLAIN_STEPS = ((4, 5), (3, 2), (5, 6), (2, 1), (6, 7))
 STEP_ORDER = (4, 3, 5, 2, 6, 1, 7)
 WEIGHTED_STEPS = ((3, 1), (4, 6), (5, 7), (4, 7))
@@ -81,6 +84,8 @@ def spline_constants(nc, consts, knots, own_knot):
 
     gain = consts.tile([P, BASES, I_TILES], F32)
     then(nc.vector.memset, ap=gain[:], constant=1.0)
+    for m, own in HEADS:
+        then(nc.vector.tensor_scalar_mul, out=gain[:, m], in0=inv_den[:, own, m], scalar1=-3.0)
     neighbour = consts.tile([P, BASES, I_TILES], F32)
     for side, own, next_to_own in ((LEFT, 0, 1), (RIGHT, SPAN, SPAN - 1)):
         then(nc.vector.tensor_mul, out=neighbour[:, side], in0=signed_den[:, own, side], in1=inv_den[:, next_to_own, side])
@@ -496,10 +501,11 @@ def tile_bsplinekanlayer_t_kernel(
 
                 def run_products(m):
                     if m < BASES:
-                        terms = [(lead[:, m, it : it + 1], f[m])] + [
+                        head_lead = {m_head: 1.0 if m_head % 2 == 0 else -1.0 for m_head, own in HEADS}
+                        terms = [(head_lead[m] if m in head_lead else lead[:, m, it : it + 1], f[m])] + [
                             (weight[:, n_step, it : it + 1], f[k])
                             for n_step, (m_step, k) in enumerate(WEIGHTED_STEPS)
-                            if m_step == m and not last
+                            if m_step == m and n_step >= chained
                         ]
                     else:
                         terms = [(-1.0, neg_silu_of[it][:, b_cols])]
@@ -513,16 +519,17 @@ def tile_bsplinekanlayer_t_kernel(
                     run_passes(m)
 
                 last = n == len(tiles) - 1
-                if last:
+                if n == BARE_AT:
                     inv_lead = consts.tile([P, BASES, I_TILES], F32)
                     nc.vector.reciprocal(out=inv_lead[:, FIRST:], in_=lead[:, FIRST:])
                     bare = consts.tile([P, len(WEIGHTED_STEPS), I_TILES], F32)
                     for n_step, (m, k) in enumerate(WEIGHTED_STEPS):
                         nc.vector.tensor_mul(out=bare[:, n_step], in0=weight[:, n_step], in1=inv_lead[:, m])
-                    for n_step, (m, k) in enumerate(WEIGHTED_STEPS):
-                        nc.vector.scalar_tensor_tensor(
-                            out=f[m], in0=f[k], scalar=bare[:, n_step, it : it + 1], in1=f[m], op0=ALU.mult, op1=ALU.add
-                        )
+                chained = CHAINED.get(n, 0)
+                for n_step, (m, k) in enumerate(WEIGHTED_STEPS[:chained]):
+                    nc.vector.scalar_tensor_tensor(
+                        out=f[m], in0=f[k], scalar=bare[:, n_step, it : it + 1], in1=f[m], op0=ALU.mult, op1=ALU.add
+                    )
                 more = it + 1 < I_TILES
                 if more and bc == 2:
                     scale_ssw(it + 1, 0)

@@ -68,12 +68,16 @@ def spline_constants(nc, consts, knots, own_knot):
     gap = consts.tile([P, SPAN, KNOTS, I_TILES], F32)
     for s in range(1, ends):
         then(nc.vector.tensor_sub, out=gap[:, s - 1, 0 : KNOTS - s], in0=knots[:, 0 : KNOTS - s], in1=knots[:, s:])
+    then(nc.vector.tensor_copy, out=own_knot[:, LEFT], in_=knots[:, LEFT])
+    then(nc.vector.tensor_copy, out=own_knot[:, RIGHT], in_=knots[:, FIRST + SPAN : FIRST_LEFT + SPAN])
     one, two, three = [gap[:, s] for s in range(SPAN)]
     pair = consts.tile([P, SPAN, BASES + 1, I_TILES], F32)
     next_m = slice(1, BASES + 1)
     then(nc.vector.tensor_mul, out=pair[:, 0], in0=one[:, 0 : BASES + 1], in1=two[:, 0 : BASES + 1])
     then(nc.vector.tensor_mul, out=pair[:, 1], in0=one[:, 0 : BASES + 1], in1=one[:, 1 : BASES + 2])
     then(nc.vector.tensor_mul, out=pair[:, 2], in0=two[:, 0 : BASES + 1], in1=one[:, 1 : BASES + 2])
+    gain = consts.tile([P, BASES, I_TILES], F32)
+    then(nc.vector.memset, ap=gain[:], constant=1.0)
     signed_den = consts.tile([P, ends, BASES, I_TILES], F32)
     then(nc.vector.tensor_mul, out=signed_den[:, 0], in0=three[:, 0:BASES], in1=pair[:, 0, 0:BASES])
     then(nc.vector.tensor_mul, out=signed_den[:, 1], in0=one[:, 0:BASES], in1=pair[:, 0, next_m])
@@ -82,8 +86,6 @@ def spline_constants(nc, consts, knots, own_knot):
     inv_den = consts.tile([P, ends, BASES, I_TILES], F32)
     then(nc.vector.reciprocal, out=inv_den[:], in_=signed_den[:])
 
-    gain = consts.tile([P, BASES, I_TILES], F32)
-    then(nc.vector.memset, ap=gain[:], constant=1.0)
     for m, own in HEADS:
         then(nc.vector.tensor_scalar_mul, out=gain[:, m], in0=inv_den[:, own, m], scalar1=-3.0)
     neighbour = consts.tile([P, BASES, I_TILES], F32)
@@ -192,6 +194,8 @@ def tile_bsplinekanlayer_t_kernel(
         make_identity(nc, ident_f32[:])
         ident_bf = consts.tile([P, P], BF16)
         make_identity(nc, ident_bf[:])
+        minus_ident_bf = consts.tile([P, P], BF16)
+        nc.vector.tensor_scalar_mul(out=minus_ident_bf[:], in0=ident_bf[:], scalar1=-1.0)
 
         warm = consts.tile([P, 1], F32)
         nc.vector.memset(warm[:], 1.0)
@@ -234,6 +238,29 @@ def tile_bsplinekanlayer_t_kernel(
                 .rearrange("p i t -> p (i t)")
                 .unsqueeze(1)
                 .to_broadcast([P, BASES // 2, P * PACK]),
+                op=ALU.mult,
+            )
+
+        sorted_banks = {}
+
+        def sort_odd_first(place):
+            bank = banks.tile([P, 2, P * PACK], BF16, tag="bank", name="sorted_bank")
+            sorted_banks[place] = bank
+            for p in range(2):
+                j = 2 * (place + p - half_of(1).start) + 1
+                nc.tensor.matmul(
+                    out=bank[:, p, :],
+                    lhsT=minus_ident_bf[:],
+                    rhs=spline_raw[0][:].rearrange("p t (i j) -> p j i t", j=BASES)[:, j],
+                    start=True,
+                    stop=True,
+                )
+
+        def scale_odd_first(place):
+            nc.vector.tensor_tensor(
+                out=ssw_sorted[0][:, place : place + 2, :],
+                in0=sorted_banks[place][:],
+                in1=scaler[:, 0:P, :].rearrange("p i t -> p (i t)").unsqueeze(1).to_broadcast([P, 2, P * PACK]),
                 op=ALU.mult,
             )
 
@@ -421,8 +448,6 @@ def tile_bsplinekanlayer_t_kernel(
                 for bc in range(1, B_CHUNKS):
                     load_rows(grad_out, bc, g_raw[bc][:])
 
-                nc.vector.tensor_copy(out=own_knot[:, LEFT], in_=knots[:, LEFT])
-                nc.vector.tensor_copy(out=own_knot[:, RIGHT], in_=knots[:, FIRST + SPAN : FIRST_LEFT + SPAN])
                 transpose_x(0, 0, nc.scalar.copy)
                 lead, weight, root, shift, head, chain = spline_constants(nc, consts, knots, own_knot)
                 for call in head:
@@ -430,10 +455,12 @@ def tile_bsplinekanlayer_t_kernel(
                 nc.scalar.copy(out=scaler[:], in_=scaler_raw[:].rearrange("p t i -> p i t"))
                 new_sorted(0)
                 others = clamp_calls(0, 1)
-                for parity in range(2):
-                    for i0 in range(0, P, P // 2):
-                        others.append(partial(sort_ssw, 0, parity, "vector", slice(i0, i0 + P // 2)))
-                others += [partial(scale_ssw, 0, parity) for parity in range(2)]
+                for i0 in range(0, P, P // 2):
+                    others.append(partial(sort_ssw, 0, 0, "vector", slice(i0, i0 + P // 2)))
+                others.append(partial(scale_ssw, 0, 0))
+                for place in range(half_of(1).start, half_of(1).stop, 2):
+                    sort_odd_first(place)
+                    others.append(partial(scale_odd_first, place))
                 weave(chain, others)
                 spline_raw.append(load_spline_tile(nc, weights, spline_flat, 1))
                 square(0)
@@ -466,6 +493,7 @@ def tile_bsplinekanlayer_t_kernel(
                 silu_minus(0)
                 for bc in range(2, B_CHUNKS):
                     transpose_g(bc, nc.vector.tensor_copy)
+                for bc in range(2, B_CHUNKS):
                     quantise_g(bc)
 
             prods = ctx.enter_context(tc.tile_pool(name="prods", bufs=2, reuse_waits="tile"))

@@ -30,6 +30,7 @@ B_SUB = N // P
 BANKS = 6
 CHAINED = {13:4,14:2,15:4}
 BARE_AT = 13
+CLAMPS_AHEAD = {1: 4, 3: 2}
 FREE_BANKS_AFTER = FIRST + BANKS - 2
 
 FLOPS = 2 * ROWS * OUTPUTS * (FEATURES + FEATURES * BASES)
@@ -222,6 +223,8 @@ def tile_bsplinekanlayer_t_kernel(
         def sort_ssw(it, parity, engine, features=slice(0, P)):
             to = ssw_sorted[it][:, half_of(parity), :].rearrange("p j (i t) -> p i t j", t=PACK)[:, features]
             by = spline_raw[it][:].rearrange("p t (i j) -> p i t j", j=BASES)[:, features, :, parity::2]
+            if engine == "scalar":
+                to, by = to.rearrange("p i t j -> p i j t"), by.rearrange("p i t j -> p i j t")
             if parity == 0:
                 copy_out = nc.vector.tensor_copy if engine == "vector" else nc.scalar.copy
                 copy_out(out=to, in_=by)
@@ -481,12 +484,12 @@ def tile_bsplinekanlayer_t_kernel(
                 step(0, nc.vector)
                 quantise_g(0)
                 base_calls[1]()
-                for call in clamp_calls(1, 1) + clamp_calls(2, 2, slice(0, 4)):
+                for call in clamp_calls(1, 1) + clamp_calls(2, 2, slice(0, CLAMPS_AHEAD[B_CHUNKS - 1])):
                     call()
                 transpose_g(1, nc.scalar.copy)
                 for it in range(1, I_TILES):
                     for bc in range(B_CHUNKS):
-                        transpose_x(it, bc, nc.scalar.copy)
+                        transpose_x(it, bc, nc.vector.tensor_copy if it == 3 else nc.scalar.copy)
                 square(1)
                 quantise_g(1)
                 sigmoid(0)
@@ -566,10 +569,10 @@ def tile_bsplinekanlayer_t_kernel(
                     quantise_ssw(it + 1)
                 if n + 2 < len(tiles):
                     if n % 2 == 0:
-                        for call in clamp_calls(n + 2, 2, slice(4, BASES - FIRST)):
+                        for call in clamp_calls(n + 2, 2, slice(CLAMPS_AHEAD[(bc - 1) % B_CHUNKS], BASES - FIRST)):
                             call()
                     elif n + 3 < len(tiles):
-                        for call in clamp_calls(n + 3, 2, slice(0, 4)):
+                        for call in clamp_calls(n + 3, 2, slice(0, CLAMPS_AHEAD[bc])):
                             call()
                     square(n + 2)
                 if not more and bc > 0:

from contextlib import ExitStack
from functools import partial

import concourse.mybir as mybir
from concourse.masks import make_identity

F32 = mybir.dt.float32
BF16 = mybir.dt.bfloat16
U32 = mybir.dt.uint32
U8 = mybir.dt.uint8
E4M3X4 = mybir.dt.float8_e4m3fn_x4
E5M2X4 = mybir.dt.float8_e5m2_x4
ALU = mybir.AluOpType
ACT = mybir.ActivationFunctionType

P = 128
PACK = 4
ROWS = 2048
FEATURES = 512
OUTPUTS = 512
BASES = 8
KNOTS = 12
SPAN = 3
FIRST = 1
FIRST_LEFT = 4
N = 512
I_TILES = FEATURES // P
B_CHUNKS = ROWS // N
B_SUB = N // P
BANKS = 6
CHAINED = {13:4,14:2,15:4}
BARE_AT = 13
CLAMPS_AHEAD = {1: 4, 3: 2}
FREE_BANKS_AFTER = FIRST + BANKS - 2

FLOPS = 2 * ROWS * OUTPUTS * (FEATURES + FEATURES * BASES)

LEFT = slice(FIRST_LEFT, BASES)
RIGHT = slice(FIRST, FIRST_LEFT)


def half_of(parity):
    return slice(parity * (BASES // 2), (parity + 1) * (BASES // 2))


def toward_edge(j):
    return 1 if j >= FIRST_LEFT else -1


HEADS = ((FIRST_LEFT, 0), (FIRST_LEFT - 1, SPAN))
PLAIN_STEPS = ((4, 5), (3, 2), (5, 6), (2, 1), (6, 7))
STEP_ORDER = (4, 3, 5, 2, 6, 1, 7)
WEIGHTED_STEPS = ((3, 1), (4, 6), (5, 7), (4, 7))


def load_knots(nc, consts, grid):
    knots = consts.tile([P, I_TILES, KNOTS], BF16)
    nc.sync.dma_start(out=knots[:], in_=grid.rearrange("(t p) k -> p t k", p=P))
    return knots[:].rearrange("p t k -> p k t")


def spline_constants(nc, consts, knots, own_knot):
    ends = SPAN + 1
    calls = []

    def then(builder, **operands):
        calls.append(partial(builder, **operands))

    gap = consts.tile([P, SPAN, KNOTS, I_TILES], F32)
    for s in range(1, ends):
        then(nc.vector.tensor_sub, out=gap[:, s - 1, 0 : KNOTS - s], in0=knots[:, 0 : KNOTS - s], in1=knots[:, s:])
    then(nc.vector.tensor_copy, out=own_knot[:, LEFT], in_=knots[:, LEFT])
    then(nc.vector.tensor_copy, out=own_knot[:, RIGHT], in_=knots[:, FIRST + SPAN : FIRST_LEFT + SPAN])
    one, two, three = [gap[:, s] for s in range(SPAN)]
    pair = consts.tile([P, SPAN, BASES + 1, I_TILES], F32)
    next_m = slice(1, BASES + 1)
    then(nc.vector.tensor_mul, out=pair[:, 0], in0=one[:, 0 : BASES + 1], in1=two[:, 0 : BASES + 1])
    then(nc.vector.tensor_mul, out=pair[:, 1], in0=one[:, 0 : BASES + 1], in1=one[:, 1 : BASES + 2])
    then(nc.vector.tensor_mul, out=pair[:, 2], in0=two[:, 0 : BASES + 1], in1=one[:, 1 : BASES + 2])
    gain = consts.tile([P, BASES, I_TILES], F32)
    then(nc.vector.memset, ap=gain[:], constant=1.0)
    signed_den = consts.tile([P, ends, BASES, I_TILES], F32)
    then(nc.vector.tensor_mul, out=signed_den[:, 0], in0=three[:, 0:BASES], in1=pair[:, 0, 0:BASES])
    then(nc.vector.tensor_mul, out=signed_den[:, 1], in0=one[:, 0:BASES], in1=pair[:, 0, next_m])
    then(nc.vector.tensor_mul, out=signed_den[:, 2], in0=two[:, 0:BASES], in1=pair[:, 1, next_m])
    then(nc.vector.tensor_mul, out=signed_den[:, 3], in0=three[:, 0:BASES], in1=pair[:, 2, next_m])
    inv_den = consts.tile([P, ends, BASES, I_TILES], F32)
    then(nc.vector.reciprocal, out=inv_den[:], in_=signed_den[:])

    for m, own in HEADS:
        then(nc.vector.tensor_scalar_mul, out=gain[:, m], in0=inv_den[:, own, m], scalar1=-3.0)
    neighbour = consts.tile([P, BASES, I_TILES], F32)
    for side, own, next_to_own in ((LEFT, 0, 1), (RIGHT, SPAN, SPAN - 1)):
        then(nc.vector.tensor_mul, out=neighbour[:, side], in0=signed_den[:, own, side], in1=inv_den[:, next_to_own, side])
    for m, k in PLAIN_STEPS:
        then(nc.vector.tensor_mul, out=gain[:, k], in0=neighbour[:, m], in1=gain[:, m])

    half_root = consts.tile([P, BASES, I_TILES], F32)
    then(nc.scalar.activation, out=half_root[:], in_=gain[:], func=ACT.Sqrt, scale=0.25)
    head, calls = calls, []
    root = consts.tile([P, BASES, I_TILES], F32)
    then(nc.vector.reciprocal, out=root[:], in_=half_root[:])
    then(
        nc.vector.scalar_tensor_tensor,
        out=root[:],
        in0=root[:],
        scalar=0.25,
        in1=gain[:],
        op0=ALU.mult,
        op1=ALU.mult,
    )
    then(nc.vector.tensor_add, out=root[:], in0=root[:], in1=half_root[:])
    shift = consts.tile([P, BASES, I_TILES], F32)
    then(
        nc.vector.scalar_tensor_tensor,
        out=shift[:, FIRST:],
        in0=root[:, FIRST:],
        scalar=-1.0,
        in1=own_knot[:, FIRST:],
        op0=ALU.mult,
        op1=ALU.mult,
    )
    inv_gain = consts.tile([P, BASES, I_TILES], F32)
    then(nc.vector.reciprocal, out=inv_gain[:], in_=gain[:])

    def factor(m, a):
        return (3.0 if m < FIRST_LEFT else -3.0) * (-1.0 if (m + a) % 2 else 1.0)

    lead = consts.tile([P, BASES, I_TILES], F32)
    weight = consts.tile([P, len(WEIGHTED_STEPS), I_TILES], F32)
    places = []
    for side, own in ((LEFT, 0), (RIGHT, SPAN)):
        for start in (side.start, side.start + 1):
            ms = slice(start, side.stop, 2)
            places.append((lead[:, ms], own, ms, ms))
    for n, (m, k) in enumerate(WEIGHTED_STEPS):
        places.append((weight[:, n : n + 1], knot_of(m, k), slice(m, m + 1), slice(k, k + 1)))
    for place, a, ms, ks in places:
        then(
            nc.vector.scalar_tensor_tensor,
            out=place,
            in0=inv_den[:, a, ms],
            scalar=factor(ms.start, a),
            in1=inv_gain[:, ks],
            op0=ALU.mult,
            op1=ALU.mult,
        )
    n46 = WEIGHTED_STEPS.index((4, 6))
    n47 = WEIGHTED_STEPS.index((4, 7))
    then(nc.vector.tensor_add, out=weight[:, n47], in0=weight[:, n47], in1=weight[:, n46])
    return lead, weight, root, shift, head, calls


def weave(chain, others):
    for n in range(max(len(chain), len(others))):
        for calls in (chain, others):
            if n < len(calls):
                calls[n]()


def knot_of(m, k):
    return k - m if m >= FIRST_LEFT else SPAN - (m - k)


def load_k_first(nc, tile, rows):
    half = OUTPUTS // 2
    for u in range(2):
        nc.sync.dma_start(
            out=tile[:, 2 * u : 2 * u + 2, :],
            in_=rows[u * half : (u + 1) * half].rearrange("(p e) w -> p e w", e=2),
        )


def load_spline_tile(nc, pool, spline_flat, it):
    spline_raw = pool.tile([P, PACK, P * BASES], BF16, bufs=1)
    load_k_first(nc, spline_raw, spline_flat[:, it * P * BASES : (it + 1) * P * BASES])
    return spline_raw


def tile_bsplinekanlayer_t_kernel(
    tc, x, base_weight, spline_weight, spline_scaler, grid, grad_out, out
):
    nc = tc.nc
    with ExitStack() as ctx:
        consts = ctx.enter_context(tc.tile_pool(name="consts", bufs=1))
        keep = ctx.enter_context(tc.tile_pool(name="keep", bufs=1))
        weights = ctx.enter_context(tc.tile_pool(name="weights", bufs=2))
        clamps = ctx.enter_context(tc.tile_pool(name="clamps", bufs=2))
        squares = ctx.enter_context(tc.tile_pool(name="squares", bufs=3))
        silu = ctx.enter_context(tc.tile_pool(name="silu", bufs=2))
        banks = ctx.enter_context(tc.psum_pool(name="banks", bufs=BANKS))
        sums = ctx.enter_context(tc.psum_pool(name="sums", bufs=1))

        ident_f32 = consts.tile([P, P], F32)
        make_identity(nc, ident_f32[:])
        ident_bf = consts.tile([P, P], BF16)
        make_identity(nc, ident_bf[:])
        minus_ident_bf = consts.tile([P, P], BF16)
        nc.vector.tensor_scalar_mul(out=minus_ident_bf[:], in0=ident_bf[:], scalar1=-1.0)

        warm = consts.tile([P, 1], F32)
        nc.vector.memset(warm[:], 1.0)
        nc.scalar.activation(out=warm[:], in_=warm[:], func=ACT.Sqrt)

        x_raw = keep.tile([P, ROWS // P, FEATURES], BF16)
        x_t = keep.tile([P, I_TILES, ROWS], BF16)
        g_codes = keep.tile([P, ROWS], U32, align_bytes=64)
        g_scales = keep.tile([P, ROWS], U8, align_bytes=64)
        base_codes = keep.tile([P, FEATURES], U32, align_bytes=64)
        base_scales = keep.tile([P, FEATURES], U8, align_bytes=64)
        scaler = keep.tile([P, FEATURES, PACK], BF16)
        own_knot = keep.tile([P, BASES, I_TILES], F32)

        spline_flat = spline_weight.rearrange("o i j -> o (i j)")
        spline_raw = []
        ssw_sorted = {}
        ssw = {}
        def load_rows(rows_in_dram, bc, tile):
            nc.sync.dma_start(
                out=tile, in_=rows_in_dram[bc * N : (bc + 1) * N, :].rearrange("(t p) c -> p t c", p=P)
            )

        def sort_ssw(it, parity, engine, features=slice(0, P)):
            to = ssw_sorted[it][:, half_of(parity), :].rearrange("p j (i t) -> p i t j", t=PACK)[:, features]
            by = spline_raw[it][:].rearrange("p t (i j) -> p i t j", j=BASES)[:, features, :, parity::2]
            if engine == "scalar":
                to, by = to.rearrange("p i t j -> p i j t"), by.rearrange("p i t j -> p i j t")
            if parity == 0:
                copy_out = nc.vector.tensor_copy if engine == "vector" else nc.scalar.copy
                copy_out(out=to, in_=by)
            elif engine == "vector":
                nc.vector.tensor_scalar_mul(out=to, in0=by, scalar1=-1.0)
            else:
                nc.scalar.mul(out=to, in_=by, mul=-1.0)

        def scale_ssw(it, parity):
            nc.vector.tensor_tensor(
                out=ssw_sorted[it][:, half_of(parity), :],
                in0=ssw_sorted[it][:, half_of(parity), :],
                in1=scaler[:, it * P : (it + 1) * P, :]
                .rearrange("p i t -> p (i t)")
                .unsqueeze(1)
                .to_broadcast([P, BASES // 2, P * PACK]),
                op=ALU.mult,
            )

        sorted_banks = {}

        def sort_odd_first(place):
            bank = banks.tile([P, 2, P * PACK], BF16, tag="bank", name="sorted_bank")
            sorted_banks[place] = bank
            for p in range(2):
                j = 2 * (place + p - half_of(1).start) + 1
                nc.tensor.matmul(
                    out=bank[:, p, :],
                    lhsT=minus_ident_bf[:],
                    rhs=spline_raw[0][:].rearrange("p t (i j) -> p j i t", j=BASES)[:, j],
                    start=True,
                    stop=True,
                )

        def scale_odd_first(place):
            nc.vector.tensor_tensor(
                out=ssw_sorted[0][:, place : place + 2, :],
                in0=sorted_banks[place][:],
                in1=scaler[:, 0:P, :].rearrange("p i t -> p (i t)").unsqueeze(1).to_broadcast([P, 2, P * PACK]),
                op=ALU.mult,
            )

        def new_sorted(it):
            ssw_sorted[it] = weights.tile([P, BASES, P * PACK], BF16, name="ssw_sorted", align_bytes=64, bufs=1)

        def quantise_ssw(it):
            ssw_codes = weights.tile([P, BASES * P], U32, align_bytes=64)
            ssw_scales = weights.tile([P, BASES * P], U8, align_bytes=64)
            ssw[it] = (ssw_codes, ssw_scales)
            nc.vector.quantize_mx(
                out=ssw_codes[:].bitcast(E4M3X4),
                scales=ssw_scales[:],
                in_=ssw_sorted[it][:].rearrange("p j w -> p (j w)"),
            )

        def transpose_x(it, bc, copy_out):
            x_bank = banks.tile([P, N], BF16, tag="bank", name="x_bank")
            for t in range(B_SUB):
                nc.tensor.transpose(
                    x_bank[:, t * P : (t + 1) * P],
                    x_raw[:, bc * B_SUB + t, it * P : (it + 1) * P],
                    ident_bf[:],
                )
            copy_out(out=x_t[:, it, bc * N : (bc + 1) * N], in_=x_bank[:])

        g_grouped = {}

        def transpose_g(bc, copy_out):
            grouped = raw.tile([P, N, PACK], BF16, name="g_grouped", align_bytes=64, bufs=2)
            g_grouped[bc] = grouped[:].rearrange("p b t -> p (b t)")
            g_words = g_grouped[bc].bitcast(F32).rearrange("p (b u) -> p b u", u=2)
            for pair in range(B_SUB // 2):
                g_t = banks.tile([P, 2, 2, P], F32, tag="bank", name="g_t")
                for t in range(2):
                    words = g_raw[bc][:, 2 * pair + t, :].bitcast(F32)
                    for u in range(2):
                        nc.tensor.transpose(g_t[:, t, u, :], words[:, u * P : (u + 1) * P], ident_f32[:])
                copy_out(
                    out=g_words[:, 2 * pair * P : (2 * pair + 2) * P, :].rearrange("p (t b) u -> p t b u", t=2),
                    in_=g_t[:].rearrange("p t u b -> p t b u"),
                )

        def quantise_g(bc):
            cols = slice(bc * N, (bc + 1) * N)
            nc.vector.quantize_mx(out=g_codes[:, cols].bitcast(E5M2X4), scales=g_scales[:, cols], in_=g_grouped[bc])

        tiles = [(it, bc) for it in range(I_TILES) for bc in range(B_CHUNKS)]
        u_pair = {}
        u_of = {}
        f_of = {}
        f_tile_of = {}

        def clamp_calls(n, count, places=slice(0, BASES - FIRST)):
            it, bc = tiles[n]
            if places.start == 0:
                u_pair[n] = clamps.tile([P, len(STEP_ORDER), count * N], BF16, name="u")
            u = u_pair[n]
            for after in range(count):
                u_of[n + after] = u[:, :, after * N : (after + 1) * N]
            v = x_t[:, it, bc * N : (bc + count) * N]
            calls = []
            for place in range(places.start, places.stop):
                m = STEP_ORDER[place]
                cut = nc.vector.tensor_scalar_max if m >= FIRST_LEFT else nc.vector.tensor_scalar_min
                calls.append(partial(cut, out=u[:, place, :], in0=v, scalar1=own_knot[:, m, it : it + 1]))
            return calls

        def square(n):
            it = tiles[n][0]
            f = squares.tile([P, len(STEP_ORDER), N], F32)
            f_tile_of[n] = f
            f_of[n] = {m: f[:, place, :] for place, m in enumerate(STEP_ORDER)}
            for place, m in enumerate(STEP_ORDER):
                nc.scalar.activation(
                    out=f_of[n][m],
                    in_=u_of[n][:, place, :],
                    func=ACT.Square,
                    bias=shift[:, m, it : it + 1],
                    scale=root[:, m, it : it + 1],
                )

        def step(n, engine):
            f = f_tile_of[n]
            steps = len(PLAIN_STEPS)
            engine.tensor_tensor(out=f[:, 0:steps, :], in0=f[:, 0:steps, :], in1=f[:, 2 : 2 + steps, :], op=ALU.subtract)

        def let_gpsimd_begin(n):
            column = f_of[n][STEP_ORDER[0]][:, 0:1]
            nc.vector.tensor_copy(out=column, in_=column)

        sigmoid_of = {}
        neg_silu_of = {}

        def sigmoid(it):
            if it == I_TILES - 1:
                sig = silu.tile([P, ROWS], F32, bufs=1)
                nc.scalar.activation(out=sig[:], in_=x_t[:, it, :], func=ACT.Sigmoid)
            else:
                sig = silu.tile([P, ROWS // P, P], F32, bufs=1)
                nc.scalar.activation(out=sig[:], in_=x_raw[:, :, it * P : (it + 1) * P], func=ACT.Sigmoid)
            sigmoid_of[it] = sig

        def silu_minus(it):
            neg_silu = silu.tile([P, ROWS], F32)
            nc.scalar.activation(out=neg_silu[:], in_=x_t[:, it, :], func=ACT.Silu, scale=-1.0)
            neg_silu_of[it] = neg_silu

        def transpose_sigmoid(it, bc):
            sig_t = sums.tile([P, B_SUB, P], F32)
            for t in range(B_SUB):
                nc.tensor.transpose(sig_t[:, t, :], sigmoid_of[it][:, bc * B_SUB + t, :], ident_f32[:])
            return sig_t[:].rearrange("p t b -> p (t b)")

        def minus_dsilu(it, bc, sig_t):
            part = neg_silu_of[it][:, bc * N : (bc + 1) * N]
            nc.vector.scalar_tensor_tensor(
                out=part,
                in0=part,
                scalar=1.0,
                in1=sig_t,
                op0=ALU.subtract,
                op1=ALU.mult,
            )

        def add_up_and_store(prod, it, bc):
            total = sums.tile([P, B_SUB, P], F32, tag="total")
            for t in range(B_SUB):
                for j in range(len(prod)):
                    nc.tensor.matmul(
                        out=total[:, t, :],
                        lhsT=prod[j][:, t * P : (t + 1) * P],
                        rhs=ident_f32[:],
                        is_transpose=True,
                        start=(j == 0),
                        stop=(j == len(prod) - 1),
                    )
            result = prods.tile([P, B_SUB, P], F32)
            nc.scalar.copy(out=result[:], in_=total[:])
            nc.sync.dma_start(
                out=out[bc * N : (bc + 1) * N, it * P : (it + 1) * P].rearrange("(t p) i -> p t i", p=P),
                in_=result[:],
            )

        added = []

        def add_to_last(totals, prod, complete):
            for j in range(len(added), len(prod)):
                for t in range(B_SUB):
                    nc.tensor.matmul(
                        out=totals[t][:],
                        lhsT=prod[j][:, t * P : (t + 1) * P],
                        rhs=ident_f32[:],
                        is_transpose=True,
                        start=(j == 0),
                        stop=(complete and j == len(prod) - 1),
                    )
                added.append(j)

        def store_last(totals, it, bc):
            for t in range(B_SUB):
                piece = prods.tile([P, P], F32, name="piece%d" % t, bufs=1)
                copy_out = nc.vector.tensor_copy if t % 2 == 0 else nc.scalar.copy
                copy_out(out=piece[:], in_=totals[t][:])
                nc.sync.dma_start(
                    out=out[bc * N + t * P : bc * N + (t + 1) * P, it * P : (it + 1) * P], in_=piece[:]
                )

        with tc.manual_schedule():
            with tc.tile_pool(name="raw", bufs=1) as raw:
                scaler_raw = raw.tile([P, PACK, FEATURES], BF16)
                base_raw = raw.tile([P, PACK, FEATURES], BF16)
                base_grouped = raw.tile([P, FEATURES, PACK], BF16, align_bytes=64)
                knots = load_knots(nc, consts, grid)
                g_raw = [raw.tile([P, B_SUB, OUTPUTS], BF16, name="g_raw%d" % bc) for bc in range(B_CHUNKS)]
                x_chunk = [x_raw[:, bc * B_SUB : (bc + 1) * B_SUB, :] for bc in range(B_CHUNKS)]
                load_rows(x, 0, x_chunk[0])
                load_k_first(nc, scaler_raw, spline_scaler)
                spline_raw.append(load_spline_tile(nc, weights, spline_flat, 0))
                load_rows(grad_out, 0, g_raw[0][:])
                load_rows(x, 1, x_chunk[1])
                load_k_first(nc, base_raw, base_weight)
                load_rows(x, 2, x_chunk[2])
                load_rows(x, 3, x_chunk[3])
                for bc in range(1, B_CHUNKS):
                    load_rows(grad_out, bc, g_raw[bc][:])

                transpose_x(0, 0, nc.scalar.copy)
                lead, weight, root, shift, head, chain = spline_constants(nc, consts, knots, own_knot)
                for call in head:
                    call()
                nc.scalar.copy(out=scaler[:], in_=scaler_raw[:].rearrange("p t i -> p i t"))
                new_sorted(0)
                others = clamp_calls(0, 1)
                for i0 in range(0, P, P // 2):
                    others.append(partial(sort_ssw, 0, 0, "vector", slice(i0, i0 + P // 2)))
                others.append(partial(scale_ssw, 0, 0))
                for place in range(half_of(1).start, half_of(1).stop, 2):
                    sort_odd_first(place)
                    others.append(partial(scale_odd_first, place))
                weave(chain, others)
                spline_raw.append(load_spline_tile(nc, weights, spline_flat, 1))
                square(0)
                transpose_g(0, nc.scalar.copy)
                for bc in range(1, B_CHUNKS):
                    transpose_x(0, bc, nc.scalar.copy)
                base_calls = [
                    partial(nc.vector.tensor_copy, out=base_grouped[:], in_=base_raw[:].rearrange("p t i -> p i t")),
                    partial(
                        nc.vector.quantize_mx,
                        out=base_codes[:].bitcast(E4M3X4),
                        scales=base_scales[:],
                        in_=base_grouped[:].rearrange("p i t -> p (i t)"),
                    ),
                ]
                quantise_ssw(0)
                base_calls[0]()
                step(0, nc.vector)
                quantise_g(0)
                base_calls[1]()
                for call in clamp_calls(1, 1) + clamp_calls(2, 2, slice(0, CLAMPS_AHEAD[B_CHUNKS - 1])):
                    call()
                transpose_g(1, nc.scalar.copy)
                for it in range(1, I_TILES):
                    for bc in range(B_CHUNKS):
                        transpose_x(it, bc, nc.vector.tensor_copy if it == 3 else nc.scalar.copy)
                square(1)
                quantise_g(1)
                sigmoid(0)
                silu_minus(0)
                for bc in range(2, B_CHUNKS):
                    transpose_g(bc, nc.vector.tensor_copy)
                for bc in range(2, B_CHUNKS):
                    quantise_g(bc)

            prods = ctx.enter_context(tc.tile_pool(name="prods", bufs=2, reuse_waits="tile"))

            before = None
            for n, (it, bc) in enumerate(tiles):
                f = f_of[n]
                b_cols = slice(bc * N, (bc + 1) * N)

                prod = []
                bank_of = {}

                def run_passes(m):
                    bank_of[m] = banks.tile([P, N], F32, tag="bank", name="bank")
                    if m < BASES:
                        passes = []
                        for j in (m, m - 1):
                            place = half_of(j % 2).start + j // 2
                            columns = slice(place * P, (place + 1) * P)
                            passes.append((ssw[it][0][:, columns], ssw[it][1][:, columns]))
                    else:
                        passes = [(base_codes[:, it * P : (it + 1) * P], base_scales[:, it * P : (it + 1) * P])]
                    for n_pass, (w_codes, w_scales) in enumerate(passes):
                        nc.tensor.matmul_mx(
                            out=bank_of[m][:],
                            lhsT=w_codes.bitcast(E4M3X4),
                            lhsT_scale=w_scales,
                            rhs=g_codes[:, b_cols].bitcast(E5M2X4),
                            rhs_scale=g_scales[:, b_cols],
                            start=(n_pass == 0),
                            stop=(n_pass == len(passes) - 1),
                        )

                def run_products(m):
                    if m < BASES:
                        head_lead = {m_head: 1.0 if m_head % 2 == 0 else -1.0 for m_head, own in HEADS}
                        terms = [(head_lead[m] if m in head_lead else lead[:, m, it : it + 1], f[m])] + [
                            (weight[:, n_step, it : it + 1], f[k])
                            for n_step, (m_step, k) in enumerate(WEIGHTED_STEPS)
                            if m_step == m and n_step >= chained
                        ]
                    else:
                        terms = [(-1.0, neg_silu_of[it][:, b_cols])]
                    for factor, other in terms:
                        prod.append(prods.tile([P, N], F32, name="prod%d" % len(prod)))
                        nc.vector.scalar_tensor_tensor(
                            out=prod[-1][:], in0=bank_of[m][:], scalar=factor, in1=other, op0=ALU.mult, op1=ALU.mult
                        )

                for m in range(FIRST, FIRST + BANKS):
                    run_passes(m)

                last = n == len(tiles) - 1
                if n == BARE_AT:
                    inv_lead = consts.tile([P, BASES, I_TILES], F32)
                    nc.vector.reciprocal(out=inv_lead[:, FIRST:], in_=lead[:, FIRST:])
                    bare = consts.tile([P, len(WEIGHTED_STEPS), I_TILES], F32)
                    for n_step, (m, k) in enumerate(WEIGHTED_STEPS):
                        nc.vector.tensor_mul(out=bare[:, n_step], in0=weight[:, n_step], in1=inv_lead[:, m])
                chained = CHAINED.get(n, 0)
                for n_step, (m, k) in enumerate(WEIGHTED_STEPS[:chained]):
                    nc.vector.scalar_tensor_tensor(
                        out=f[m], in0=f[k], scalar=bare[:, n_step, it : it + 1], in1=f[m], op0=ALU.mult, op1=ALU.add
                    )
                more = it + 1 < I_TILES
                if more and bc == 2:
                    scale_ssw(it + 1, 0)
                if more and bc == 3:
                    scale_ssw(it + 1, 1)
                    quantise_ssw(it + 1)
                if n + 2 < len(tiles):
                    if n % 2 == 0:
                        for call in clamp_calls(n + 2, 2, slice(CLAMPS_AHEAD[(bc - 1) % B_CHUNKS], BASES - FIRST)):
                            call()
                    elif n + 3 < len(tiles):
                        for call in clamp_calls(n + 3, 2, slice(0, CLAMPS_AHEAD[bc])):
                            call()
                    square(n + 2)
                if not more and bc > 0:
                    minus_dsilu(it, bc, sigmoid_of[it][:, b_cols])
                if n + 1 < len(tiles):
                    let_gpsimd_begin(n + 1)
                    step(n + 1, nc.gpsimd)

                if bc > 0 and more:
                    sig_t = transpose_sigmoid(it, bc)
                if before:
                    add_up_and_store(*before)
                if bc == 0 and more:
                    sig_t = transpose_sigmoid(it, bc)
                if more and bc == 0:
                    new_sorted(it + 1)
                if more and bc < 2:
                    sort_ssw(it + 1, bc, "scalar")
                if bc == 1 and it + 2 < I_TILES:
                    spline_raw.append(load_spline_tile(nc, weights, spline_flat, it + 2))
                if more and bc == 2:
                    silu_minus(it + 1)
                if more and bc == 3:
                    sigmoid(it + 1)

                for m in range(FIRST, BASES + 1):
                    if m == BASES - 1 and more:
                        minus_dsilu(it, bc, sig_t)
                    if m == BASES - 1 and not more and bc == 0:
                        minus_dsilu(it, bc, sigmoid_of[it][:, b_cols])
                    run_products(m)
                    if m + BANKS <= BASES:
                        run_passes(m + BANKS)
                    if last and m == FREE_BANKS_AFTER:
                        totals = [sums.tile([P, P], F32, tag="total", name="total")]
                        totals += [banks.tile([P, P], F32, tag="bank", name="bank") for t in range(1, B_SUB)]
                    if last and m >= FREE_BANKS_AFTER:
                        add_to_last(totals, prod, m == BASES)
                before = (prod, it, bc)
            store_last(totals, it, bc)
